import numpy as np
import ml_dtypes


def mxq(x, axis, fmt="e4m3"):
    dtype, down = {"e4m3": (ml_dtypes.float8_e4m3fn, 7), "e5m2": (ml_dtypes.float8_e5m2, 14)}[fmt]
    v = np.moveaxis(np.asarray(x, np.float32).astype(ml_dtypes.bfloat16).astype(np.float64), axis, -1)
    blocks = v.reshape(v.shape[:-1] + (-1, 32))
    amax = np.abs(blocks).max(-1, keepdims=True)
    byte = np.maximum(np.where(amax > 0, np.frexp(amax)[1] - 1 + 127, 0) - down, 1)
    scale = np.exp2(byte - 127.0)
    codes = (blocks / scale).astype(np.float32).astype(dtype).astype(np.float64)
    return np.moveaxis((codes * scale).reshape(v.shape), -1, axis)


WIDE = False


def mx_kscale(k):
    if not WIDE:
        return np.ones(k)
    levels = np.array([10, -10, 5, -5, 0])
    a = np.random.permutation(np.resize(levels, k // 512 * 4)).reshape(k // 512, 4)
    idx = np.arange(k)
    return np.exp2(a[idx // 512, idx % 128 // 32])


BF16 = ml_dtypes.bfloat16


def bf(x):
    return np.asarray(x, np.float32).astype(BF16)


def f64(x):
    return np.asarray(x).astype(np.float64)


E2M1 = np.array([0.0, 0.5, 1.0, 1.5, 2.0, 3.0, 4.0, 6.0, -0.0, -0.5, -1.0, -1.5, -2.0, -3.0, -4.0, -6.0])


def pack_weight(w, fmt):
    k, n = w.shape
    w = f64(bf(w)).reshape(k // 32, 32, n)
    amax = np.abs(w).max(1)
    if fmt == "e4m3":
        byte = np.frexp(amax)[1] - 1 + 127 - 7
    else:
        mant, ex = np.frexp(amax / 6.0)
        byte = np.where(mant > 0.5, ex, ex - 1) + 127
    byte = np.clip(np.where(amax > 0, byte, 1), 1, 254)
    scaled = (w * np.exp2(127.0 - byte)[:, None, :]).reshape(k, n).astype(np.float32)
    by_word = np.ascontiguousarray(scaled.reshape(k // 512, 128, 4, n).transpose(0, 1, 3, 2))
    if fmt == "e4m3":
        words = by_word.astype(ml_dtypes.float8_e4m3fn).view(np.uint8)
    else:
        c = by_word.astype(ml_dtypes.float4_e2m1fn).view(np.uint8) & 0xF
        words = c[..., 0::2] | (c[..., 1::2] << 4)
    return np.ascontiguousarray(words), np.ascontiguousarray(byte.astype(np.uint8).reshape(k // 512, 16, n))


def unpack_weight(words, scales, fmt):
    g, p, n, _ = words.shape
    if fmt == "e4m3":
        vals = np.ascontiguousarray(words).view(ml_dtypes.float8_e4m3fn).astype(np.float64)
    else:
        nib = np.empty((g, p, n, 4), np.uint8)
        nib[..., 0::2] = words & 0xF
        nib[..., 1::2] = words >> 4
        vals = E2M1[nib]
    vals = vals * np.repeat(np.exp2(scales.astype(np.float64) - 127.0), 8, axis=1)[..., None]
    return vals.transpose(0, 1, 3, 2).reshape(g * 512, n)

def pack4(w):
    words, scales = pack_weight(w, "e2m1")
    return words.reshape(words.shape[0], 128, -1), scales


def unpack4(words, scales):
    return unpack_weight(words.reshape(words.shape[0], 128, -1, 2), scales, "e2m1")


B, H, FEAT, AUX, NS, FC, C = 4096, 512, 128, 128, 2, 1024, 256
IN = FEAT + AUX + NS


def sigmoid(v):
    return 1.0 / (1.0 + np.exp(-v))


def setup_inputs():
    s = mx_kscale(H)
    s = s / s.max()
    col = np.concatenate([np.full(FEAT, 0.6 / np.sqrt(FEAT)), np.full(AUX, 0.6 / np.sqrt(AUX)), np.full(NS, 0.6 / np.sqrt(NS))])
    x = bf(np.random.standard_normal((B, NS)))
    feat = bf(np.random.standard_normal((B, FEAT)))
    aux1 = bf(np.random.standard_normal((B, AUX)))
    h = bf(np.random.standard_normal((B, H)) * s)
    w_ih = bf(np.random.standard_normal((3 * H, IN)) * col)
    w_hh = np.random.standard_normal((3 * H, H)) / np.sqrt(H) / s
    w_hh_words, w_hh_scales = pack4(np.ascontiguousarray(w_hh.T))
    b_ih = bf(np.random.standard_normal(3 * H) * 0.3)
    b_hh = bf(np.random.standard_normal(3 * H) * 0.3)
    return {"x": x,
            "feat": feat,
            "aux1": aux1,
            "h": h,
            "w_ih": w_ih,
            "w_hh_words": w_hh_words,
            "w_hh_scales": w_hh_scales,
            "b_ih": b_ih,
            "b_hh": b_hh}


def reference(x, feat, aux1, h, w_ih, w_hh_words, w_hh_scales, b_ih, b_hh):
    hh, wi, xx = f64(h), f64(w_ih), f64(x)
    gi = f64(feat) @ wi[:, :FEAT].T + f64(aux1) @ wi[:, FEAT:FEAT + AUX].T
    for j in range(NS):
        gi = gi + xx[:, j:j + 1] * wi[:, FEAT + AUX + j][None, :]
    gi = gi + f64(b_ih)
    gh = (mxq(hh, 1, "e4m3") @ unpack4(w_hh_words, w_hh_scales)) + f64(b_hh)
    i_r, i_z, i_n = np.split(gi, 3, axis=1)
    h_r, h_z, h_n = np.split(gh, 3, axis=1)
    r = sigmoid(i_r + h_r)
    z = sigmoid(i_z + h_z)
    n = np.tanh(i_n + r * h_n)
    return (1.0 - z) * n + z * hh

@@ -1,0 +1,249 @@
+from contextlib import ExitStack
+
+import concourse.mybir as mybir
+from concourse.masks import make_identity
+
+FP8X4 = mybir.dt.float8_e4m3fn_x4
+FP4X4 = mybir.dt.float4_e2m1fn_x4
+BF16 = mybir.dt.bfloat16
+F32 = mybir.dt.float32
+I32 = mybir.dt.int32
+U32 = mybir.dt.uint32
+U8 = mybir.dt.uint8
+ALU = mybir.AluOpType
+ACT = mybir.ActivationFunctionType
+
+P = 128
+PACK = 4
+BATCH = 4096
+HID = 512
+STREAM = 128
+N_X = 2
+IN = 2 * STREAM + N_X
+GATES = 3
+R_GATE, Z_GATE, N_GATE = 0, 1, 2
+JT = HID // P
+COL_TILES = GATES * JT
+NB = 512
+SUB = NB // P
+NBLK = BATCH // NB
+TILES = BATCH // P
+
+FLOPS = 2 * BATCH * GATES * HID * (HID + IN)
+
+
+def tile_wavernncell_pa_t_kernel(tc, x, feat, aux1, h, w_ih, w_hh_words, w_hh_scales, b_ih, b_hh, out):
+    nc = tc.nc
+    with ExitStack() as ctx:
+        const = ctx.enter_context(tc.tile_pool(name="const", bufs=1))
+        block = ctx.enter_context(tc.tile_pool(name="block", bufs=2))
+        work = ctx.enter_context(tc.tile_pool(name="work", bufs=3))
+        psum_mm = ctx.enter_context(tc.psum_pool(name="psum_mm", bufs=2))
+        psum_tr = ctx.enter_context(tc.psum_pool(name="psum_tr", bufs=4))
+
+        w4_scales = const.tile([P, GATES * HID], U8, align_bytes=64)
+        nc.vector.memset(w4_scales[:].bitcast(I32), 0)
+        bias_rows = const.tile([P, P], BF16)
+        nc.vector.memset(bias_rows[:].bitcast(I32), 0)
+        x_rows = const.tile([P, BATCH, N_X], BF16)
+        nc.vector.memset(x_rows[:].rearrange("p b c -> p (b c)").bitcast(I32), 0)
+
+        w_sb = const.tile([P, COL_TILES, IN], BF16)
+        h_sb = const.tile([P, TILES, HID], BF16)
+        fa_sb = const.tile([P, TILES, 2, STREAM], BF16)
+        x_bc = const.tile([P, NBLK, NB, N_X], BF16)
+        w4_words = const.tile([P, 2 * GATES * HID], U8, align_bytes=64)
+        h_view = h.rearrange("(t p) k -> p t k", p=P)
+        feat_view = feat.rearrange("(t p) k -> p t k", p=P)
+        aux_view = aux1.rearrange("(t p) k -> p t k", p=P)
+        x_flat = x.rearrange("b c -> (b c)")
+
+        def load_block(bb):
+            tiles = slice(bb * SUB, (bb + 1) * SUB)
+            nc.sync.dma_start(out=h_sb[:, tiles, :], in_=h_view[:, tiles, :])
+            nc.sync.dma_start(out=fa_sb[:, tiles, 0, :], in_=feat_view[:, tiles, :])
+            nc.sync.dma_start(out=fa_sb[:, tiles, 1, :], in_=aux_view[:, tiles, :])
+            nc.sync.dma_start(
+                out=x_bc[:, bb, :, :].rearrange("p b c -> p (b c)"),
+                in_=x_flat[bb * NB * N_X : (bb + 1) * NB * N_X].partition_broadcast(P),
+            )
+
+        nc.sync.dma_start(out=w_sb[:], in_=w_ih.rearrange("(c p) k -> p c k", p=P))
+        load_block(0)
+        nc.sync.dma_start(out=w4_words[:].bitcast(I32), in_=w_hh_words[0].bitcast(I32))
+        for quad in range(4):
+            nc.sync.dma_start(
+                out=w4_scales[32 * quad : 32 * quad + 4, :].bitcast(I32),
+                in_=w_hh_scales[0, 4 * quad : 4 * quad + 4, :].bitcast(I32),
+            )
+        nc.sync.dma_start(out=bias_rows[0:COL_TILES, :], in_=b_ih.rearrange("(c p) -> c p", p=P))
+        nc.sync.dma_start(out=bias_rows[COL_TILES : 2 * COL_TILES, :], in_=b_hh.rearrange("(c p) -> c p", p=P))
+        x_rows_flat = x_rows[:].rearrange("p b c -> p (b c)")
+        nc.sync.dma_start(out=x_rows_flat[P - 2 : P - 1, :], in_=x_flat.unsqueeze(0))
+        nc.sync.dma_start(out=x_rows_flat[P - 1 : P, 0 : BATCH * N_X - 1], in_=x_flat[1 : BATCH * N_X].unsqueeze(0))
+        for bb in range(1, NBLK):
+            load_block(bb)
+
+        ident_bf = const.tile([P, P], BF16)
+        make_identity(nc, ident_bf[:])
+        ident_f32 = const.tile([P, P], F32)
+        make_identity(nc, ident_f32[:])
+
+        wT = const.tile([P, 2, GATES * HID], BF16)
+        for s in range(2):
+            for gate in range(GATES):
+                wt_ps = psum_tr.tile([P, HID], BF16, tag="tr")
+                for jt in range(JT):
+                    nc.tensor.transpose(
+                        out=wt_ps[:, jt * P : (jt + 1) * P],
+                        in_=w_sb[:, gate * JT + jt, s * STREAM : (s + 1) * STREAM],
+                        identity=ident_bf[:],
+                    )
+                nc.scalar.copy(out=wT[:, s, gate * HID : (gate + 1) * HID], in_=wt_ps[:])
+        wxT = const.tile([P, HID], BF16)
+        wx_ps = psum_tr.tile([P, HID], BF16, tag="tr")
+        for jt in range(JT):
+            nc.tensor.transpose(
+                out=wx_ps[:, jt * P : (jt + 1) * P], in_=w_sb[:, N_GATE * JT + jt, IN - P : IN], identity=ident_bf[:]
+            )
+        nc.scalar.copy(out=wxT[:], in_=wx_ps[:])
+        wx = const.tile([P, COL_TILES, N_X], F32)
+        nc.vector.tensor_copy(out=wx[:], in_=w_sb[:, :, 2 * STREAM : IN])
+        bias_ps = psum_tr.tile([P, P], BF16, tag="tr")
+        nc.tensor.transpose(out=bias_ps[:], in_=bias_rows[:], identity=ident_bf[:])
+        bias = const.tile([P, 2 * COL_TILES], F32)
+        nc.vector.tensor_copy(out=bias[:], in_=bias_ps[:, 0 : 2 * COL_TILES])
+        bias_rz = const.tile([P, 2 * JT], F32)
+        nc.vector.tensor_tensor(
+            out=bias_rz[:], in0=bias[:, 0 : 2 * JT], in1=bias[:, COL_TILES : COL_TILES + 2 * JT], op=ALU.add
+        )
+        bias_rz_neg = const.tile([P, 2 * JT], F32)
+        nc.vector.tensor_scalar_mul(out=bias_rz_neg[:], in0=bias_rz[:], scalar1=-1.0)
+
+        def prepare(bb):
+            grouped = block.tile([P, SUB, P, PACK], BF16, align_bytes=64)
+            grouped_flat = grouped[:].rearrange("p s b t -> p (s b t)")
+            grouped_words = grouped_flat.bitcast(F32).rearrange("p (s b u) -> p s b u", s=SUB, u=2)
+            for pair in range(SUB // 2):
+                hw_ps = psum_tr.tile([P, 2, 2, P], F32, tag="tr")
+                for s in range(2):
+                    words = h_sb[:, bb * SUB + 2 * pair + s, :].bitcast(F32)
+                    for u in range(2):
+                        nc.tensor.transpose(out=hw_ps[:, s, u, :], in_=words[:, u : HID // 2 : 2], identity=ident_f32[:])
+                nc.scalar.copy(
+                    out=grouped_words[:, 2 * pair : 2 * pair + 2, :, :], in_=hw_ps[:].rearrange("p s u b -> p s b u")
+                )
+            cat_ps = psum_tr.tile([P, 2, NB], BF16, tag="tr")
+            for s in range(SUB):
+                for stream in range(2):
+                    nc.tensor.transpose(
+                        out=cat_ps[:, stream, s * P : (s + 1) * P], in_=fa_sb[:, bb * SUB + s, stream, :], identity=ident_bf[:]
+                    )
+            catT = block.tile([P, 2, NB], BF16)
+            nc.scalar.copy(out=catT[:], in_=cat_ps[:])
+            h_codes = block.tile([P, NB], U32, align_bytes=64)
+            h_scales = block.tile([P, NB], U8, align_bytes=64)
+            nc.vector.quantize_mx(out=h_codes[:].bitcast(FP8X4), scales=h_scales[:], in_=grouped_flat)
+            return h_codes, h_scales, catT
+
+        def products(bb, operands, gate, jt):
+            h_codes, h_scales, catT = operands
+            c = gate * JT + jt
+            gi = psum_mm.tile([P, NB], F32)
+            nc.tensor.matmul(out=gi[:], lhsT=wT[:, 0, c * P : (c + 1) * P], rhs=catT[:, 0, :], start=True, stop=False)
+            nc.tensor.matmul(
+                out=gi[:], lhsT=wT[:, 1, c * P : (c + 1) * P], rhs=catT[:, 1, :], start=False, stop=(gate != N_GATE)
+            )
+            if gate == N_GATE:
+                nc.tensor.matmul(
+                    out=gi[:],
+                    lhsT=wxT[:, jt * P : (jt + 1) * P],
+                    rhs=x_rows[:, bb * NB : (bb + 1) * NB, 0],
+                    start=False,
+                    stop=True,
+                )
+            gh = psum_mm.tile([P, NB], F32)
+            nc.tensor.matmul_mx(
+                out=gh[:],
+                lhsT=w4_words[:, 2 * c * P : 2 * (c + 1) * P].bitcast(FP4X4),
+                lhsT_scale=w4_scales[:, c * P : (c + 1) * P],
+                rhs=h_codes[:].bitcast(FP8X4),
+                rhs_scale=h_scales[:],
+                start=True,
+                stop=True,
+            )
+            return gi, gh
+
+        def sigmoid_argument(bb, operands, gate, jt):
+            c = gate * JT + jt
+            gi, gh = products(bb, operands, gate, jt)
+            gi_x0 = work.tile([P, NB], F32)
+            nc.vector.scalar_tensor_tensor(
+                out=gi_x0[:], in0=x_bc[:, bb, :, 0], scalar=wx[:, c, 0:1], in1=gi[:], op0=ALU.mult, op1=ALU.add
+            )
+            gh_x1 = work.tile([P, NB], F32)
+            nc.vector.scalar_tensor_tensor(
+                out=gh_x1[:], in0=x_bc[:, bb, :, 1], scalar=wx[:, c, 1:2], in1=gh[:], op0=ALU.mult, op1=ALU.add
+            )
+            total = work.tile([P, NB], F32)
+            nc.gpsimd.tensor_tensor(out=total[:], in0=gi_x0[:], in1=gh_x1[:], op=ALU.add)
+            return total
+
+        def gates(bb, operands, z_blk, q_blk, jt):
+            r_arg = sigmoid_argument(bb, operands, R_GATE, jt)
+            r = work.tile([P, NB], F32)
+            nc.scalar.activation(out=r[:], in_=r_arg[:], func=ACT.Sigmoid, bias=bias_rz[:, jt : jt + 1], scale=1.0)
+
+            z_arg = sigmoid_argument(bb, operands, Z_GATE, jt)
+            nc.scalar.activation(
+                out=z_blk[:, jt, :], in_=z_arg[:], func=ACT.Sigmoid, bias=bias_rz[:, JT + jt : JT + jt + 1], scale=1.0
+            )
+            one_minus_z = work.tile([P, NB], F32)
+            nc.scalar.activation(
+                out=one_minus_z[:], in_=z_arg[:], func=ACT.Sigmoid, bias=bias_rz_neg[:, JT + jt : JT + jt + 1], scale=-1.0
+            )
+
+            c = N_GATE * JT + jt
+            gi, gh = products(bb, operands, N_GATE, jt)
+            r_hn = work.tile([P, NB], F32)
+            nc.vector.scalar_tensor_tensor(
+                out=r_hn[:], in0=gh[:], scalar=bias[:, COL_TILES + c : COL_TILES + c + 1], in1=r[:], op0=ALU.add, op1=ALU.mult
+            )
+            n_arg = work.tile([P, NB], F32)
+            nc.vector.tensor_tensor(out=n_arg[:], in0=r_hn[:], in1=gi[:], op=ALU.add)
+            n = work.tile([P, NB], F32)
+            nc.scalar.activation(out=n[:], in_=n_arg[:], func=ACT.Tanh, bias=bias[:, c : c + 1], scale=1.0)
+            nc.gpsimd.tensor_tensor(out=q_blk[:, jt, :], in0=one_minus_z[:], in1=n[:], op=ALU.mult)
+
+        def finish(bb, z_blk, q_blk, s):
+            t = bb * SUB + s
+            z_ps = psum_tr.tile([P, HID], F32, tag="tr")
+            q_ps = psum_tr.tile([P, HID], F32, tag="tr")
+            for jt in range(JT):
+                nc.tensor.transpose(
+                    out=z_ps[:, jt * P : (jt + 1) * P], in_=z_blk[:, jt, s * P : (s + 1) * P], identity=ident_f32[:]
+                )
+            for jt in range(JT):
+                nc.tensor.transpose(
+                    out=q_ps[:, jt * P : (jt + 1) * P], in_=q_blk[:, jt, s * P : (s + 1) * P], identity=ident_f32[:]
+                )
+            zh = work.tile([P, HID], F32)
+            nc.vector.tensor_tensor(out=zh[:], in0=h_sb[:, t, :], in1=z_ps[:], op=ALU.mult)
+            res = work.tile([P, HID], F32)
+            nc.vector.tensor_tensor(out=res[:], in0=zh[:], in1=q_ps[:], op=ALU.add)
+            nc.sync.dma_start(out=out[t * P : (t + 1) * P, :], in_=res[:])
+
+        operands = prepare(0)
+        done = None
+        for bb in range(NBLK):
+            following = prepare(bb + 1) if bb + 1 < NBLK else None
+            z_blk = block.tile([P, JT, NB], F32)
+            q_blk = block.tile([P, JT, NB], F32)
+            for jt in range(JT):
+                gates(bb, operands, z_blk, q_blk, jt)
+                if done is not None:
+                    finish(bb - 1, done[0], done[1], jt)
+            done = (z_blk, q_blk)
+            operands = following
+        for s in range(SUB):
+            finish(NBLK - 1, done[0], done[1], s)

@@ -28,6 +28,9 @@ NB = 512
 SUB = NB // P
 NBLK = BATCH // NB
 TILES = BATCH // P
+UNITS = NBLK * JT
+PREP_LEAD = 5
+FINISH_LAG = 5
 
 FLOPS = 2 * BATCH * GATES * HID * (HID + IN)
 
@@ -36,10 +39,9 @@ def tile_wavernncell_pa_t_kernel(tc, x, feat, aux1, h, w_ih, w_hh_words, w_hh_sc
     nc = tc.nc
     with ExitStack() as ctx:
         const = ctx.enter_context(tc.tile_pool(name="const", bufs=1))
+        operand = ctx.enter_context(tc.tile_pool(name="operand", bufs=3))
         block = ctx.enter_context(tc.tile_pool(name="block", bufs=2))
         work = ctx.enter_context(tc.tile_pool(name="work", bufs=3))
-        psum_mm = ctx.enter_context(tc.psum_pool(name="psum_mm", bufs=2))
-        psum_tr = ctx.enter_context(tc.psum_pool(name="psum_tr", bufs=4))
 
         w4_scales = const.tile([P, GATES * HID], U8, align_bytes=64)
         nc.vector.memset(w4_scales[:].bitcast(I32), 0)
@@ -89,65 +91,71 @@ def tile_wavernncell_pa_t_kernel(tc, x, feat, aux1, h, w_ih, w_hh_words, w_hh_sc
         ident_f32 = const.tile([P, P], F32)
         make_identity(nc, ident_f32[:])
 
-        wT = const.tile([P, 2, GATES * HID], BF16)
-        for s in range(2):
-            for gate in range(GATES):
-                wt_ps = psum_tr.tile([P, HID], BF16, tag="tr")
-                for jt in range(JT):
-                    nc.tensor.transpose(
-                        out=wt_ps[:, jt * P : (jt + 1) * P],
-                        in_=w_sb[:, gate * JT + jt, s * STREAM : (s + 1) * STREAM],
-                        identity=ident_bf[:],
-                    )
-                nc.scalar.copy(out=wT[:, s, gate * HID : (gate + 1) * HID], in_=wt_ps[:])
-        wxT = const.tile([P, HID], BF16)
-        wx_ps = psum_tr.tile([P, HID], BF16, tag="tr")
-        for jt in range(JT):
-            nc.tensor.transpose(
-                out=wx_ps[:, jt * P : (jt + 1) * P], in_=w_sb[:, N_GATE * JT + jt, IN - P : IN], identity=ident_bf[:]
-            )
-        nc.scalar.copy(out=wxT[:], in_=wx_ps[:])
-        wx = const.tile([P, COL_TILES, N_X], F32)
-        nc.vector.tensor_copy(out=wx[:], in_=w_sb[:, :, 2 * STREAM : IN])
-        bias_ps = psum_tr.tile([P, P], BF16, tag="tr")
-        nc.tensor.transpose(out=bias_ps[:], in_=bias_rows[:], identity=ident_bf[:])
-        bias = const.tile([P, 2 * COL_TILES], F32)
-        nc.vector.tensor_copy(out=bias[:], in_=bias_ps[:, 0 : 2 * COL_TILES])
-        bias_rz = const.tile([P, 2 * JT], F32)
-        nc.vector.tensor_tensor(
-            out=bias_rz[:], in0=bias[:, 0 : 2 * JT], in1=bias[:, COL_TILES : COL_TILES + 2 * JT], op=ALU.add
-        )
-        bias_rz_neg = const.tile([P, 2 * JT], F32)
-        nc.vector.tensor_scalar_mul(out=bias_rz_neg[:], in0=bias_rz[:], scalar1=-1.0)
-
-        def prepare(bb):
-            grouped = block.tile([P, SUB, P, PACK], BF16, align_bytes=64)
-            grouped_flat = grouped[:].rearrange("p s b t -> p (s b t)")
-            grouped_words = grouped_flat.bitcast(F32).rearrange("p (s b u) -> p s b u", s=SUB, u=2)
-            for pair in range(SUB // 2):
-                hw_ps = psum_tr.tile([P, 2, 2, P], F32, tag="tr")
-                for s in range(2):
-                    words = h_sb[:, bb * SUB + 2 * pair + s, :].bitcast(F32)
-                    for u in range(2):
-                        nc.tensor.transpose(out=hw_ps[:, s, u, :], in_=words[:, u : HID // 2 : 2], identity=ident_f32[:])
-                nc.scalar.copy(
-                    out=grouped_words[:, 2 * pair : 2 * pair + 2, :, :], in_=hw_ps[:].rearrange("p s u b -> p s b u")
+        with tc.psum_pool(name="psum_setup", bufs=4) as psum_setup:
+            wT = const.tile([P, 2, GATES * HID], BF16)
+            for s in range(2):
+                for gate in range(GATES):
+                    wt_ps = psum_setup.tile([P, HID], BF16, tag="turned")
+                    for jt in range(JT):
+                        nc.tensor.transpose(
+                            out=wt_ps[:, jt * P : (jt + 1) * P],
+                            in_=w_sb[:, gate * JT + jt, s * STREAM : (s + 1) * STREAM],
+                            identity=ident_bf[:],
+                        )
+                    nc.scalar.copy(out=wT[:, s, gate * HID : (gate + 1) * HID], in_=wt_ps[:])
+            wxT = const.tile([P, HID], BF16)
+            wx_ps = psum_setup.tile([P, HID], BF16, tag="turned")
+            for jt in range(JT):
+                nc.tensor.transpose(
+                    out=wx_ps[:, jt * P : (jt + 1) * P], in_=w_sb[:, N_GATE * JT + jt, IN - P : IN], identity=ident_bf[:]
                 )
-            cat_ps = psum_tr.tile([P, 2, NB], BF16, tag="tr")
-            for s in range(SUB):
-                for stream in range(2):
-                    nc.tensor.transpose(
-                        out=cat_ps[:, stream, s * P : (s + 1) * P], in_=fa_sb[:, bb * SUB + s, stream, :], identity=ident_bf[:]
-                    )
-            catT = block.tile([P, 2, NB], BF16)
-            nc.scalar.copy(out=catT[:], in_=cat_ps[:])
-            h_codes = block.tile([P, NB], U32, align_bytes=64)
-            h_scales = block.tile([P, NB], U8, align_bytes=64)
-            nc.vector.quantize_mx(out=h_codes[:].bitcast(FP8X4), scales=h_scales[:], in_=grouped_flat)
-            return h_codes, h_scales, catT
+            nc.scalar.copy(out=wxT[:], in_=wx_ps[:])
+            wx = const.tile([P, COL_TILES, N_X], F32)
+            nc.vector.tensor_copy(out=wx[:], in_=w_sb[:, :, 2 * STREAM : IN])
+            bias_ps = psum_setup.tile([P, P], BF16, tag="turned")
+            nc.tensor.transpose(out=bias_ps[:], in_=bias_rows[:], identity=ident_bf[:])
+            bias = const.tile([P, 2 * COL_TILES], F32)
+            nc.vector.tensor_copy(out=bias[:], in_=bias_ps[:, 0 : 2 * COL_TILES])
+            bias_rz = const.tile([P, 2 * JT], F32)
+            nc.vector.tensor_tensor(
+                out=bias_rz[:], in0=bias[:, 0 : 2 * JT], in1=bias[:, COL_TILES : COL_TILES + 2 * JT], op=ALU.add
+            )
 
-        def products(bb, operands, gate, jt):
-            h_codes, h_scales, catT = operands
+        psum_mm = ctx.enter_context(tc.psum_pool(name="psum_mm", bufs=2))
+        psum_tr = ctx.enter_context(tc.psum_pool(name="psum_tr", bufs=1))
+
+        operands = {}
+        r_products, z_products, n_products = {}, {}, {}
+        r_args, z_args, r_gate, z_gate, h_turned = {}, {}, {}, {}, {}
+        n_blocks, diff_blocks = {}, {}
+
+        def prepare(t):
+            bb, s = divmod(t, SUB)
+            if s == 0:
+                h_codes = operand.tile([P, NB], U32, align_bytes=64)
+                h_scales = operand.tile([P, NB], U8, align_bytes=64)
+                catT = operand.tile([P, 2, NB], BF16)
+                operands[bb] = (h_codes, h_scales, catT)
+            h_codes, h_scales, catT = operands[bb]
+            rows = slice(s * P, (s + 1) * P)
+            words = h_sb[:, t, :].bitcast(F32)
+            hw_ps = psum_tr.tile([P, 2, P], F32)
+            for u in range(2):
+                nc.tensor.transpose(out=hw_ps[:, u, :], in_=words[:, u : HID // 2 : 2], identity=ident_f32[:])
+            cat_ps = psum_tr.tile([P, 2, P], BF16)
+            for stream in range(2):
+                nc.tensor.transpose(out=cat_ps[:, stream, :], in_=fa_sb[:, t, stream, :], identity=ident_bf[:])
+            grouped = work.tile([P, P, PACK], BF16, align_bytes=64)
+            grouped_flat = grouped[:].rearrange("p b t -> p (b t)")
+            nc.scalar.copy(
+                out=grouped_flat.bitcast(F32).rearrange("p (b u) -> p b u", u=2), in_=hw_ps[:].rearrange("p u b -> p b u")
+            )
+            nc.scalar.copy(out=catT[:, :, rows], in_=cat_ps[:])
+            nc.vector.quantize_mx(out=h_codes[:, rows].bitcast(FP8X4), scales=h_scales[:, rows], in_=grouped_flat)
+
+        def products(u, gate):
+            bb, jt = divmod(u, JT)
+            h_codes, h_scales, catT = operands[bb]
             c = gate * JT + jt
             gi = psum_mm.tile([P, NB], F32)
             nc.tensor.matmul(out=gi[:], lhsT=wT[:, 0, c * P : (c + 1) * P], rhs=catT[:, 0, :], start=True, stop=False)
@@ -174,9 +182,9 @@ def tile_wavernncell_pa_t_kernel(tc, x, feat, aux1, h, w_ih, w_hh_words, w_hh_sc
             )
             return gi, gh
 
-        def sigmoid_argument(bb, operands, gate, jt):
+        def sigmoid_argument(u, gate, gi, gh):
+            bb, jt = divmod(u, JT)
             c = gate * JT + jt
-            gi, gh = products(bb, operands, gate, jt)
             gi_x0 = work.tile([P, NB], F32)
             nc.vector.scalar_tensor_tensor(
                 out=gi_x0[:], in0=x_bc[:, bb, :, 0], scalar=wx[:, c, 0:1], in1=gi[:], op0=ALU.mult, op1=ALU.add
@@ -189,61 +197,84 @@ def tile_wavernncell_pa_t_kernel(tc, x, feat, aux1, h, w_ih, w_hh_words, w_hh_sc
             nc.gpsimd.tensor_tensor(out=total[:], in0=gi_x0[:], in1=gh_x1[:], op=ALU.add)
             return total
 
-        def gates(bb, operands, z_blk, q_blk, jt):
-            r_arg = sigmoid_argument(bb, operands, R_GATE, jt)
-            r = work.tile([P, NB], F32)
-            nc.scalar.activation(out=r[:], in_=r_arg[:], func=ACT.Sigmoid, bias=bias_rz[:, jt : jt + 1], scale=1.0)
+        def sigmoid(u, gate, argument):
+            c = gate * JT + u % JT
+            value = work.tile([P, NB], F32, tag="gate%d" % gate)
+            nc.scalar.activation(out=value[:], in_=argument[:], func=ACT.Sigmoid, bias=bias_rz[:, c : c + 1], scale=1.0)
+            return value
 
-            z_arg = sigmoid_argument(bb, operands, Z_GATE, jt)
-            nc.scalar.activation(
-                out=z_blk[:, jt, :], in_=z_arg[:], func=ACT.Sigmoid, bias=bias_rz[:, JT + jt : JT + jt + 1], scale=1.0
-            )
-            one_minus_z = work.tile([P, NB], F32)
-            nc.scalar.activation(
-                out=one_minus_z[:], in_=z_arg[:], func=ACT.Sigmoid, bias=bias_rz_neg[:, JT + jt : JT + jt + 1], scale=-1.0
-            )
-
+        def candidate(u):
+            bb, jt = divmod(u, JT)
             c = N_GATE * JT + jt
-            gi, gh = products(bb, operands, N_GATE, jt)
+            if jt == 0:
+                n_blk = block.tile([P, JT, NB], F32)
+                n_blocks[bb] = n_blk
+            gi, gh = n_products[u]
             r_hn = work.tile([P, NB], F32)
             nc.vector.scalar_tensor_tensor(
-                out=r_hn[:], in0=gh[:], scalar=bias[:, COL_TILES + c : COL_TILES + c + 1], in1=r[:], op0=ALU.add, op1=ALU.mult
+                out=r_hn[:],
+                in0=gh[:],
+                scalar=bias[:, COL_TILES + c : COL_TILES + c + 1],
+                in1=r_gate[u][:],
+                op0=ALU.add,
+                op1=ALU.mult,
             )
             n_arg = work.tile([P, NB], F32)
             nc.vector.tensor_tensor(out=n_arg[:], in0=r_hn[:], in1=gi[:], op=ALU.add)
-            n = work.tile([P, NB], F32)
-            nc.scalar.activation(out=n[:], in_=n_arg[:], func=ACT.Tanh, bias=bias[:, c : c + 1], scale=1.0)
-            nc.gpsimd.tensor_tensor(out=q_blk[:, jt, :], in0=one_minus_z[:], in1=n[:], op=ALU.mult)
+            nc.scalar.activation(out=n_blocks[bb][:, jt, :], in_=n_arg[:], func=ACT.Tanh, bias=bias[:, c : c + 1], scale=1.0)
 
-        def finish(bb, z_blk, q_blk, s):
-            t = bb * SUB + s
-            z_ps = psum_tr.tile([P, HID], F32, tag="tr")
-            q_ps = psum_tr.tile([P, HID], F32, tag="tr")
-            for jt in range(JT):
+        def turn_h(u):
+            bb, jt = divmod(u, JT)
+            hT_ps = psum_tr.tile([P, NB], BF16)
+            for s in range(SUB):
                 nc.tensor.transpose(
-                    out=z_ps[:, jt * P : (jt + 1) * P], in_=z_blk[:, jt, s * P : (s + 1) * P], identity=ident_f32[:]
+                    out=hT_ps[:, s * P : (s + 1) * P], in_=h_sb[:, bb * SUB + s, jt * P : (jt + 1) * P], identity=ident_bf[:]
                 )
+            return hT_ps
+
+        def difference(u):
+            bb, jt = divmod(u, JT)
+            if jt == 0:
+                diff_blk = block.tile([P, JT, NB], F32)
+                diff_blocks[bb] = diff_blk
+            h_minus_n = work.tile([P, NB], F32)
+            nc.vector.tensor_tensor(out=h_minus_n[:], in0=h_turned[u][:], in1=n_blocks[bb][:, jt, :], op=ALU.subtract)
+            nc.gpsimd.tensor_tensor(out=diff_blocks[bb][:, jt, :], in0=z_gate[u][:], in1=h_minus_n[:], op=ALU.mult)
+
+        def finish(t):
+            bb, s = divmod(t, SUB)
+            rows = slice(s * P, (s + 1) * P)
+            out_ps = psum_tr.tile([P, HID], F32)
             for jt in range(JT):
-                nc.tensor.transpose(
-                    out=q_ps[:, jt * P : (jt + 1) * P], in_=q_blk[:, jt, s * P : (s + 1) * P], identity=ident_f32[:]
+                cols = slice(jt * P, (jt + 1) * P)
+                nc.tensor.matmul(
+                    out=out_ps[:, cols], lhsT=n_blocks[bb][:, jt, rows], rhs=ident_f32[:], is_transpose=True, start=True, stop=False
                 )
-            zh = work.tile([P, HID], F32)
-            nc.vector.tensor_tensor(out=zh[:], in0=h_sb[:, t, :], in1=z_ps[:], op=ALU.mult)
+                nc.tensor.matmul(
+                    out=out_ps[:, cols], lhsT=diff_blocks[bb][:, jt, rows], rhs=ident_f32[:], is_transpose=True, start=False, stop=True
+                )
             res = work.tile([P, HID], F32)
-            nc.vector.tensor_tensor(out=res[:], in0=zh[:], in1=q_ps[:], op=ALU.add)
+            nc.scalar.copy(out=res[:], in_=out_ps[:])
             nc.sync.dma_start(out=out[t * P : (t + 1) * P, :], in_=res[:])
 
-        operands = prepare(0)
-        done = None
-        for bb in range(NBLK):
-            following = prepare(bb + 1) if bb + 1 < NBLK else None
-            z_blk = block.tile([P, JT, NB], F32)
-            q_blk = block.tile([P, JT, NB], F32)
-            for jt in range(JT):
-                gates(bb, operands, z_blk, q_blk, jt)
-                if done is not None:
-                    finish(bb - 1, done[0], done[1], jt)
-            done = (z_blk, q_blk)
-            operands = following
-        for s in range(SUB):
-            finish(NBLK - 1, done[0], done[1], s)
+        with tc.manual_schedule():
+            for i in range(-PREP_LEAD, TILES + FINISH_LAG):
+                if 0 <= i < UNITS:
+                    r_args[i] = sigmoid_argument(i, R_GATE, r_products[i][0], r_products[i][1])
+                if 0 <= i - 1 < UNITS:
+                    z_gate[i - 1] = sigmoid(i - 1, Z_GATE, z_args[i - 1])
+                    n_products[i - 1] = products(i - 1, N_GATE)
+                    candidate(i - 1)
+                if 0 <= i < UNITS:
+                    r_gate[i] = sigmoid(i, R_GATE, r_args[i])
+                    z_products[i] = products(i, Z_GATE)
+                    z_args[i] = sigmoid_argument(i, Z_GATE, z_products[i][0], z_products[i][1])
+                if 0 <= i - 1 < UNITS:
+                    h_turned[i - 1] = turn_h(i - 1)
+                    difference(i - 1)
+                if 0 <= i - FINISH_LAG < TILES:
+                    finish(i - FINISH_LAG)
+                if 0 <= i + PREP_LEAD < TILES:
+                    prepare(i + PREP_LEAD)
+                if 0 <= i + 1 < UNITS:
+                    r_products[i + 1] = products(i + 1, R_GATE)

@@ -29,8 +29,6 @@ SUB = NB // P
 NBLK = BATCH // NB
 TILES = BATCH // P
 UNITS = NBLK * JT
-PREP_LEAD = 5
-FINISH_LAG = 5
 
 FLOPS = 2 * BATCH * GATES * HID * (HID + IN)
 
@@ -40,8 +38,7 @@ def tile_wavernncell_pa_t_kernel(tc, x, feat, aux1, h, w_ih, w_hh_words, w_hh_sc
     with ExitStack() as ctx:
         const = ctx.enter_context(tc.tile_pool(name="const", bufs=1))
         operand = ctx.enter_context(tc.tile_pool(name="operand", bufs=3))
-        block = ctx.enter_context(tc.tile_pool(name="block", bufs=2))
-        work = ctx.enter_context(tc.tile_pool(name="work", bufs=3))
+        work = ctx.enter_context(tc.tile_pool(name="work", bufs=4))
 
         w4_scales = const.tile([P, GATES * HID], U8, align_bytes=64)
         nc.vector.memset(w4_scales[:].bitcast(I32), 0)
@@ -91,7 +88,38 @@ def tile_wavernncell_pa_t_kernel(tc, x, feat, aux1, h, w_ih, w_hh_words, w_hh_sc
         ident_f32 = const.tile([P, P], F32)
         make_identity(nc, ident_f32[:])
 
-        with tc.psum_pool(name="psum_setup", bufs=4) as psum_setup:
+        operands = {}
+        grouped_tiles = {}
+
+        def turn_inputs(t, psum):
+            bb, s = divmod(t, SUB)
+            if s == 0:
+                h_codes = operand.tile([P, NB], U32, align_bytes=64)
+                h_scales = operand.tile([P, NB], U8, align_bytes=64)
+                catT = operand.tile([P, 2, NB], BF16)
+                operands[bb] = (h_codes, h_scales, catT)
+            catT = operands[bb][2]
+            words = h_sb[:, t, :].bitcast(F32)
+            hw_ps = psum.tile([P, 2, P], F32)
+            for u in range(2):
+                nc.tensor.transpose(out=hw_ps[:, u, :], in_=words[:, u : HID // 2 : 2], identity=ident_f32[:])
+            cat_ps = psum.tile([P, 2, P], BF16)
+            for stream in range(2):
+                nc.tensor.transpose(out=cat_ps[:, stream, :], in_=fa_sb[:, t, stream, :], identity=ident_bf[:])
+            grouped = work.tile([P, P * PACK], BF16, align_bytes=64)
+            nc.scalar.copy(
+                out=grouped[:].bitcast(F32).rearrange("p (b u) -> p b u", u=2), in_=hw_ps[:].rearrange("p u b -> p b u")
+            )
+            nc.scalar.copy(out=catT[:, :, s * P : (s + 1) * P], in_=cat_ps[:])
+            grouped_tiles[t] = grouped
+
+        def quantise(t):
+            bb, s = divmod(t, SUB)
+            h_codes, h_scales = operands[bb][0], operands[bb][1]
+            rows = slice(s * P, (s + 1) * P)
+            nc.vector.quantize_mx(out=h_codes[:, rows].bitcast(FP8X4), scales=h_scales[:, rows], in_=grouped_tiles[t][:])
+
+        with tc.psum_pool(name="psum_setup", bufs=2) as psum_setup:
             wT = const.tile([P, 2, GATES * HID], BF16)
             for s in range(2):
                 for gate in range(GATES):
@@ -120,38 +148,15 @@ def tile_wavernncell_pa_t_kernel(tc, x, feat, aux1, h, w_ih, w_hh_words, w_hh_sc
             nc.vector.tensor_tensor(
                 out=bias_rz[:], in0=bias[:, 0 : 2 * JT], in1=bias[:, COL_TILES : COL_TILES + 2 * JT], op=ALU.add
             )
+            for t in range(SUB):
+                turn_inputs(t, psum_setup)
+                quantise(t)
 
         psum_mm = ctx.enter_context(tc.psum_pool(name="psum_mm", bufs=2))
         psum_tr = ctx.enter_context(tc.psum_pool(name="psum_tr", bufs=1))
 
-        operands = {}
         r_products, z_products, n_products = {}, {}, {}
-        r_args, z_args, r_gate, z_gate, h_turned = {}, {}, {}, {}, {}
-        n_blocks, diff_blocks = {}, {}
-
-        def prepare(t):
-            bb, s = divmod(t, SUB)
-            if s == 0:
-                h_codes = operand.tile([P, NB], U32, align_bytes=64)
-                h_scales = operand.tile([P, NB], U8, align_bytes=64)
-                catT = operand.tile([P, 2, NB], BF16)
-                operands[bb] = (h_codes, h_scales, catT)
-            h_codes, h_scales, catT = operands[bb]
-            rows = slice(s * P, (s + 1) * P)
-            words = h_sb[:, t, :].bitcast(F32)
-            hw_ps = psum_tr.tile([P, 2, P], F32)
-            for u in range(2):
-                nc.tensor.transpose(out=hw_ps[:, u, :], in_=words[:, u : HID // 2 : 2], identity=ident_f32[:])
-            cat_ps = psum_tr.tile([P, 2, P], BF16)
-            for stream in range(2):
-                nc.tensor.transpose(out=cat_ps[:, stream, :], in_=fa_sb[:, t, stream, :], identity=ident_bf[:])
-            grouped = work.tile([P, P, PACK], BF16, align_bytes=64)
-            grouped_flat = grouped[:].rearrange("p b t -> p (b t)")
-            nc.scalar.copy(
-                out=grouped_flat.bitcast(F32).rearrange("p (b u) -> p b u", u=2), in_=hw_ps[:].rearrange("p u b -> p b u")
-            )
-            nc.scalar.copy(out=catT[:, :, rows], in_=cat_ps[:])
-            nc.vector.quantize_mx(out=h_codes[:, rows].bitcast(FP8X4), scales=h_scales[:, rows], in_=grouped_flat)
+        r_args, z_args, r_gate, z_gate, n_gate, h_turned, z_diff = {}, {}, {}, {}, {}, {}, {}
 
         def products(u, gate):
             bb, jt = divmod(u, JT)
@@ -204,11 +209,7 @@ def tile_wavernncell_pa_t_kernel(tc, x, feat, aux1, h, w_ih, w_hh_words, w_hh_sc
             return value
 
         def candidate(u):
-            bb, jt = divmod(u, JT)
-            c = N_GATE * JT + jt
-            if jt == 0:
-                n_blk = block.tile([P, JT, NB], F32)
-                n_blocks[bb] = n_blk
+            c = N_GATE * JT + u % JT
             gi, gh = n_products[u]
             r_hn = work.tile([P, NB], F32)
             nc.vector.scalar_tensor_tensor(
@@ -221,7 +222,9 @@ def tile_wavernncell_pa_t_kernel(tc, x, feat, aux1, h, w_ih, w_hh_words, w_hh_sc
             )
             n_arg = work.tile([P, NB], F32)
             nc.vector.tensor_tensor(out=n_arg[:], in0=r_hn[:], in1=gi[:], op=ALU.add)
-            nc.scalar.activation(out=n_blocks[bb][:, jt, :], in_=n_arg[:], func=ACT.Tanh, bias=bias[:, c : c + 1], scale=1.0)
+            n = work.tile([P, NB], F32)
+            nc.scalar.activation(out=n[:], in_=n_arg[:], func=ACT.Tanh, bias=bias[:, c : c + 1], scale=1.0)
+            return n
 
         def turn_h(u):
             bb, jt = divmod(u, JT)
@@ -233,48 +236,49 @@ def tile_wavernncell_pa_t_kernel(tc, x, feat, aux1, h, w_ih, w_hh_words, w_hh_sc
             return hT_ps
 
         def difference(u):
-            bb, jt = divmod(u, JT)
-            if jt == 0:
-                diff_blk = block.tile([P, JT, NB], F32)
-                diff_blocks[bb] = diff_blk
             h_minus_n = work.tile([P, NB], F32)
-            nc.vector.tensor_tensor(out=h_minus_n[:], in0=h_turned[u][:], in1=n_blocks[bb][:, jt, :], op=ALU.subtract)
-            nc.gpsimd.tensor_tensor(out=diff_blocks[bb][:, jt, :], in0=z_gate[u][:], in1=h_minus_n[:], op=ALU.mult)
+            nc.vector.tensor_tensor(out=h_minus_n[:], in0=h_turned[u][:], in1=n_gate[u][:], op=ALU.subtract)
+            diff = work.tile([P, NB], F32)
+            nc.gpsimd.tensor_tensor(out=diff[:], in0=z_gate[u][:], in1=h_minus_n[:], op=ALU.mult)
+            return diff
 
-        def finish(t):
-            bb, s = divmod(t, SUB)
-            rows = slice(s * P, (s + 1) * P)
-            out_ps = psum_tr.tile([P, HID], F32)
-            for jt in range(JT):
-                cols = slice(jt * P, (jt + 1) * P)
+        out_view = out.rearrange("(t p) j -> p t j", p=P)
+
+        def finish(u):
+            bb, jt = divmod(u, JT)
+            out_ps = psum_tr.tile([P, SUB, P], F32)
+            for s in range(SUB):
+                rows = slice(s * P, (s + 1) * P)
                 nc.tensor.matmul(
-                    out=out_ps[:, cols], lhsT=n_blocks[bb][:, jt, rows], rhs=ident_f32[:], is_transpose=True, start=True, stop=False
+                    out=out_ps[:, s, :], lhsT=n_gate[u][:, rows], rhs=ident_f32[:], is_transpose=True, start=True, stop=False
                 )
                 nc.tensor.matmul(
-                    out=out_ps[:, cols], lhsT=diff_blocks[bb][:, jt, rows], rhs=ident_f32[:], is_transpose=True, start=False, stop=True
+                    out=out_ps[:, s, :], lhsT=z_diff[u][:, rows], rhs=ident_f32[:], is_transpose=True, start=False, stop=True
                 )
-            res = work.tile([P, HID], F32)
+            res = work.tile([P, SUB, P], F32)
             nc.scalar.copy(out=res[:], in_=out_ps[:])
-            nc.sync.dma_start(out=out[t * P : (t + 1) * P, :], in_=res[:])
+            nc.sync.dma_start(out=out_view[:, bb * SUB : (bb + 1) * SUB, jt * P : (jt + 1) * P], in_=res[:])
 
         with tc.manual_schedule():
-            for i in range(-PREP_LEAD, TILES + FINISH_LAG):
+            for i in range(-2, UNITS + 4):
                 if 0 <= i < UNITS:
                     r_args[i] = sigmoid_argument(i, R_GATE, r_products[i][0], r_products[i][1])
+                if SUB <= i + 5 < TILES:
+                    quantise(i + 5)
                 if 0 <= i - 1 < UNITS:
                     z_gate[i - 1] = sigmoid(i - 1, Z_GATE, z_args[i - 1])
                     n_products[i - 1] = products(i - 1, N_GATE)
-                    candidate(i - 1)
+                    n_gate[i - 1] = candidate(i - 1)
                 if 0 <= i < UNITS:
                     r_gate[i] = sigmoid(i, R_GATE, r_args[i])
                     z_products[i] = products(i, Z_GATE)
                     z_args[i] = sigmoid_argument(i, Z_GATE, z_products[i][0], z_products[i][1])
-                if 0 <= i - 1 < UNITS:
-                    h_turned[i - 1] = turn_h(i - 1)
-                    difference(i - 1)
-                if 0 <= i - FINISH_LAG < TILES:
-                    finish(i - FINISH_LAG)
-                if 0 <= i + PREP_LEAD < TILES:
-                    prepare(i + PREP_LEAD)
+                if 0 <= i - 2 < UNITS:
+                    h_turned[i - 2] = turn_h(i - 2)
+                    z_diff[i - 2] = difference(i - 2)
+                if 0 <= i - 3 < UNITS:
+                    finish(i - 3)
+                if SUB <= i + 6 < TILES:
+                    turn_inputs(i + 6, psum_tr)
                 if 0 <= i + 1 < UNITS:
                     r_products[i + 1] = products(i + 1, R_GATE)

@@ -62,6 +62,8 @@ def tile_wavernncell_pa_t_kernel(tc, x, feat, aux1, h, w_ih, w_hh_words, w_hh_sc
             nc.sync.dma_start(out=h_sb[:, tiles, :], in_=h_view[:, tiles, :])
             nc.sync.dma_start(out=fa_sb[:, tiles, 0, :], in_=feat_view[:, tiles, :])
             nc.sync.dma_start(out=fa_sb[:, tiles, 1, :], in_=aux_view[:, tiles, :])
+
+        def load_x(bb):
             nc.sync.dma_start(
                 out=x_bc[:, bb, :, :].rearrange("p b c -> p (b c)"),
                 in_=x_flat[bb * NB * N_X : (bb + 1) * NB * N_X].partition_broadcast(P),
@@ -75,6 +77,7 @@ def tile_wavernncell_pa_t_kernel(tc, x, feat, aux1, h, w_ih, w_hh_words, w_hh_sc
                 out=w4_scales[32 * quad : 32 * quad + 4, :].bitcast(I32),
                 in_=w_hh_scales[0, 4 * quad : 4 * quad + 4, :].bitcast(I32),
             )
+        load_x(0)
         nc.sync.dma_start(out=bias_rows[0:COL_TILES, :], in_=b_ih.rearrange("(c p) -> c p", p=P))
         nc.sync.dma_start(out=bias_rows[COL_TILES : 2 * COL_TILES, :], in_=b_hh.rearrange("(c p) -> c p", p=P))
         x_rows_flat = x_rows[:].rearrange("p b c -> p (b c)")
@@ -82,6 +85,7 @@ def tile_wavernncell_pa_t_kernel(tc, x, feat, aux1, h, w_ih, w_hh_words, w_hh_sc
         nc.sync.dma_start(out=x_rows_flat[P - 1 : P, 0 : BATCH * N_X - 1], in_=x_flat[1 : BATCH * N_X].unsqueeze(0))
         for bb in range(1, NBLK):
             load_block(bb)
+            load_x(bb)
 
         ident_bf = const.tile([P, P], BF16)
         make_identity(nc, ident_bf[:])
@@ -89,7 +93,6 @@ def tile_wavernncell_pa_t_kernel(tc, x, feat, aux1, h, w_ih, w_hh_words, w_hh_sc
         make_identity(nc, ident_f32[:])
 
         operands = {}
-        grouped_tiles = {}
 
         def turn_inputs(t, psum):
             bb, s = divmod(t, SUB)
@@ -97,8 +100,9 @@ def tile_wavernncell_pa_t_kernel(tc, x, feat, aux1, h, w_ih, w_hh_words, w_hh_sc
                 h_codes = operand.tile([P, NB], U32, align_bytes=64)
                 h_scales = operand.tile([P, NB], U8, align_bytes=64)
                 catT = operand.tile([P, 2, NB], BF16)
-                operands[bb] = (h_codes, h_scales, catT)
-            catT = operands[bb][2]
+                grouped = operand.tile([P, SUB, P * PACK], BF16, align_bytes=64)
+                operands[bb] = (h_codes, h_scales, catT, grouped)
+            catT, grouped = operands[bb][2], operands[bb][3]
             words = h_sb[:, t, :].bitcast(F32)
             hw_ps = psum.tile([P, 2, P], F32)
             for u in range(2):
@@ -106,18 +110,16 @@ def tile_wavernncell_pa_t_kernel(tc, x, feat, aux1, h, w_ih, w_hh_words, w_hh_sc
             cat_ps = psum.tile([P, 2, P], BF16)
             for stream in range(2):
                 nc.tensor.transpose(out=cat_ps[:, stream, :], in_=fa_sb[:, t, stream, :], identity=ident_bf[:])
-            grouped = work.tile([P, P * PACK], BF16, align_bytes=64)
             nc.scalar.copy(
-                out=grouped[:].bitcast(F32).rearrange("p (b u) -> p b u", u=2), in_=hw_ps[:].rearrange("p u b -> p b u")
+                out=grouped[:, s, :].bitcast(F32).rearrange("p (b u) -> p b u", u=2), in_=hw_ps[:].rearrange("p u b -> p b u")
             )
             nc.scalar.copy(out=catT[:, :, s * P : (s + 1) * P], in_=cat_ps[:])
-            grouped_tiles[t] = grouped
 
-        def quantise(t):
-            bb, s = divmod(t, SUB)
-            h_codes, h_scales = operands[bb][0], operands[bb][1]
-            rows = slice(s * P, (s + 1) * P)
-            nc.vector.quantize_mx(out=h_codes[:, rows].bitcast(FP8X4), scales=h_scales[:, rows], in_=grouped_tiles[t][:])
+        def quantise(bb):
+            h_codes, h_scales, grouped = operands[bb][0], operands[bb][1], operands[bb][3]
+            nc.vector.quantize_mx(
+                out=h_codes[:].bitcast(FP8X4), scales=h_scales[:], in_=grouped[:].rearrange("p s e -> p (s e)")
+            )
 
         with tc.psum_pool(name="psum_setup", bufs=2) as psum_setup:
             wT = const.tile([P, 2, GATES * HID], BF16)
@@ -150,17 +152,18 @@ def tile_wavernncell_pa_t_kernel(tc, x, feat, aux1, h, w_ih, w_hh_words, w_hh_sc
             )
             for t in range(SUB):
                 turn_inputs(t, psum_setup)
-                quantise(t)
+            quantise(0)
 
         psum_mm = ctx.enter_context(tc.psum_pool(name="psum_mm", bufs=2))
         psum_tr = ctx.enter_context(tc.psum_pool(name="psum_tr", bufs=1))
 
         r_products, z_products, n_products = {}, {}, {}
-        r_args, z_args, r_gate, z_gate, n_gate, h_turned, z_diff = {}, {}, {}, {}, {}, {}, {}
+        r_args, z_args, n_args, r_gate, z_gate, n_gate = {}, {}, {}, {}, {}, {}
+        z_halves, r_hidden, h_turned, z_diff = {}, {}, {}, {}
 
         def products(u, gate):
             bb, jt = divmod(u, JT)
-            h_codes, h_scales, catT = operands[bb]
+            h_codes, h_scales, catT = operands[bb][0], operands[bb][1], operands[bb][2]
             c = gate * JT + jt
             gi = psum_mm.tile([P, NB], F32)
             nc.tensor.matmul(out=gi[:], lhsT=wT[:, 0, c * P : (c + 1) * P], rhs=catT[:, 0, :], start=True, stop=False)
@@ -187,16 +190,19 @@ def tile_wavernncell_pa_t_kernel(tc, x, feat, aux1, h, w_ih, w_hh_words, w_hh_sc
             )
             return gi, gh
 
-        def sigmoid_argument(u, gate, gi, gh):
+        def take_gi(u, gate, gi):
             bb, jt = divmod(u, JT)
-            c = gate * JT + jt
             gi_x0 = work.tile([P, NB], F32)
             nc.vector.scalar_tensor_tensor(
-                out=gi_x0[:], in0=x_bc[:, bb, :, 0], scalar=wx[:, c, 0:1], in1=gi[:], op0=ALU.mult, op1=ALU.add
+                out=gi_x0[:], in0=x_bc[:, bb, :, 0], scalar=wx[:, gate * JT + jt, 0:1], in1=gi[:], op0=ALU.mult, op1=ALU.add
             )
+            return gi_x0
+
+        def take_gh_and_join(u, gate, gh, gi_x0):
+            bb, jt = divmod(u, JT)
             gh_x1 = work.tile([P, NB], F32)
             nc.vector.scalar_tensor_tensor(
-                out=gh_x1[:], in0=x_bc[:, bb, :, 1], scalar=wx[:, c, 1:2], in1=gh[:], op0=ALU.mult, op1=ALU.add
+                out=gh_x1[:], in0=x_bc[:, bb, :, 1], scalar=wx[:, gate * JT + jt, 1:2], in1=gh[:], op0=ALU.mult, op1=ALU.add
             )
             total = work.tile([P, NB], F32)
             nc.gpsimd.tensor_tensor(out=total[:], in0=gi_x0[:], in1=gh_x1[:], op=ALU.add)
@@ -208,9 +214,8 @@ def tile_wavernncell_pa_t_kernel(tc, x, feat, aux1, h, w_ih, w_hh_words, w_hh_sc
             nc.scalar.activation(out=value[:], in_=argument[:], func=ACT.Sigmoid, bias=bias_rz[:, c : c + 1], scale=1.0)
             return value
 
-        def candidate(u):
+        def reset_hidden(u, gh):
             c = N_GATE * JT + u % JT
-            gi, gh = n_products[u]
             r_hn = work.tile([P, NB], F32)
             nc.vector.scalar_tensor_tensor(
                 out=r_hn[:],
@@ -220,10 +225,22 @@ def tile_wavernncell_pa_t_kernel(tc, x, feat, aux1, h, w_ih, w_hh_words, w_hh_sc
                 op0=ALU.add,
                 op1=ALU.mult,
             )
+            return r_hn
+
+        def candidate_argument(u, gi):
             n_arg = work.tile([P, NB], F32)
-            nc.vector.tensor_tensor(out=n_arg[:], in0=r_hn[:], in1=gi[:], op=ALU.add)
+            if u % 2 == 0:
+                nc.vector.tensor_tensor(out=n_arg[:], in0=r_hidden[u][:], in1=gi[:], op=ALU.add)
+            else:
+                gi_sb = work.tile([P, NB], F32)
+                nc.scalar.copy(out=gi_sb[:], in_=gi[:])
+                nc.gpsimd.tensor_tensor(out=n_arg[:], in0=r_hidden[u][:], in1=gi_sb[:], op=ALU.add)
+            return n_arg
+
+        def candidate(u):
+            c = N_GATE * JT + u % JT
             n = work.tile([P, NB], F32)
-            nc.scalar.activation(out=n[:], in_=n_arg[:], func=ACT.Tanh, bias=bias[:, c : c + 1], scale=1.0)
+            nc.scalar.activation(out=n[:], in_=n_args[u][:], func=ACT.Tanh, bias=bias[:, c : c + 1], scale=1.0)
             return n
 
         def turn_h(u):
@@ -262,17 +279,25 @@ def tile_wavernncell_pa_t_kernel(tc, x, feat, aux1, h, w_ih, w_hh_words, w_hh_sc
         with tc.manual_schedule():
             for i in range(-2, UNITS + 4):
                 if 0 <= i < UNITS:
-                    r_args[i] = sigmoid_argument(i, R_GATE, r_products[i][0], r_products[i][1])
-                if SUB <= i + 5 < TILES:
-                    quantise(i + 5)
+                    r_half = take_gi(i, R_GATE, r_products[i][0])
+                    r_args[i] = take_gh_and_join(i, R_GATE, r_products[i][1], r_half)
+                if SUB <= i + 5 < TILES and (i + 5) % SUB == SUB - 1:
+                    quantise((i + 5) // SUB)
                 if 0 <= i - 1 < UNITS:
                     z_gate[i - 1] = sigmoid(i - 1, Z_GATE, z_args[i - 1])
                     n_products[i - 1] = products(i - 1, N_GATE)
-                    n_gate[i - 1] = candidate(i - 1)
+                    r_hidden[i - 1] = reset_hidden(i - 1, n_products[i - 1][1])
+                if 0 <= i < UNITS:
+                    z_products[i] = products(i, Z_GATE)
+                    z_halves[i] = take_gi(i, Z_GATE, z_products[i][0])
+                if 0 <= i - 1 < UNITS:
+                    n_args[i - 1] = candidate_argument(i - 1, n_products[i - 1][0])
                 if 0 <= i < UNITS:
                     r_gate[i] = sigmoid(i, R_GATE, r_args[i])
-                    z_products[i] = products(i, Z_GATE)
-                    z_args[i] = sigmoid_argument(i, Z_GATE, z_products[i][0], z_products[i][1])
+                if 0 <= i - 1 < UNITS:
+                    n_gate[i - 1] = candidate(i - 1)
+                if 0 <= i < UNITS:
+                    z_args[i] = take_gh_and_join(i, Z_GATE, z_products[i][1], z_halves[i])
                 if 0 <= i - 2 < UNITS:
                     h_turned[i - 2] = turn_h(i - 2)
                     z_diff[i - 2] = difference(i - 2)

@@ -29,6 +29,7 @@ SUB = NB // P
 NBLK = BATCH // NB
 TILES = BATCH // P
 UNITS = NBLK * JT
+ONES_ROW = P - 3
 
 FLOPS = 2 * BATCH * GATES * HID * (HID + IN)
 
@@ -38,14 +39,23 @@ def tile_wavernncell_pa_t_kernel(tc, x, feat, aux1, h, w_ih, w_hh_words, w_hh_sc
     with ExitStack() as ctx:
         const = ctx.enter_context(tc.tile_pool(name="const", bufs=1))
         operand = ctx.enter_context(tc.tile_pool(name="operand", bufs=3))
-        work = ctx.enter_context(tc.tile_pool(name="work", bufs=4))
+        work = ctx.enter_context(tc.tile_pool(name="work", bufs=2))
+
+        ident_bf = const.tile([P, P], BF16)
+        make_identity(nc, ident_bf[:])
+        ident_f32 = const.tile([P, P], F32)
+        make_identity(nc, ident_f32[:])
 
         w4_scales = const.tile([P, GATES * HID], U8, align_bytes=64)
         nc.vector.memset(w4_scales[:].bitcast(I32), 0)
         bias_rows = const.tile([P, P], BF16)
         nc.vector.memset(bias_rows[:].bitcast(I32), 0)
         x_rows = const.tile([P, BATCH, N_X], BF16)
-        nc.vector.memset(x_rows[:].rearrange("p b c -> p (b c)").bitcast(I32), 0)
+        x_rows_flat = x_rows[:].rearrange("p b c -> p (b c)")
+        nc.vector.memset(x_rows_flat.bitcast(I32), 0)
+        nc.vector.tensor_scalar(
+            out=x_rows_flat, in0=x_rows_flat, scalar1=ident_f32[:, ONES_ROW : ONES_ROW + 1], scalar2=None, op0=ALU.add
+        )
 
         w_sb = const.tile([P, COL_TILES, IN], BF16)
         h_sb = const.tile([P, TILES, HID], BF16)
@@ -80,36 +90,35 @@ def tile_wavernncell_pa_t_kernel(tc, x, feat, aux1, h, w_ih, w_hh_words, w_hh_sc
         load_x(0)
         nc.sync.dma_start(out=bias_rows[0:COL_TILES, :], in_=b_ih.rearrange("(c p) -> c p", p=P))
         nc.sync.dma_start(out=bias_rows[COL_TILES : 2 * COL_TILES, :], in_=b_hh.rearrange("(c p) -> c p", p=P))
-        x_rows_flat = x_rows[:].rearrange("p b c -> p (b c)")
         nc.sync.dma_start(out=x_rows_flat[P - 2 : P - 1, :], in_=x_flat.unsqueeze(0))
         nc.sync.dma_start(out=x_rows_flat[P - 1 : P, 0 : BATCH * N_X - 1], in_=x_flat[1 : BATCH * N_X].unsqueeze(0))
         for bb in range(1, NBLK):
             load_block(bb)
             load_x(bb)
 
-        ident_bf = const.tile([P, P], BF16)
-        make_identity(nc, ident_bf[:])
-        ident_f32 = const.tile([P, P], F32)
-        make_identity(nc, ident_f32[:])
-
         operands = {}
+        turned_inputs = {}
 
         def turn_inputs(t, psum):
+            words = h_sb[:, t, :].bitcast(F32)
+            hw_ps = psum.tile([P, 2, P], F32, tag="hw_ps")
+            for u in range(2):
+                nc.tensor.transpose(out=hw_ps[:, u, :], in_=words[:, u : HID // 2 : 2], identity=ident_f32[:])
+            cat_ps = psum.tile([P, 2, P], BF16, tag="cat_ps")
+            for stream in range(2):
+                nc.tensor.transpose(out=cat_ps[:, stream, :], in_=fa_sb[:, t, stream, :], identity=ident_bf[:])
+            turned_inputs[t] = (hw_ps, cat_ps)
+
+        def keep_inputs(t):
             bb, s = divmod(t, SUB)
             if s == 0:
                 h_codes = operand.tile([P, NB], U32, align_bytes=64)
                 h_scales = operand.tile([P, NB], U8, align_bytes=64)
-                catT = operand.tile([P, 2, NB], BF16)
+                catT = operand.tile([P, 2, NB], BF16, bufs=4)
                 grouped = operand.tile([P, SUB, P * PACK], BF16, align_bytes=64)
                 operands[bb] = (h_codes, h_scales, catT, grouped)
             catT, grouped = operands[bb][2], operands[bb][3]
-            words = h_sb[:, t, :].bitcast(F32)
-            hw_ps = psum.tile([P, 2, P], F32)
-            for u in range(2):
-                nc.tensor.transpose(out=hw_ps[:, u, :], in_=words[:, u : HID // 2 : 2], identity=ident_f32[:])
-            cat_ps = psum.tile([P, 2, P], BF16)
-            for stream in range(2):
-                nc.tensor.transpose(out=cat_ps[:, stream, :], in_=fa_sb[:, t, stream, :], identity=ident_bf[:])
+            hw_ps, cat_ps = turned_inputs[t]
             nc.scalar.copy(
                 out=grouped[:, s, :].bitcast(F32).rearrange("p (b u) -> p b u", u=2), in_=hw_ps[:].rearrange("p u b -> p b u")
             )
@@ -123,8 +132,8 @@ def tile_wavernncell_pa_t_kernel(tc, x, feat, aux1, h, w_ih, w_hh_words, w_hh_sc
 
         with tc.psum_pool(name="psum_setup", bufs=2) as psum_setup:
             wT = const.tile([P, 2, GATES * HID], BF16)
-            for s in range(2):
-                for gate in range(GATES):
+            for gate in range(GATES):
+                for s in range(2):
                     wt_ps = psum_setup.tile([P, HID], BF16, tag="turned")
                     for jt in range(JT):
                         nc.tensor.transpose(
@@ -133,13 +142,6 @@ def tile_wavernncell_pa_t_kernel(tc, x, feat, aux1, h, w_ih, w_hh_words, w_hh_sc
                             identity=ident_bf[:],
                         )
                     nc.scalar.copy(out=wT[:, s, gate * HID : (gate + 1) * HID], in_=wt_ps[:])
-            wxT = const.tile([P, HID], BF16)
-            wx_ps = psum_setup.tile([P, HID], BF16, tag="turned")
-            for jt in range(JT):
-                nc.tensor.transpose(
-                    out=wx_ps[:, jt * P : (jt + 1) * P], in_=w_sb[:, N_GATE * JT + jt, IN - P : IN], identity=ident_bf[:]
-                )
-            nc.scalar.copy(out=wxT[:], in_=wx_ps[:])
             wx = const.tile([P, COL_TILES, N_X], F32)
             nc.vector.tensor_copy(out=wx[:], in_=w_sb[:, :, 2 * STREAM : IN])
             bias_ps = psum_setup.tile([P, P], BF16, tag="turned")
@@ -152,33 +154,31 @@ def tile_wavernncell_pa_t_kernel(tc, x, feat, aux1, h, w_ih, w_hh_words, w_hh_sc
             )
             for t in range(SUB):
                 turn_inputs(t, psum_setup)
+                keep_inputs(t)
             quantise(0)
-
-        psum_mm = ctx.enter_context(tc.psum_pool(name="psum_mm", bufs=2))
-        psum_tr = ctx.enter_context(tc.psum_pool(name="psum_tr", bufs=1))
-
-        r_products, z_products, n_products = {}, {}, {}
-        r_args, z_args, n_args, r_gate, z_gate, n_gate = {}, {}, {}, {}, {}, {}
-        z_halves, r_hidden, h_turned, z_diff = {}, {}, {}, {}
-
-        def products(u, gate):
-            bb, jt = divmod(u, JT)
-            h_codes, h_scales, catT = operands[bb][0], operands[bb][1], operands[bb][2]
-            c = gate * JT + jt
-            gi = psum_mm.tile([P, NB], F32)
-            nc.tensor.matmul(out=gi[:], lhsT=wT[:, 0, c * P : (c + 1) * P], rhs=catT[:, 0, :], start=True, stop=False)
-            nc.tensor.matmul(
-                out=gi[:], lhsT=wT[:, 1, c * P : (c + 1) * P], rhs=catT[:, 1, :], start=False, stop=(gate != N_GATE)
+            nc.vector.tensor_copy(
+                out=w_sb[:, N_GATE * JT : COL_TILES, IN - P + ONES_ROW : IN - P + ONES_ROW + 1],
+                in_=bias[:, N_GATE * JT : COL_TILES].unsqueeze(2),
             )
-            if gate == N_GATE:
-                nc.tensor.matmul(
-                    out=gi[:],
-                    lhsT=wxT[:, jt * P : (jt + 1) * P],
-                    rhs=x_rows[:, bb * NB : (bb + 1) * NB, 0],
-                    start=False,
-                    stop=True,
+            wxT = const.tile([P, HID], BF16)
+            wx_ps = psum_setup.tile([P, HID], BF16, tag="turned")
+            for jt in range(JT):
+                nc.tensor.transpose(
+                    out=wx_ps[:, jt * P : (jt + 1) * P], in_=w_sb[:, N_GATE * JT + jt, IN - P : IN], identity=ident_bf[:]
                 )
-            gh = psum_mm.tile([P, NB], F32)
+            nc.scalar.copy(out=wxT[:], in_=wx_ps[:])
+
+        psum = ctx.enter_context(tc.psum_pool(name="psum", bufs=1))
+
+        r_plain, r_hidden_ps, r_halves, r_args, r_gate = {}, {}, {}, {}, {}
+        reset_hidden, z_hidden, z_input = {}, {}, {}
+        z_bank, n_bank, z_gate, n_gate, h_minus_n, z_diff = {}, {}, {}, {}, {}, {}
+
+        def hidden_product(u, gate):
+            bb, jt = divmod(u, JT)
+            h_codes, h_scales = operands[bb][0], operands[bb][1]
+            c = gate * JT + jt
+            gh = psum.tile([P, NB], F32, tag="gh", bufs=3)
             nc.tensor.matmul_mx(
                 out=gh[:],
                 lhsT=w4_words[:, 2 * c * P : 2 * (c + 1) * P].bitcast(FP4X4),
@@ -188,122 +188,130 @@ def tile_wavernncell_pa_t_kernel(tc, x, feat, aux1, h, w_ih, w_hh_words, w_hh_sc
                 start=True,
                 stop=True,
             )
-            return gi, gh
+            return gh
 
-        def take_gi(u, gate, gi):
+        def r_input_product(u):
             bb, jt = divmod(u, JT)
-            gi_x0 = work.tile([P, NB], F32)
-            nc.vector.scalar_tensor_tensor(
-                out=gi_x0[:], in0=x_bc[:, bb, :, 0], scalar=wx[:, gate * JT + jt, 0:1], in1=gi[:], op0=ALU.mult, op1=ALU.add
-            )
-            return gi_x0
+            catT = operands[bb][2]
+            c = R_GATE * JT + jt
+            gi = psum.tile([P, NB], F32, tag="gi")
+            nc.tensor.matmul(out=gi[:], lhsT=wT[:, 0, c * P : (c + 1) * P], rhs=catT[:, 0, :], start=True, stop=False)
+            nc.tensor.matmul(out=gi[:], lhsT=wT[:, 1, c * P : (c + 1) * P], rhs=catT[:, 1, :], start=False, stop=True)
+            return gi
 
-        def take_gh_and_join(u, gate, gh, gi_x0):
+        def with_x(u, gate, column, product, tag):
             bb, jt = divmod(u, JT)
-            gh_x1 = work.tile([P, NB], F32)
+            total = work.tile([P, NB], F32, tag=tag, bufs=(8 if tag == "z_hidden" else 2))
             nc.vector.scalar_tensor_tensor(
-                out=gh_x1[:], in0=x_bc[:, bb, :, 1], scalar=wx[:, gate * JT + jt, 1:2], in1=gh[:], op0=ALU.mult, op1=ALU.add
+                out=total[:],
+                in0=x_bc[:, bb, :, column],
+                scalar=wx[:, gate * JT + jt, column : column + 1],
+                in1=product[:],
+                op0=ALU.mult,
+                op1=ALU.add,
             )
-            total = work.tile([P, NB], F32)
-            nc.gpsimd.tensor_tensor(out=total[:], in0=gi_x0[:], in1=gh_x1[:], op=ALU.add)
             return total
 
-        def sigmoid(u, gate, argument):
-            c = gate * JT + u % JT
-            value = work.tile([P, NB], F32, tag="gate%d" % gate)
-            nc.scalar.activation(out=value[:], in_=argument[:], func=ACT.Sigmoid, bias=bias_rz[:, c : c + 1], scale=1.0)
-            return value
+        def straight_products(v, gate, tag):
+            bb, s = divmod(v, SUB)
+            catT = operands[bb][2]
+            rows = slice(s * P, (s + 1) * P)
+            cols = slice(gate * HID, (gate + 1) * HID)
+            bank = psum.tile([P, HID], F32, tag=tag)
+            nc.tensor.matmul(out=bank[:], lhsT=catT[:, 0, rows], rhs=wT[:, 0, cols], start=True, stop=False)
+            nc.tensor.matmul(out=bank[:], lhsT=catT[:, 1, rows], rhs=wT[:, 1, cols], start=False, stop=False)
+            if gate == N_GATE:
+                nc.tensor.matmul(out=bank[:], lhsT=x_rows[:, v * P : (v + 1) * P, 0], rhs=wxT[:], start=False, stop=False)
+            return bank
 
-        def reset_hidden(u, gh):
-            c = N_GATE * JT + u % JT
-            r_hn = work.tile([P, NB], F32)
-            nc.vector.scalar_tensor_tensor(
-                out=r_hn[:],
-                in0=gh[:],
-                scalar=bias[:, COL_TILES + c : COL_TILES + c + 1],
-                in1=r_gate[u][:],
-                op0=ALU.add,
-                op1=ALU.mult,
-            )
-            return r_hn
-
-        def candidate_argument(u, gi):
-            n_arg = work.tile([P, NB], F32)
-            if u % 2 == 0:
-                nc.vector.tensor_tensor(out=n_arg[:], in0=r_hidden[u][:], in1=gi[:], op=ALU.add)
-            else:
-                gi_sb = work.tile([P, NB], F32)
-                nc.scalar.copy(out=gi_sb[:], in_=gi[:])
-                nc.gpsimd.tensor_tensor(out=n_arg[:], in0=r_hidden[u][:], in1=gi_sb[:], op=ALU.add)
-            return n_arg
-
-        def candidate(u):
-            c = N_GATE * JT + u % JT
-            n = work.tile([P, NB], F32)
-            nc.scalar.activation(out=n[:], in_=n_args[u][:], func=ACT.Tanh, bias=bias[:, c : c + 1], scale=1.0)
-            return n
-
-        def turn_h(u):
-            bb, jt = divmod(u, JT)
-            hT_ps = psum_tr.tile([P, NB], BF16)
-            for s in range(SUB):
-                nc.tensor.transpose(
-                    out=hT_ps[:, s * P : (s + 1) * P], in_=h_sb[:, bb * SUB + s, jt * P : (jt + 1) * P], identity=ident_bf[:]
-                )
-            return hT_ps
-
-        def difference(u):
-            h_minus_n = work.tile([P, NB], F32)
-            nc.vector.tensor_tensor(out=h_minus_n[:], in0=h_turned[u][:], in1=n_gate[u][:], op=ALU.subtract)
-            diff = work.tile([P, NB], F32)
-            nc.gpsimd.tensor_tensor(out=diff[:], in0=z_gate[u][:], in1=h_minus_n[:], op=ALU.mult)
-            return diff
-
-        out_view = out.rearrange("(t p) j -> p t j", p=P)
-
-        def finish(u):
-            bb, jt = divmod(u, JT)
-            out_ps = psum_tr.tile([P, SUB, P], F32)
-            for s in range(SUB):
-                rows = slice(s * P, (s + 1) * P)
-                nc.tensor.matmul(
-                    out=out_ps[:, s, :], lhsT=n_gate[u][:, rows], rhs=ident_f32[:], is_transpose=True, start=True, stop=False
-                )
-                nc.tensor.matmul(
-                    out=out_ps[:, s, :], lhsT=z_diff[u][:, rows], rhs=ident_f32[:], is_transpose=True, start=False, stop=True
-                )
-            res = work.tile([P, SUB, P], F32)
-            nc.scalar.copy(out=res[:], in_=out_ps[:])
-            nc.sync.dma_start(out=out_view[:, bb * SUB : (bb + 1) * SUB, jt * P : (jt + 1) * P], in_=res[:])
+        def add_turned(v, bank, sources):
+            bb, s = divmod(v, SUB)
+            rows = slice(s * P, (s + 1) * P)
+            for jt in range(JT):
+                for k, source in enumerate(sources):
+                    nc.tensor.matmul(
+                        out=bank[:, jt * P : (jt + 1) * P],
+                        lhsT=source[bb * JT + jt][:, rows],
+                        rhs=ident_f32[:],
+                        is_transpose=True,
+                        start=False,
+                        stop=(jt == JT - 1 and k == len(sources) - 1),
+                    )
 
         with tc.manual_schedule():
-            for i in range(-2, UNITS + 4):
+            for i in range(-2, UNITS + 10):
                 if 0 <= i < UNITS:
-                    r_half = take_gi(i, R_GATE, r_products[i][0])
-                    r_args[i] = take_gh_and_join(i, R_GATE, r_products[i][1], r_half)
+                    r_plain[i] = r_input_product(i)
+                    r_hidden_ps[i] = hidden_product(i, R_GATE)
+                    r_halves[i] = (
+                        with_x(i, R_GATE, 0, r_plain[i], "r_half0"),
+                        with_x(i, R_GATE, 1, r_hidden_ps[i], "r_half1"),
+                    )
+                if 0 <= i - 7 < TILES:
+                    v = i - 7
+                    h_minus_n[v] = work.tile([P, HID], F32, name="h_minus_n", tag="h_minus_n", bufs=3)
+                    nc.gpsimd.tensor_tensor(out=h_minus_n[v][:], in0=h_sb[:, v, :], in1=n_gate[v][:], op=ALU.subtract)
+                if 0 <= i < UNITS:
+                    r_args[i] = work.tile([P, NB], F32, name="r_arg", tag="r_arg")
+                    nc.gpsimd.tensor_tensor(out=r_args[i][:], in0=r_halves[i][0][:], in1=r_halves[i][1][:], op=ALU.add)
+                if 0 <= i - 1 < UNITS:
+                    u = i - 1
+                    gh_n = hidden_product(u, N_GATE)
+                    c = N_GATE * JT + u % JT
+                    reset_hidden[u] = work.tile([P, NB], F32, name="reset_hidden", tag="reset_hidden", bufs=8)
+                    nc.vector.scalar_tensor_tensor(
+                        out=reset_hidden[u][:],
+                        in0=gh_n[:],
+                        scalar=bias[:, COL_TILES + c : COL_TILES + c + 1],
+                        in1=r_gate[u][:],
+                        op0=ALU.add,
+                        op1=ALU.mult,
+                    )
+                if 0 <= i < UNITS:
+                    gh_z = hidden_product(i, Z_GATE)
+                    z_hidden[i] = with_x(i, Z_GATE, 1, gh_z, "z_hidden")
+                if 0 <= i - 4 < TILES:
+                    z_bank[i - 4] = straight_products(i - 4, Z_GATE, "z_bank")
+                if 0 <= i - 5 < TILES:
+                    n_bank[i - 5] = straight_products(i - 5, N_GATE, "n_bank")
+                if 0 <= i - 4 < TILES:
+                    add_turned(i - 4, z_bank[i - 4], (z_hidden, z_input))
+                if 0 <= i - 5 < TILES:
+                    add_turned(i - 5, n_bank[i - 5], (reset_hidden,))
+                if SUB <= i + 6 < TILES:
+                    turn_inputs(i + 6, psum)
+                if 0 <= i - 8 < TILES:
+                    v = i - 8
+                    z_diff[v] = work.tile([P, HID], F32, name="z_diff", tag="z_diff")
+                    nc.vector.tensor_tensor(out=z_diff[v][:], in0=z_gate[v][:], in1=h_minus_n[v][:], op=ALU.mult)
+                if 0 <= i - 9 < TILES:
+                    v = i - 9
+                    res = work.tile([P, HID], F32, tag="res", bufs=4)
+                    nc.vector.tensor_tensor(out=res[:], in0=n_gate[v][:], in1=z_diff[v][:], op=ALU.add)
+                    nc.sync.dma_start(out=out[v * P : (v + 1) * P, :], in_=res[:])
                 if SUB <= i + 5 < TILES and (i + 5) % SUB == SUB - 1:
                     quantise((i + 5) // SUB)
-                if 0 <= i - 1 < UNITS:
-                    z_gate[i - 1] = sigmoid(i - 1, Z_GATE, z_args[i - 1])
-                    n_products[i - 1] = products(i - 1, N_GATE)
-                    r_hidden[i - 1] = reset_hidden(i - 1, n_products[i - 1][1])
                 if 0 <= i < UNITS:
-                    z_products[i] = products(i, Z_GATE)
-                    z_halves[i] = take_gi(i, Z_GATE, z_products[i][0])
-                if 0 <= i - 1 < UNITS:
-                    n_args[i - 1] = candidate_argument(i - 1, n_products[i - 1][0])
-                if 0 <= i < UNITS:
-                    r_gate[i] = sigmoid(i, R_GATE, r_args[i])
-                if 0 <= i - 1 < UNITS:
-                    n_gate[i - 1] = candidate(i - 1)
-                if 0 <= i < UNITS:
-                    z_args[i] = take_gh_and_join(i, Z_GATE, z_products[i][1], z_halves[i])
-                if 0 <= i - 2 < UNITS:
-                    h_turned[i - 2] = turn_h(i - 2)
-                    z_diff[i - 2] = difference(i - 2)
-                if 0 <= i - 3 < UNITS:
-                    finish(i - 3)
+                    c = R_GATE * JT + i % JT
+                    r_gate[i] = work.tile([P, NB], F32, name="r_gate", tag="r_gate", bufs=3)
+                    nc.scalar.activation(
+                        out=r_gate[i][:], in_=r_args[i][:], func=ACT.Sigmoid, bias=bias_rz[:, c : c + 1], scale=1.0
+                    )
+                if 0 <= i - 4 < TILES:
+                    z_gate[i - 4] = work.tile([P, HID], F32, name="z_gate", tag="z_gate", bufs=5)
+                    nc.scalar.activation(out=z_gate[i - 4][:], in_=z_bank[i - 4][:], func=ACT.Sigmoid)
+                if 0 <= i - 5 < TILES:
+                    n_gate[i - 5] = work.tile([P, HID], F32, name="n_gate", tag="n_gate", bufs=5)
+                    nc.scalar.activation(out=n_gate[i - 5][:], in_=n_bank[i - 5][:], func=ACT.Tanh)
                 if SUB <= i + 6 < TILES:
-                    turn_inputs(i + 6, psum_tr)
-                if 0 <= i + 1 < UNITS:
-                    r_products[i + 1] = products(i + 1, R_GATE)
+                    keep_inputs(i + 6)
+                if 0 <= i < UNITS:
+                    c = Z_GATE * JT + i % JT
+                    z_input[i] = work.tile([P, NB], F32, name="z_input", tag="z_input", bufs=8)
+                    nc.scalar.activation(
+                        out=z_input[i][:],
+                        in_=x_bc[:, i // JT, :, 0],
+                        func=ACT.Identity,
+                        bias=bias_rz[:, c : c + 1],
+                        scale=wx[:, c, 0:1],
+                    )

@@ -69,9 +69,9 @@ def tile_wavernncell_pa_t_kernel(tc, x, feat, aux1, h, w_ih, w_hh_words, w_hh_sc
 
         def load_block(bb):
             tiles = slice(bb * SUB, (bb + 1) * SUB)
-            nc.sync.dma_start(out=h_sb[:, tiles, :], in_=h_view[:, tiles, :])
             nc.sync.dma_start(out=fa_sb[:, tiles, 0, :], in_=feat_view[:, tiles, :])
             nc.sync.dma_start(out=fa_sb[:, tiles, 1, :], in_=aux_view[:, tiles, :])
+            nc.sync.dma_start(out=h_sb[:, tiles, :], in_=h_view[:, tiles, :])
 
         def load_x(bb):
             nc.sync.dma_start(
@@ -79,7 +79,8 @@ def tile_wavernncell_pa_t_kernel(tc, x, feat, aux1, h, w_ih, w_hh_words, w_hh_sc
                 in_=x_flat[bb * NB * N_X : (bb + 1) * NB * N_X].partition_broadcast(P),
             )
 
-        nc.sync.dma_start(out=w_sb[:], in_=w_ih.rearrange("(c p) k -> p c k", p=P))
+        w_view = w_ih.rearrange("(c p) k -> p c k", p=P)
+        nc.sync.dma_start(out=w_sb[:, 0:JT, :], in_=w_view[:, 0:JT, :])
         load_block(0)
         nc.sync.dma_start(out=w4_words[:].bitcast(I32), in_=w_hh_words[0].bitcast(I32))
         for quad in range(4):
@@ -90,26 +91,29 @@ def tile_wavernncell_pa_t_kernel(tc, x, feat, aux1, h, w_ih, w_hh_words, w_hh_sc
         load_x(0)
         nc.sync.dma_start(out=bias_rows[0:COL_TILES, :], in_=b_ih.rearrange("(c p) -> c p", p=P))
         nc.sync.dma_start(out=bias_rows[COL_TILES : 2 * COL_TILES, :], in_=b_hh.rearrange("(c p) -> c p", p=P))
+        nc.sync.dma_start(out=w_sb[:, JT:COL_TILES, :], in_=w_view[:, JT:COL_TILES, :])
+        load_block(1)
+        load_x(1)
         nc.sync.dma_start(out=x_rows_flat[P - 2 : P - 1, :], in_=x_flat.unsqueeze(0))
         nc.sync.dma_start(out=x_rows_flat[P - 1 : P, 0 : BATCH * N_X - 1], in_=x_flat[1 : BATCH * N_X].unsqueeze(0))
-        for bb in range(1, NBLK):
+        for bb in range(2, NBLK):
             load_block(bb)
             load_x(bb)
 
         operands = {}
         turned_inputs = {}
 
-        def turn_inputs(t, psum):
+        def turn_inputs(t, pool, hw_tag, cat_tag):
             words = h_sb[:, t, :].bitcast(F32)
-            hw_ps = psum.tile([P, 2, P], F32, tag="hw_ps")
+            hw_ps = pool.tile([P, 2, P], F32, tag=hw_tag)
             for u in range(2):
                 nc.tensor.transpose(out=hw_ps[:, u, :], in_=words[:, u : HID // 2 : 2], identity=ident_f32[:])
-            cat_ps = psum.tile([P, 2, P], BF16, tag="cat_ps")
+            cat_ps = pool.tile([P, 2, P], BF16, tag=cat_tag)
             for stream in range(2):
                 nc.tensor.transpose(out=cat_ps[:, stream, :], in_=fa_sb[:, t, stream, :], identity=ident_bf[:])
             turned_inputs[t] = (hw_ps, cat_ps)
 
-        def keep_inputs(t):
+        def keep_inputs(t, copy_words):
             bb, s = divmod(t, SUB)
             if s == 0:
                 h_codes = operand.tile([P, NB], U32, align_bytes=64)
@@ -119,7 +123,7 @@ def tile_wavernncell_pa_t_kernel(tc, x, feat, aux1, h, w_ih, w_hh_words, w_hh_sc
                 operands[bb] = (h_codes, h_scales, catT, grouped)
             catT, grouped = operands[bb][2], operands[bb][3]
             hw_ps, cat_ps = turned_inputs[t]
-            nc.scalar.copy(
+            copy_words(
                 out=grouped[:, s, :].bitcast(F32).rearrange("p (b u) -> p b u", u=2), in_=hw_ps[:].rearrange("p u b -> p b u")
             )
             nc.scalar.copy(out=catT[:, :, s * P : (s + 1) * P], in_=cat_ps[:])
@@ -130,20 +134,29 @@ def tile_wavernncell_pa_t_kernel(tc, x, feat, aux1, h, w_ih, w_hh_words, w_hh_sc
                 out=h_codes[:].bitcast(FP8X4), scales=h_scales[:], in_=grouped[:].rearrange("p s e -> p (s e)")
             )
 
+        wT = const.tile([P, 2, GATES * HID], BF16)
+        wx = const.tile([P, COL_TILES, N_X], F32)
+        wxT = const.tile([P, HID], BF16)
+
+        def turn_weights(gate, first_column, pool, tag):
+            wt_ps = pool.tile([P, HID], BF16, tag=tag)
+            for jt in range(JT):
+                nc.tensor.transpose(
+                    out=wt_ps[:, jt * P : (jt + 1) * P],
+                    in_=w_sb[:, gate * JT + jt, first_column : first_column + P],
+                    identity=ident_bf[:],
+                )
+            return wt_ps
+
         with tc.psum_pool(name="psum_setup", bufs=2) as psum_setup:
-            wT = const.tile([P, 2, GATES * HID], BF16)
-            for gate in range(GATES):
-                for s in range(2):
-                    wt_ps = psum_setup.tile([P, HID], BF16, tag="turned")
-                    for jt in range(JT):
-                        nc.tensor.transpose(
-                            out=wt_ps[:, jt * P : (jt + 1) * P],
-                            in_=w_sb[:, gate * JT + jt, s * STREAM : (s + 1) * STREAM],
-                            identity=ident_bf[:],
-                        )
-                    nc.scalar.copy(out=wT[:, s, gate * HID : (gate + 1) * HID], in_=wt_ps[:])
-            wx = const.tile([P, COL_TILES, N_X], F32)
-            nc.vector.tensor_copy(out=wx[:], in_=w_sb[:, :, 2 * STREAM : IN])
+            for s in range(2):
+                wt_ps = turn_weights(R_GATE, s * STREAM, psum_setup, "turned")
+                nc.scalar.copy(out=wT[:, s, 0:HID], in_=wt_ps[:])
+            nc.vector.tensor_copy(out=wx[:, 0:JT, :], in_=w_sb[:, 0:JT, 2 * STREAM : IN])
+            for t in range(SUB):
+                turn_inputs(t, psum_setup, "hw_ps", "cat_ps")
+                keep_inputs(t, nc.vector.tensor_copy)
+            quantise(0)
             bias_ps = psum_setup.tile([P, P], BF16, tag="turned")
             nc.tensor.transpose(out=bias_ps[:], in_=bias_rows[:], identity=ident_bf[:])
             bias = const.tile([P, 2 * COL_TILES], F32)
@@ -152,21 +165,6 @@ def tile_wavernncell_pa_t_kernel(tc, x, feat, aux1, h, w_ih, w_hh_words, w_hh_sc
             nc.vector.tensor_tensor(
                 out=bias_rz[:], in0=bias[:, 0 : 2 * JT], in1=bias[:, COL_TILES : COL_TILES + 2 * JT], op=ALU.add
             )
-            for t in range(SUB):
-                turn_inputs(t, psum_setup)
-                keep_inputs(t)
-            quantise(0)
-            nc.vector.tensor_copy(
-                out=w_sb[:, N_GATE * JT : COL_TILES, IN - P + ONES_ROW : IN - P + ONES_ROW + 1],
-                in_=bias[:, N_GATE * JT : COL_TILES].unsqueeze(2),
-            )
-            wxT = const.tile([P, HID], BF16)
-            wx_ps = psum_setup.tile([P, HID], BF16, tag="turned")
-            for jt in range(JT):
-                nc.tensor.transpose(
-                    out=wx_ps[:, jt * P : (jt + 1) * P], in_=w_sb[:, N_GATE * JT + jt, IN - P : IN], identity=ident_bf[:]
-                )
-            nc.scalar.copy(out=wxT[:], in_=wx_ps[:])
 
         psum = ctx.enter_context(tc.psum_pool(name="psum", bufs=1))
 
@@ -239,7 +237,9 @@ def tile_wavernncell_pa_t_kernel(tc, x, feat, aux1, h, w_ih, w_hh_words, w_hh_sc
                     )
 
         with tc.manual_schedule():
-            for i in range(-2, UNITS + 10):
+            for i in range(UNITS + 10):
+                turning = (2 * i + SUB, 2 * i + SUB + 1) if i < 2 else (i + 6,) if i + 6 < TILES else ()
+                late_weights = {2: Z_GATE, 3: N_GATE}.get(i)
                 if 0 <= i < UNITS:
                     r_plain[i] = r_input_product(i)
                     r_hidden_ps[i] = hidden_product(i, R_GATE)
@@ -247,6 +247,8 @@ def tile_wavernncell_pa_t_kernel(tc, x, feat, aux1, h, w_ih, w_hh_words, w_hh_sc
                         with_x(i, R_GATE, 0, r_plain[i], "r_half0"),
                         with_x(i, R_GATE, 1, r_hidden_ps[i], "r_half1"),
                     )
+                if i == 0:
+                    nc.vector.tensor_copy(out=wx[:, JT:COL_TILES, :], in_=w_sb[:, JT:COL_TILES, 2 * STREAM : IN])
                 if 0 <= i - 7 < TILES:
                     v = i - 7
                     h_minus_n[v] = work.tile([P, HID], F32, name="h_minus_n", tag="h_minus_n", bufs=3)
@@ -274,12 +276,22 @@ def tile_wavernncell_pa_t_kernel(tc, x, feat, aux1, h, w_ih, w_hh_words, w_hh_sc
                     z_bank[i - 4] = straight_products(i - 4, Z_GATE, "z_bank")
                 if 0 <= i - 5 < TILES:
                     n_bank[i - 5] = straight_products(i - 5, N_GATE, "n_bank")
+                if i == 4:
+                    nc.vector.tensor_copy(
+                        out=w_sb[:, N_GATE * JT : COL_TILES, IN - P + ONES_ROW : IN - P + ONES_ROW + 1],
+                        in_=bias[:, N_GATE * JT : COL_TILES].unsqueeze(2),
+                    )
+                    wx_ps = turn_weights(N_GATE, IN - P, psum, "n_bank")
                 if 0 <= i - 4 < TILES:
                     add_turned(i - 4, z_bank[i - 4], (z_hidden, z_input))
                 if 0 <= i - 5 < TILES:
                     add_turned(i - 5, n_bank[i - 5], (reset_hidden,))
-                if SUB <= i + 6 < TILES:
-                    turn_inputs(i + 6, psum)
+                if late_weights is not None:
+                    late_feat = turn_weights(late_weights, 0, psum, "z_bank")
+                    late_aux = turn_weights(late_weights, STREAM, psum, "n_bank")
+                    nc.vector.tensor_copy(out=wT[:, 1, late_weights * HID : (late_weights + 1) * HID], in_=late_aux[:])
+                for k, t in enumerate(turning):
+                    turn_inputs(t, psum, "hw_ps" if k == 0 else "z_bank", "cat_ps" if k == 0 else "n_bank")
                 if 0 <= i - 8 < TILES:
                     v = i - 8
                     z_diff[v] = work.tile([P, HID], F32, name="z_diff", tag="z_diff")
@@ -303,8 +315,12 @@ def tile_wavernncell_pa_t_kernel(tc, x, feat, aux1, h, w_ih, w_hh_words, w_hh_sc
                 if 0 <= i - 5 < TILES:
                     n_gate[i - 5] = work.tile([P, HID], F32, name="n_gate", tag="n_gate", bufs=5)
                     nc.scalar.activation(out=n_gate[i - 5][:], in_=n_bank[i - 5][:], func=ACT.Tanh)
-                if SUB <= i + 6 < TILES:
-                    keep_inputs(i + 6)
+                if late_weights is not None:
+                    nc.scalar.copy(out=wT[:, 0, late_weights * HID : (late_weights + 1) * HID], in_=late_feat[:])
+                if i == 4:
+                    nc.scalar.copy(out=wxT[:], in_=wx_ps[:])
+                for t in turning:
+                    keep_inputs(t, nc.scalar.copy)
                 if 0 <= i < UNITS:
                     c = Z_GATE * JT + i % JT
                     z_input[i] = work.tile([P, NB], F32, name="z_input", tag="z_input", bufs=8)

@@ -210,12 +210,12 @@ def tile_wavernncell_pa_t_kernel(tc, x, feat, aux1, h, w_ih, w_hh_words, w_hh_sc
             )
             return total
 
-        def straight_products(v, gate, tag):
+        def straight_products(v, gate, tag, bufs):
             bb, s = divmod(v, SUB)
             catT = operands[bb][2]
             rows = slice(s * P, (s + 1) * P)
             cols = slice(gate * HID, (gate + 1) * HID)
-            bank = psum.tile([P, HID], F32, tag=tag)
+            bank = psum.tile([P, HID], F32, tag=tag, bufs=bufs)
             nc.tensor.matmul(out=bank[:], lhsT=catT[:, 0, rows], rhs=wT[:, 0, cols], start=True, stop=False)
             nc.tensor.matmul(out=bank[:], lhsT=catT[:, 1, rows], rhs=wT[:, 1, cols], start=False, stop=False)
             if gate == N_GATE:
@@ -252,7 +252,8 @@ def tile_wavernncell_pa_t_kernel(tc, x, feat, aux1, h, w_ih, w_hh_words, w_hh_sc
                 if 0 <= i - 7 < TILES:
                     v = i - 7
                     h_minus_n[v] = work.tile([P, HID], F32, name="h_minus_n", tag="h_minus_n", bufs=3)
-                    nc.gpsimd.tensor_tensor(out=h_minus_n[v][:], in0=h_sb[:, v, :], in1=n_gate[v][:], op=ALU.subtract)
+                    subtractor = nc.vector if v == TILES - 1 else nc.gpsimd
+                    subtractor.tensor_tensor(out=h_minus_n[v][:], in0=h_sb[:, v, :], in1=n_gate[v][:], op=ALU.subtract)
                 if 0 <= i < UNITS:
                     r_args[i] = work.tile([P, NB], F32, name="r_arg", tag="r_arg")
                     nc.gpsimd.tensor_tensor(out=r_args[i][:], in0=r_halves[i][0][:], in1=r_halves[i][1][:], op=ALU.add)
@@ -272,10 +273,17 @@ def tile_wavernncell_pa_t_kernel(tc, x, feat, aux1, h, w_ih, w_hh_words, w_hh_sc
                 if 0 <= i < UNITS:
                     gh_z = hidden_product(i, Z_GATE)
                     z_hidden[i] = with_x(i, Z_GATE, 1, gh_z, "z_hidden")
+                mx_done = i > UNITS
                 if 0 <= i - 4 < TILES:
-                    z_bank[i - 4] = straight_products(i - 4, Z_GATE, "z_bank")
+                    if mx_done and (i - 4) % 2 == 1:
+                        z_bank[i - 4] = straight_products(i - 4, Z_GATE, "gh", 3)
+                    else:
+                        z_bank[i - 4] = straight_products(i - 4, Z_GATE, "z_bank", 1)
                 if 0 <= i - 5 < TILES:
-                    n_bank[i - 5] = straight_products(i - 5, N_GATE, "n_bank")
+                    if mx_done and (i - 5) % 2 == 1:
+                        n_bank[i - 5] = straight_products(i - 5, N_GATE, "gh", 3)
+                    else:
+                        n_bank[i - 5] = straight_products(i - 5, N_GATE, "n_bank", 1)
                 if i == 4:
                     nc.vector.tensor_copy(
                         out=w_sb[:, N_GATE * JT : COL_TILES, IN - P + ONES_ROW : IN - P + ONES_ROW + 1],

@@ -237,7 +237,7 @@ def tile_wavernncell_pa_t_kernel(tc, x, feat, aux1, h, w_ih, w_hh_words, w_hh_sc
                     )
 
         with tc.manual_schedule():
-            for i in range(UNITS + 10):
+            for i in range(UNITS + 9):
                 turning = (2 * i + SUB, 2 * i + SUB + 1) if i < 2 else (i + 6,) if i + 6 < TILES else ()
                 late_weights = {2: Z_GATE, 3: N_GATE}.get(i)
                 if 0 <= i < UNITS:
@@ -274,26 +274,28 @@ def tile_wavernncell_pa_t_kernel(tc, x, feat, aux1, h, w_ih, w_hh_words, w_hh_sc
                     gh_z = hidden_product(i, Z_GATE)
                     z_hidden[i] = with_x(i, Z_GATE, 1, gh_z, "z_hidden")
                 mx_done = i > UNITS
-                if 0 <= i - 4 < TILES:
-                    if mx_done and (i - 4) % 2 == 1:
-                        z_bank[i - 4] = straight_products(i - 4, Z_GATE, "gh", 3)
+                z_tiles = [v for v in (i - 4,) if 0 <= v < TILES - 1] + ([TILES - 1] if i == TILES + 4 else [])
+                n_tiles = [v for v in (i - 5,) if 0 <= v < TILES - 1] + ([TILES - 1] if i == TILES + 3 else [])
+                for v in z_tiles:
+                    if mx_done and v % 2 == 1:
+                        z_bank[v] = straight_products(v, Z_GATE, "gh", 3)
                     else:
-                        z_bank[i - 4] = straight_products(i - 4, Z_GATE, "z_bank", 1)
-                if 0 <= i - 5 < TILES:
-                    if mx_done and (i - 5) % 2 == 1:
-                        n_bank[i - 5] = straight_products(i - 5, N_GATE, "gh", 3)
+                        z_bank[v] = straight_products(v, Z_GATE, "z_bank", 1)
+                for v in n_tiles:
+                    if mx_done and v % 2 == 1:
+                        n_bank[v] = straight_products(v, N_GATE, "gh", 3)
                     else:
-                        n_bank[i - 5] = straight_products(i - 5, N_GATE, "n_bank", 1)
+                        n_bank[v] = straight_products(v, N_GATE, "n_bank", 1)
                 if i == 4:
                     nc.vector.tensor_copy(
                         out=w_sb[:, N_GATE * JT : COL_TILES, IN - P + ONES_ROW : IN - P + ONES_ROW + 1],
                         in_=bias[:, N_GATE * JT : COL_TILES].unsqueeze(2),
                     )
                     wx_ps = turn_weights(N_GATE, IN - P, psum, "n_bank")
-                if 0 <= i - 4 < TILES:
-                    add_turned(i - 4, z_bank[i - 4], (z_hidden, z_input))
-                if 0 <= i - 5 < TILES:
-                    add_turned(i - 5, n_bank[i - 5], (reset_hidden,))
+                for v in z_tiles:
+                    add_turned(v, z_bank[v], (z_hidden, z_input))
+                for v in n_tiles:
+                    add_turned(v, n_bank[v], (reset_hidden,))
                 if late_weights is not None:
                     late_feat = turn_weights(late_weights, 0, psum, "z_bank")
                     late_aux = turn_weights(late_weights, STREAM, psum, "n_bank")
@@ -302,13 +304,13 @@ def tile_wavernncell_pa_t_kernel(tc, x, feat, aux1, h, w_ih, w_hh_words, w_hh_sc
                     turn_inputs(t, psum, "hw_ps" if k == 0 else "z_bank", "cat_ps" if k == 0 else "n_bank")
                 if 0 <= i - 8 < TILES:
                     v = i - 8
-                    z_diff[v] = work.tile([P, HID], F32, name="z_diff", tag="z_diff")
-                    nc.vector.tensor_tensor(out=z_diff[v][:], in0=z_gate[v][:], in1=h_minus_n[v][:], op=ALU.mult)
-                if 0 <= i - 9 < TILES:
-                    v = i - 9
                     res = work.tile([P, HID], F32, tag="res", bufs=4)
                     nc.vector.tensor_tensor(out=res[:], in0=n_gate[v][:], in1=z_diff[v][:], op=ALU.add)
                     nc.sync.dma_start(out=out[v * P : (v + 1) * P, :], in_=res[:])
+                if 0 <= i - 7 < TILES:
+                    v = i - 7
+                    z_diff[v] = work.tile([P, HID], F32, name="z_diff", tag="z_diff")
+                    nc.vector.tensor_tensor(out=z_diff[v][:], in0=z_gate[v][:], in1=h_minus_n[v][:], op=ALU.mult)
                 if SUB <= i + 5 < TILES and (i + 5) % SUB == SUB - 1:
                     quantise((i + 5) // SUB)
                 if 0 <= i < UNITS:
@@ -317,12 +319,12 @@ def tile_wavernncell_pa_t_kernel(tc, x, feat, aux1, h, w_ih, w_hh_words, w_hh_sc
                     nc.scalar.activation(
                         out=r_gate[i][:], in_=r_args[i][:], func=ACT.Sigmoid, bias=bias_rz[:, c : c + 1], scale=1.0
                     )
-                if 0 <= i - 4 < TILES:
-                    z_gate[i - 4] = work.tile([P, HID], F32, name="z_gate", tag="z_gate", bufs=5)
-                    nc.scalar.activation(out=z_gate[i - 4][:], in_=z_bank[i - 4][:], func=ACT.Sigmoid)
-                if 0 <= i - 5 < TILES:
-                    n_gate[i - 5] = work.tile([P, HID], F32, name="n_gate", tag="n_gate", bufs=5)
-                    nc.scalar.activation(out=n_gate[i - 5][:], in_=n_bank[i - 5][:], func=ACT.Tanh)
+                for v in z_tiles:
+                    z_gate[v] = work.tile([P, HID], F32, name="z_gate", tag="z_gate", bufs=5)
+                    nc.scalar.activation(out=z_gate[v][:], in_=z_bank[v][:], func=ACT.Sigmoid)
+                for v in n_tiles:
+                    n_gate[v] = work.tile([P, HID], F32, name="n_gate", tag="n_gate", bufs=5)
+                    nc.scalar.activation(out=n_gate[v][:], in_=n_bank[v][:], func=ACT.Tanh)
                 if late_weights is not None:
                     nc.scalar.copy(out=wT[:, 0, late_weights * HID : (late_weights + 1) * HID], in_=late_feat[:])
                 if i == 4:

@@ -252,7 +252,7 @@ def tile_wavernncell_pa_t_kernel(tc, x, feat, aux1, h, w_ih, w_hh_words, w_hh_sc
                 if 0 <= i - 7 < TILES:
                     v = i - 7
                     h_minus_n[v] = work.tile([P, HID], F32, name="h_minus_n", tag="h_minus_n", bufs=3)
-                    subtractor = nc.vector if v == TILES - 1 else nc.gpsimd
+                    subtractor = nc.vector if i > UNITS else nc.gpsimd
                     subtractor.tensor_tensor(out=h_minus_n[v][:], in0=h_sb[:, v, :], in1=n_gate[v][:], op=ALU.subtract)
                 if 0 <= i < UNITS:
                     r_args[i] = work.tile([P, NB], F32, name="r_arg", tag="r_arg")

@@ -46,21 +46,23 @@ def tile_wavernncell_pa_t_kernel(tc, x, feat, aux1, h, w_ih, w_hh_words, w_hh_sc
         ident_f32 = const.tile([P, P], F32)
         make_identity(nc, ident_f32[:])
 
+        table_use = const.tile([P, 1], F32)
+        nc.scalar.activation(out=table_use[:], in_=ident_f32[:, 0:1], func=ACT.Sigmoid)
+
         w4_scales = const.tile([P, GATES * HID], U8, align_bytes=64)
         nc.vector.memset(w4_scales[:].bitcast(I32), 0)
         bias_rows = const.tile([P, P], BF16)
         nc.vector.memset(bias_rows[:].bitcast(I32), 0)
         x_rows = const.tile([P, BATCH, N_X], BF16)
         x_rows_flat = x_rows[:].rearrange("p b c -> p (b c)")
-        nc.vector.memset(x_rows_flat.bitcast(I32), 0)
-        nc.vector.tensor_scalar(
-            out=x_rows_flat, in0=x_rows_flat, scalar1=ident_f32[:, ONES_ROW : ONES_ROW + 1], scalar2=None, op0=ALU.add
-        )
+        x_head = 2 * NB * N_X
+        nc.vector.tensor_copy(out=x_rows_flat[:, 0:x_head], in_=ident_bf[:, ONES_ROW : ONES_ROW + 1].to_broadcast([P, x_head]))
 
         w_sb = const.tile([P, COL_TILES, IN], BF16)
         h_sb = const.tile([P, TILES, HID], BF16)
         fa_sb = const.tile([P, TILES, 2, STREAM], BF16)
         x_bc = const.tile([P, NBLK, NB, N_X], BF16)
+        x_cols = const.tile([P, SUB, N_X], BF16)
         w4_words = const.tile([P, 2 * GATES * HID], U8, align_bytes=64)
         h_view = h.rearrange("(t p) k -> p t k", p=P)
         feat_view = feat.rearrange("(t p) k -> p t k", p=P)
@@ -81,6 +83,7 @@ def tile_wavernncell_pa_t_kernel(tc, x, feat, aux1, h, w_ih, w_hh_words, w_hh_sc
 
         w_view = w_ih.rearrange("(c p) k -> p c k", p=P)
         nc.sync.dma_start(out=w_sb[:, 0:JT, :], in_=w_view[:, 0:JT, :])
+        nc.sync.dma_start(out=x_cols[:], in_=x[0:NB, :].rearrange("(s p) c -> p s c", p=P))
         load_block(0)
         nc.sync.dma_start(out=w4_words[:].bitcast(I32), in_=w_hh_words[0].bitcast(I32))
         for quad in range(4):
@@ -88,30 +91,30 @@ def tile_wavernncell_pa_t_kernel(tc, x, feat, aux1, h, w_ih, w_hh_words, w_hh_sc
                 out=w4_scales[32 * quad : 32 * quad + 4, :].bitcast(I32),
                 in_=w_hh_scales[0, 4 * quad : 4 * quad + 4, :].bitcast(I32),
             )
-        load_x(0)
         nc.sync.dma_start(out=bias_rows[0:COL_TILES, :], in_=b_ih.rearrange("(c p) -> c p", p=P))
         nc.sync.dma_start(out=bias_rows[COL_TILES : 2 * COL_TILES, :], in_=b_hh.rearrange("(c p) -> c p", p=P))
         nc.sync.dma_start(out=w_sb[:, JT:COL_TILES, :], in_=w_view[:, JT:COL_TILES, :])
         load_block(1)
+        nc.sync.dma_start(out=x_rows_flat[P - 2 : P - 1, 0:x_head], in_=x_flat[0:x_head].unsqueeze(0))
+        nc.sync.dma_start(out=x_rows_flat[P - 1 : P, 0:x_head], in_=x_flat[1 : x_head + 1].unsqueeze(0))
+        load_block(2)
         load_x(1)
-        nc.sync.dma_start(out=x_rows_flat[P - 2 : P - 1, :], in_=x_flat.unsqueeze(0))
-        nc.sync.dma_start(out=x_rows_flat[P - 1 : P, 0 : BATCH * N_X - 1], in_=x_flat[1 : BATCH * N_X].unsqueeze(0))
-        for bb in range(2, NBLK):
+        for bb in range(3, NBLK):
             load_block(bb)
-            load_x(bb)
+            load_x(bb - 1)
+        load_x(NBLK - 1)
 
         operands = {}
         turned_inputs = {}
 
-        def turn_inputs(t, pool, hw_tag, cat_tag):
-            words = h_sb[:, t, :].bitcast(F32)
-            hw_ps = pool.tile([P, 2, P], F32, tag=hw_tag)
+        def turn_inputs(t, pool_tag, bufs):
+            in_ps = psum.tile([P, 3, P], F32, name="in_ps", tag=pool_tag, bufs=bufs)
+            h_words = h_sb[:, t, :].bitcast(F32)
             for u in range(2):
-                nc.tensor.transpose(out=hw_ps[:, u, :], in_=words[:, u : HID // 2 : 2], identity=ident_f32[:])
-            cat_ps = pool.tile([P, 2, P], BF16, tag=cat_tag)
-            for stream in range(2):
-                nc.tensor.transpose(out=cat_ps[:, stream, :], in_=fa_sb[:, t, stream, :], identity=ident_bf[:])
-            turned_inputs[t] = (hw_ps, cat_ps)
+                nc.tensor.transpose(out=in_ps[:, u, :], in_=h_words[:, u : HID // 2 : 2], identity=ident_f32[:])
+            cat_words = fa_sb[:, t, :, :].rearrange("p s k -> p (s k)").bitcast(F32)
+            nc.tensor.transpose(out=in_ps[:, 2, :], in_=cat_words, identity=ident_f32[:])
+            turned_inputs[t] = in_ps
 
         def keep_inputs(t, copy_words):
             bb, s = divmod(t, SUB)
@@ -122,11 +125,14 @@ def tile_wavernncell_pa_t_kernel(tc, x, feat, aux1, h, w_ih, w_hh_words, w_hh_sc
                 grouped = operand.tile([P, SUB, P * PACK], BF16, align_bytes=64)
                 operands[bb] = (h_codes, h_scales, catT, grouped)
             catT, grouped = operands[bb][2], operands[bb][3]
-            hw_ps, cat_ps = turned_inputs[t]
+            in_ps = turned_inputs[t]
             copy_words(
-                out=grouped[:, s, :].bitcast(F32).rearrange("p (b u) -> p b u", u=2), in_=hw_ps[:].rearrange("p u b -> p b u")
+                out=grouped[:, s, :].bitcast(F32).rearrange("p (b u) -> p b u", u=2),
+                in_=in_ps[:, 0:2, :].rearrange("p u b -> p b u"),
             )
-            nc.scalar.copy(out=catT[:, :, s * P : (s + 1) * P], in_=cat_ps[:])
+            nc.scalar.copy(
+                out=catT[:, :, s * P : (s + 1) * P], in_=in_ps[:, 2, :].bitcast(BF16).rearrange("p (b e) -> p e b", e=2)
+            )
 
         def quantise(bb):
             h_codes, h_scales, grouped = operands[bb][0], operands[bb][1], operands[bb][3]
@@ -138,35 +144,45 @@ def tile_wavernncell_pa_t_kernel(tc, x, feat, aux1, h, w_ih, w_hh_words, w_hh_sc
         wx = const.tile([P, COL_TILES, N_X], F32)
         wxT = const.tile([P, HID], BF16)
 
-        def turn_weights(gate, first_column, pool, tag):
-            wt_ps = pool.tile([P, HID], BF16, tag=tag)
+        def turn_weights(gate, columns, wt_ps):
             for jt in range(JT):
                 nc.tensor.transpose(
-                    out=wt_ps[:, jt * P : (jt + 1) * P],
-                    in_=w_sb[:, gate * JT + jt, first_column : first_column + P],
-                    identity=ident_bf[:],
+                    out=wt_ps[:, jt * P : (jt + 1) * P], in_=w_sb[:, gate * JT + jt, columns], identity=ident_bf[:]
                 )
-            return wt_ps
-
-        with tc.psum_pool(name="psum_setup", bufs=2) as psum_setup:
-            for s in range(2):
-                wt_ps = turn_weights(R_GATE, s * STREAM, psum_setup, "turned")
-                nc.scalar.copy(out=wT[:, s, 0:HID], in_=wt_ps[:])
-            nc.vector.tensor_copy(out=wx[:, 0:JT, :], in_=w_sb[:, 0:JT, 2 * STREAM : IN])
-            for t in range(SUB):
-                turn_inputs(t, psum_setup, "hw_ps", "cat_ps")
-                keep_inputs(t, nc.vector.tensor_copy)
-            quantise(0)
-            bias_ps = psum_setup.tile([P, P], BF16, tag="turned")
-            nc.tensor.transpose(out=bias_ps[:], in_=bias_rows[:], identity=ident_bf[:])
-            bias = const.tile([P, 2 * COL_TILES], F32)
-            nc.vector.tensor_copy(out=bias[:], in_=bias_ps[:, 0 : 2 * COL_TILES])
-            bias_rz = const.tile([P, 2 * JT], F32)
-            nc.vector.tensor_tensor(
-                out=bias_rz[:], in0=bias[:, 0 : 2 * JT], in1=bias[:, COL_TILES : COL_TILES + 2 * JT], op=ALU.add
-            )
 
         psum = ctx.enter_context(tc.psum_pool(name="psum", bufs=1))
+
+        for e in range(2):
+            wt_ps = psum.tile([P, HID], BF16, name="wt_ps", tag="z_bank", bufs=2)
+            turn_weights(R_GATE, slice(e, 2 * STREAM, 2), wt_ps)
+            nc.scalar.copy(out=wT[:, e, 0:HID], in_=wt_ps[:])
+        nc.vector.tensor_copy(out=wx[:, 0:JT, :], in_=w_sb[:, 0:JT, 2 * STREAM : IN])
+        x_ps = psum.tile([P, N_X, NB], BF16, name="x_ps", tag="n_bank")
+        for c in range(N_X):
+            for s in range(SUB):
+                nc.tensor.transpose(
+                    out=x_ps[:, c, s * P : (s + 1) * P],
+                    in_=x_cols[:, s, c : c + 1].to_broadcast([P, P]),
+                    identity=ident_bf[:],
+                )
+        nc.scalar.copy(out=x_bc[:, 0, :, :], in_=x_ps[:].rearrange("p c b -> p b c"))
+        for t in range(SUB):
+            if t == 0:
+                turn_inputs(t, "in_ps", 1)
+            else:
+                turn_inputs(t, "gh", 3)
+            keep_inputs(t, nc.scalar.copy if t == 3 else nc.vector.tensor_copy)
+        quantise(0)
+        bias = const.tile([P, 2 * COL_TILES], F32)
+        bias_rz = const.tile([P, 2 * JT], F32)
+
+        def turn_biases():
+            bias_ps = psum.tile([P, P], BF16, name="bias_ps", tag="n_bank")
+            nc.tensor.transpose(out=bias_ps[:], in_=bias_rows[:], identity=ident_bf[:])
+            nc.vector.tensor_copy(out=bias[:], in_=bias_ps[:, 0 : 2 * COL_TILES])
+            nc.vector.tensor_tensor(
+                out=bias_rz[:], in0=bias_ps[:, 0 : 2 * JT], in1=bias[:, COL_TILES : COL_TILES + 2 * JT], op=ALU.add
+            )
 
         r_plain, r_hidden_ps, r_halves, r_args, r_gate = {}, {}, {}, {}, {}
         reset_hidden, z_hidden, z_input = {}, {}, {}
@@ -238,8 +254,13 @@ def tile_wavernncell_pa_t_kernel(tc, x, feat, aux1, h, w_ih, w_hh_words, w_hh_sc
 
         with tc.manual_schedule():
             for i in range(UNITS + 9):
-                turning = (2 * i + SUB, 2 * i + SUB + 1) if i < 2 else (i + 6,) if i + 6 < TILES else ()
+                turning = () if i == 0 else (2 * i + 2, 2 * i + 3) if i < 4 else (i + 6,) if i + 6 < TILES else ()
                 late_weights = {2: Z_GATE, 3: N_GATE}.get(i)
+                if i == 4:
+                    nc.vector.tensor_copy(
+                        out=w_sb[:, N_GATE * JT : COL_TILES, IN - P + ONES_ROW : IN - P + ONES_ROW + 1],
+                        in_=bias[:, N_GATE * JT : COL_TILES].unsqueeze(2),
+                    )
                 if 0 <= i < UNITS:
                     r_plain[i] = r_input_product(i)
                     r_hidden_ps[i] = hidden_product(i, R_GATE)
@@ -248,7 +269,8 @@ def tile_wavernncell_pa_t_kernel(tc, x, feat, aux1, h, w_ih, w_hh_words, w_hh_sc
                         with_x(i, R_GATE, 1, r_hidden_ps[i], "r_half1"),
                     )
                 if i == 0:
-                    nc.vector.tensor_copy(out=wx[:, JT:COL_TILES, :], in_=w_sb[:, JT:COL_TILES, 2 * STREAM : IN])
+                    turn_biases()
+                    nc.scalar.copy(out=wx[:, JT:COL_TILES, :], in_=w_sb[:, JT:COL_TILES, 2 * STREAM : IN])
                 if 0 <= i - 7 < TILES:
                     v = i - 7
                     h_minus_n[v] = work.tile([P, HID], F32, name="h_minus_n", tag="h_minus_n", bufs=3)
@@ -257,6 +279,8 @@ def tile_wavernncell_pa_t_kernel(tc, x, feat, aux1, h, w_ih, w_hh_words, w_hh_sc
                 if 0 <= i < UNITS:
                     r_args[i] = work.tile([P, NB], F32, name="r_arg", tag="r_arg")
                     nc.gpsimd.tensor_tensor(out=r_args[i][:], in0=r_halves[i][0][:], in1=r_halves[i][1][:], op=ALU.add)
+                if i == 3:
+                    quantise(1)
                 if 0 <= i - 1 < UNITS:
                     u = i - 1
                     gh_n = hidden_product(u, N_GATE)
@@ -277,31 +301,30 @@ def tile_wavernncell_pa_t_kernel(tc, x, feat, aux1, h, w_ih, w_hh_words, w_hh_sc
                 z_tiles = [v for v in (i - 4,) if 0 <= v < TILES - 1] + ([TILES - 1] if i == TILES + 4 else [])
                 n_tiles = [v for v in (i - 5,) if 0 <= v < TILES - 1] + ([TILES - 1] if i == TILES + 3 else [])
                 for v in z_tiles:
-                    if mx_done and v % 2 == 1:
-                        z_bank[v] = straight_products(v, Z_GATE, "gh", 3)
-                    else:
-                        z_bank[v] = straight_products(v, Z_GATE, "z_bank", 1)
+                    z_bank[v] = straight_products(v, Z_GATE, "z_bank", 2)
                 for v in n_tiles:
-                    if mx_done and v % 2 == 1:
-                        n_bank[v] = straight_products(v, N_GATE, "gh", 3)
+                    if i > TILES - 6 and v % 2 == 1:
+                        n_bank[v] = straight_products(v, N_GATE, "in_ps", 1)
                     else:
                         n_bank[v] = straight_products(v, N_GATE, "n_bank", 1)
                 if i == 4:
-                    nc.vector.tensor_copy(
-                        out=w_sb[:, N_GATE * JT : COL_TILES, IN - P + ONES_ROW : IN - P + ONES_ROW + 1],
-                        in_=bias[:, N_GATE * JT : COL_TILES].unsqueeze(2),
-                    )
-                    wx_ps = turn_weights(N_GATE, IN - P, psum, "n_bank")
+                    wx_ps = psum.tile([P, HID], BF16, name="wx_ps", tag="n_bank")
+                    turn_weights(N_GATE, slice(IN - P, IN), wx_ps)
                 for v in z_tiles:
                     add_turned(v, z_bank[v], (z_hidden, z_input))
                 for v in n_tiles:
                     add_turned(v, n_bank[v], (reset_hidden,))
                 if late_weights is not None:
-                    late_feat = turn_weights(late_weights, 0, psum, "z_bank")
-                    late_aux = turn_weights(late_weights, STREAM, psum, "n_bank")
-                    nc.vector.tensor_copy(out=wT[:, 1, late_weights * HID : (late_weights + 1) * HID], in_=late_aux[:])
+                    late_even = psum.tile([P, HID], BF16, name="late_even", tag="z_bank", bufs=2)
+                    turn_weights(late_weights, slice(0, 2 * STREAM, 2), late_even)
+                    late_odd = psum.tile([P, HID], BF16, name="late_odd", tag="n_bank")
+                    turn_weights(late_weights, slice(1, 2 * STREAM, 2), late_odd)
+                    nc.vector.tensor_copy(out=wT[:, 1, late_weights * HID : (late_weights + 1) * HID], in_=late_odd[:])
                 for k, t in enumerate(turning):
-                    turn_inputs(t, psum, "hw_ps" if k == 0 else "z_bank", "cat_ps" if k == 0 else "n_bank")
+                    if k == 0:
+                        turn_inputs(t, "in_ps", 1)
+                    else:
+                        turn_inputs(t, "z_bank", 2)
                 if 0 <= i - 8 < TILES:
                     v = i - 8
                     res = work.tile([P, HID], F32, tag="res", bufs=4)
@@ -311,8 +334,17 @@ def tile_wavernncell_pa_t_kernel(tc, x, feat, aux1, h, w_ih, w_hh_words, w_hh_sc
                     v = i - 7
                     z_diff[v] = work.tile([P, HID], F32, name="z_diff", tag="z_diff")
                     nc.vector.tensor_tensor(out=z_diff[v][:], in0=z_gate[v][:], in1=h_minus_n[v][:], op=ALU.mult)
-                if SUB <= i + 5 < TILES and (i + 5) % SUB == SUB - 1:
-                    quantise((i + 5) // SUB)
+                if i > 3 and i % SUB == 2 and i + 2 < UNITS:
+                    quantise((i + 2) // SUB)
+                if i < 4:
+                    for t in turning:
+                        keep_inputs(t, nc.scalar.copy)
+                if 4 <= i < 7:
+                    part = slice((i - 3) * x_head, (i - 2) * x_head)
+                    nc.vector.tensor_copy(out=x_rows_flat[:, part], in_=ident_bf[:, ONES_ROW : ONES_ROW + 1].to_broadcast([P, x_head]))
+                    nc.sync.dma_start(out=x_rows_flat[P - 2 : P - 1, part], in_=x_flat[part].unsqueeze(0))
+                    last = min((i - 2) * x_head, BATCH * N_X - 1)
+                    nc.sync.dma_start(out=x_rows_flat[P - 1 : P, (i - 3) * x_head : last], in_=x_flat[(i - 3) * x_head + 1 : last + 1].unsqueeze(0))
                 if 0 <= i < UNITS:
                     c = R_GATE * JT + i % JT
                     r_gate[i] = work.tile([P, NB], F32, name="r_gate", tag="r_gate", bufs=3)
@@ -326,11 +358,12 @@ def tile_wavernncell_pa_t_kernel(tc, x, feat, aux1, h, w_ih, w_hh_words, w_hh_sc
                     n_gate[v] = work.tile([P, HID], F32, name="n_gate", tag="n_gate", bufs=5)
                     nc.scalar.activation(out=n_gate[v][:], in_=n_bank[v][:], func=ACT.Tanh)
                 if late_weights is not None:
-                    nc.scalar.copy(out=wT[:, 0, late_weights * HID : (late_weights + 1) * HID], in_=late_feat[:])
+                    nc.scalar.copy(out=wT[:, 0, late_weights * HID : (late_weights + 1) * HID], in_=late_even[:])
                 if i == 4:
                     nc.scalar.copy(out=wxT[:], in_=wx_ps[:])
-                for t in turning:
-                    keep_inputs(t, nc.scalar.copy)
+                if i >= 4:
+                    for t in turning:
+                        keep_inputs(t, nc.scalar.copy)
                 if 0 <= i < UNITS:
                     c = Z_GATE * JT + i % JT
                     z_input[i] = work.tile([P, NB], F32, name="z_input", tag="z_input", bufs=8)

@@ -53,6 +53,8 @@ def tile_wavernncell_pa_t_kernel(tc, x, feat, aux1, h, w_ih, w_hh_words, w_hh_sc
         nc.vector.memset(w4_scales[:].bitcast(I32), 0)
         bias_rows = const.tile([P, P], BF16)
         nc.vector.memset(bias_rows[:].bitcast(I32), 0)
+        x_block0 = const.tile([P, P, N_X], BF16)
+        nc.vector.memset(x_block0[:].rearrange("p j c -> p (j c)").bitcast(I32), 0)
         x_rows = const.tile([P, BATCH, N_X], BF16)
         x_rows_flat = x_rows[:].rearrange("p b c -> p (b c)")
         x_head = 2 * NB * N_X
@@ -62,7 +64,8 @@ def tile_wavernncell_pa_t_kernel(tc, x, feat, aux1, h, w_ih, w_hh_words, w_hh_sc
         h_sb = const.tile([P, TILES, HID], BF16)
         fa_sb = const.tile([P, TILES, 2, STREAM], BF16)
         x_bc = const.tile([P, NBLK, NB, N_X], BF16)
-        x_cols = const.tile([P, SUB, N_X], BF16)
+        x_bc0 = const.tile([P, N_X, NB], BF16)
+        x_cols = const.tile([P, N_X, SUB], BF16)
         w4_words = const.tile([P, 2 * GATES * HID], U8, align_bytes=64)
         h_view = h.rearrange("(t p) k -> p t k", p=P)
         feat_view = feat.rearrange("(t p) k -> p t k", p=P)
@@ -82,8 +85,16 @@ def tile_wavernncell_pa_t_kernel(tc, x, feat, aux1, h, w_ih, w_hh_words, w_hh_sc
             )
 
         w_view = w_ih.rearrange("(c p) k -> p c k", p=P)
-        nc.sync.dma_start(out=w_sb[:, 0:JT, :], in_=w_view[:, 0:JT, :])
-        nc.sync.dma_start(out=x_cols[:], in_=x[0:NB, :].rearrange("(s p) c -> p s c", p=P))
+
+        def load_weights(gate):
+            rows = slice(gate * JT, (gate + 1) * JT)
+            nc.sync.dma_start(out=w_sb[:, rows, :], in_=w_view[:, rows, :])
+
+        load_weights(R_GATE)
+        nc.sync.dma_start(
+            out=x_block0[0:SUB, :, :].rearrange("s j c -> s (j c)"),
+            in_=x[0:NB, :].rearrange("(s j) c -> s (j c)", s=SUB),
+        )
         load_block(0)
         nc.sync.dma_start(out=w4_words[:].bitcast(I32), in_=w_hh_words[0].bitcast(I32))
         for quad in range(4):
@@ -91,18 +102,19 @@ def tile_wavernncell_pa_t_kernel(tc, x, feat, aux1, h, w_ih, w_hh_words, w_hh_sc
                 out=w4_scales[32 * quad : 32 * quad + 4, :].bitcast(I32),
                 in_=w_hh_scales[0, 4 * quad : 4 * quad + 4, :].bitcast(I32),
             )
-        nc.sync.dma_start(out=bias_rows[0:COL_TILES, :], in_=b_ih.rearrange("(c p) -> c p", p=P))
-        nc.sync.dma_start(out=bias_rows[COL_TILES : 2 * COL_TILES, :], in_=b_hh.rearrange("(c p) -> c p", p=P))
-        nc.sync.dma_start(out=w_sb[:, JT:COL_TILES, :], in_=w_view[:, JT:COL_TILES, :])
+        load_weights(Z_GATE)
         load_block(1)
-        nc.sync.dma_start(out=x_rows_flat[P - 2 : P - 1, 0:x_head], in_=x_flat[0:x_head].unsqueeze(0))
-        nc.sync.dma_start(out=x_rows_flat[P - 1 : P, 0:x_head], in_=x_flat[1 : x_head + 1].unsqueeze(0))
+        load_weights(N_GATE)
         load_block(2)
         load_x(1)
         for bb in range(3, NBLK):
             load_block(bb)
             load_x(bb - 1)
         load_x(NBLK - 1)
+        nc.gpsimd.dma_start(out=bias_rows[0:COL_TILES, :], in_=b_ih.rearrange("(c p) -> c p", p=P))
+        nc.gpsimd.dma_start(out=bias_rows[COL_TILES : 2 * COL_TILES, :], in_=b_hh.rearrange("(c p) -> c p", p=P))
+        nc.gpsimd.dma_start(out=x_rows_flat[P - 2 : P - 1, 0:x_head], in_=x_flat[0:x_head].unsqueeze(0))
+        nc.gpsimd.dma_start(out=x_rows_flat[P - 1 : P, 0:x_head], in_=x_flat[1 : x_head + 1].unsqueeze(0))
 
         operands = {}
         turned_inputs = {}
@@ -157,15 +169,23 @@ def tile_wavernncell_pa_t_kernel(tc, x, feat, aux1, h, w_ih, w_hh_words, w_hh_sc
             turn_weights(R_GATE, slice(e, 2 * STREAM, 2), wt_ps)
             nc.scalar.copy(out=wT[:, e, 0:HID], in_=wt_ps[:])
         nc.vector.tensor_copy(out=wx[:, 0:JT, :], in_=w_sb[:, 0:JT, 2 * STREAM : IN])
+        cols_ps = psum.tile([P, N_X, P], BF16, name="cols_ps", tag="in_ps")
+        for c in range(N_X):
+            nc.tensor.transpose(out=cols_ps[:, c, :], in_=x_block0[:, :, c], identity=ident_bf[:])
+        nc.vector.tensor_copy(out=x_cols[:], in_=cols_ps[:, :, 0:SUB])
         x_ps = psum.tile([P, N_X, NB], BF16, name="x_ps", tag="n_bank")
         for c in range(N_X):
             for s in range(SUB):
                 nc.tensor.transpose(
                     out=x_ps[:, c, s * P : (s + 1) * P],
-                    in_=x_cols[:, s, c : c + 1].to_broadcast([P, P]),
+                    in_=x_cols[:, c, s : s + 1].to_broadcast([P, P]),
                     identity=ident_bf[:],
                 )
-        nc.scalar.copy(out=x_bc[:, 0, :, :], in_=x_ps[:].rearrange("p c b -> p b c"))
+        nc.scalar.copy(out=x_bc0[:], in_=x_ps[:])
+
+        def x_column(bb, c):
+            return x_bc0[:, c, :] if bb == 0 else x_bc[:, bb, :, c]
+
         for t in range(SUB):
             if t == 0:
                 turn_inputs(t, "in_ps", 1)
@@ -218,7 +238,7 @@ def tile_wavernncell_pa_t_kernel(tc, x, feat, aux1, h, w_ih, w_hh_words, w_hh_sc
             total = work.tile([P, NB], F32, tag=tag, bufs=(8 if tag == "z_hidden" else 2))
             nc.vector.scalar_tensor_tensor(
                 out=total[:],
-                in0=x_bc[:, bb, :, column],
+                in0=x_column(bb, column),
                 scalar=wx[:, gate * JT + jt, column : column + 1],
                 in1=product[:],
                 op0=ALU.mult,
@@ -270,7 +290,7 @@ def tile_wavernncell_pa_t_kernel(tc, x, feat, aux1, h, w_ih, w_hh_words, w_hh_sc
                     )
                 if i == 0:
                     turn_biases()
-                    nc.scalar.copy(out=wx[:, JT:COL_TILES, :], in_=w_sb[:, JT:COL_TILES, 2 * STREAM : IN])
+                    nc.scalar.copy(out=wx[:, JT : 2 * JT, :], in_=w_sb[:, JT : 2 * JT, 2 * STREAM : IN])
                 if 0 <= i - 7 < TILES:
                     v = i - 7
                     h_minus_n[v] = work.tile([P, HID], F32, name="h_minus_n", tag="h_minus_n", bufs=3)
@@ -369,7 +389,7 @@ def tile_wavernncell_pa_t_kernel(tc, x, feat, aux1, h, w_ih, w_hh_words, w_hh_sc
                     z_input[i] = work.tile([P, NB], F32, name="z_input", tag="z_input", bufs=8)
                     nc.scalar.activation(
                         out=z_input[i][:],
-                        in_=x_bc[:, i // JT, :, 0],
+                        in_=x_column(i // JT, 0),
                         func=ACT.Identity,
                         bias=bias_rz[:, c : c + 1],
                         scale=wx[:, c, 0:1],

@@ -29,6 +29,7 @@ SUB = NB // P
 NBLK = BATCH // NB
 TILES = BATCH // P
 UNITS = NBLK * JT
+X_SETS = 3
 ONES_ROW = P - 3
 
 FLOPS = 2 * BATCH * GATES * HID * (HID + IN)
@@ -40,6 +41,7 @@ def tile_wavernncell_pa_t_kernel(tc, x, feat, aux1, h, w_ih, w_hh_words, w_hh_sc
         const = ctx.enter_context(tc.tile_pool(name="const", bufs=1))
         operand = ctx.enter_context(tc.tile_pool(name="operand", bufs=3))
         work = ctx.enter_context(tc.tile_pool(name="work", bufs=2))
+        ctx.enter_context(tc.manual_schedule())
 
         ident_bf = const.tile([P, P], BF16)
         make_identity(nc, ident_bf[:])
@@ -51,16 +53,17 @@ def tile_wavernncell_pa_t_kernel(tc, x, feat, aux1, h, w_ih, w_hh_words, w_hh_sc
 
         w4_scales = const.tile([P, GATES * HID], U8, align_bytes=64)
         nc.vector.memset(w4_scales[:].bitcast(I32), 0)
-        bias_rows = const.tile([P, P], BF16)
-        nc.vector.memset(bias_rows[:].bitcast(I32), 0)
         x_block0 = const.tile([P, P, N_X], BF16)
         nc.vector.memset(x_block0[:].rearrange("p j c -> p (j c)").bitcast(I32), 0)
-        x_rows = const.tile([P, BATCH, N_X], BF16)
-        x_rows_flat = x_rows[:].rearrange("p b c -> p (b c)")
-        x_head = 2 * NB * N_X
-        nc.vector.tensor_copy(out=x_rows_flat[:, 0:x_head], in_=ident_bf[:, ONES_ROW : ONES_ROW + 1].to_broadcast([P, x_head]))
+        bias_rows = const.tile([P, P], BF16)
+        nc.vector.memset(bias_rows[:].bitcast(I32), 0)
+        x_rows = [const.tile([P, NB, N_X], BF16, name="x_rows_%d" % k) for k in range(X_SETS)]
+        for rows in x_rows:
+            nc.vector.tensor_copy(
+                out=rows[:].rearrange("p b c -> p (b c)"), in_=ident_bf[:, ONES_ROW : ONES_ROW + 1].to_broadcast([P, NB * N_X])
+            )
 
-        w_sb = const.tile([P, COL_TILES, IN], BF16)
+        w_sb = [const.tile([P, JT, IN], BF16, name="w_sb_%d" % gate) for gate in range(GATES)]
         h_sb = const.tile([P, TILES, HID], BF16)
         fa_sb = const.tile([P, TILES, 2, STREAM], BF16)
         x_bc = const.tile([P, NBLK, NB, N_X], BF16)
@@ -72,11 +75,14 @@ def tile_wavernncell_pa_t_kernel(tc, x, feat, aux1, h, w_ih, w_hh_words, w_hh_sc
         aux_view = aux1.rearrange("(t p) k -> p t k", p=P)
         x_flat = x.rearrange("b c -> (b c)")
 
-        def load_block(bb):
+        def load_h(bb):
+            tiles = slice(bb * SUB, (bb + 1) * SUB)
+            nc.sync.dma_start(out=h_sb[:, tiles, :], in_=h_view[:, tiles, :])
+
+        def load_streams(bb):
             tiles = slice(bb * SUB, (bb + 1) * SUB)
             nc.sync.dma_start(out=fa_sb[:, tiles, 0, :], in_=feat_view[:, tiles, :])
             nc.sync.dma_start(out=fa_sb[:, tiles, 1, :], in_=aux_view[:, tiles, :])
-            nc.sync.dma_start(out=h_sb[:, tiles, :], in_=h_view[:, tiles, :])
 
         def load_x(bb):
             nc.sync.dma_start(
@@ -84,37 +90,52 @@ def tile_wavernncell_pa_t_kernel(tc, x, feat, aux1, h, w_ih, w_hh_words, w_hh_sc
                 in_=x_flat[bb * NB * N_X : (bb + 1) * NB * N_X].partition_broadcast(P),
             )
 
+        def load_x_rows(bb):
+            rows = x_rows[bb % X_SETS][:].rearrange("p b c -> p (b c)")
+            first, count = bb * NB * N_X, NB * N_X
+            nc.sync.dma_start(out=rows[P - 2 : P - 1, :], in_=x_flat[first : first + count].unsqueeze(0))
+            nc.sync.dma_start(out=rows[P - 1 : P, 0 : count - 1], in_=x_flat[first + 1 : first + count].unsqueeze(0))
+
         w_view = w_ih.rearrange("(c p) k -> p c k", p=P)
 
         def load_weights(gate):
             rows = slice(gate * JT, (gate + 1) * JT)
-            nc.sync.dma_start(out=w_sb[:, rows, :], in_=w_view[:, rows, :])
+            nc.sync.dma_start(out=w_sb[gate][:], in_=w_view[:, rows, :])
 
-        load_weights(R_GATE)
-        nc.sync.dma_start(
+        def load_biases(vector, row):
+            rows = vector.rearrange("(c p) -> c p", p=P)
+            for first, last in ((0, 8), (8, COL_TILES)):
+                nc.sync.dma_start(out=bias_rows[row + first : row + last, :], in_=rows[first:last, :])
+
+        nc.gpsimd.dma_start(
             out=x_block0[0:SUB, :, :].rearrange("s j c -> s (j c)"),
             in_=x[0:NB, :].rearrange("(s j) c -> s (j c)", s=SUB),
         )
-        load_block(0)
-        nc.sync.dma_start(out=w4_words[:].bitcast(I32), in_=w_hh_words[0].bitcast(I32))
+        load_h(0)
         for quad in range(4):
             nc.sync.dma_start(
                 out=w4_scales[32 * quad : 32 * quad + 4, :].bitcast(I32),
                 in_=w_hh_scales[0, 4 * quad : 4 * quad + 4, :].bitcast(I32),
             )
+        load_weights(R_GATE)
+        load_streams(0)
+        nc.sync.dma_start(out=w4_words[:].bitcast(I32), in_=w_hh_words[0].bitcast(I32))
         load_weights(Z_GATE)
-        load_block(1)
+        load_biases(b_ih, 0)
+        load_biases(b_hh, COL_TILES)
+        load_h(1)
+        load_streams(1)
         load_weights(N_GATE)
-        load_block(2)
+        load_h(2)
+        load_streams(2)
+        for bb in range(X_SETS):
+            load_x_rows(bb)
         load_x(1)
         for bb in range(3, NBLK):
-            load_block(bb)
+            load_h(bb)
+            load_streams(bb)
             load_x(bb - 1)
         load_x(NBLK - 1)
-        nc.gpsimd.dma_start(out=bias_rows[0:COL_TILES, :], in_=b_ih.rearrange("(c p) -> c p", p=P))
-        nc.gpsimd.dma_start(out=bias_rows[COL_TILES : 2 * COL_TILES, :], in_=b_hh.rearrange("(c p) -> c p", p=P))
-        nc.gpsimd.dma_start(out=x_rows_flat[P - 2 : P - 1, 0:x_head], in_=x_flat[0:x_head].unsqueeze(0))
-        nc.gpsimd.dma_start(out=x_rows_flat[P - 1 : P, 0:x_head], in_=x_flat[1 : x_head + 1].unsqueeze(0))
 
         operands = {}
         turned_inputs = {}
@@ -128,17 +149,20 @@ def tile_wavernncell_pa_t_kernel(tc, x, feat, aux1, h, w_ih, w_hh_words, w_hh_sc
             nc.tensor.transpose(out=in_ps[:, 2, :], in_=cat_words, identity=ident_f32[:])
             turned_inputs[t] = in_ps
 
-        def keep_inputs(t, copy_words):
+        def new_operands(bb):
+            h_codes = operand.tile([P, NB], U32, align_bytes=64)
+            h_scales = operand.tile([P, NB], U8, align_bytes=64)
+            catT = operand.tile([P, 2, NB], BF16, bufs=4)
+            grouped = operand.tile([P, SUB, P * PACK], BF16, align_bytes=64)
+            operands[bb] = (h_codes, h_scales, catT, grouped)
+
+        def keep_inputs(t):
             bb, s = divmod(t, SUB)
             if s == 0:
-                h_codes = operand.tile([P, NB], U32, align_bytes=64)
-                h_scales = operand.tile([P, NB], U8, align_bytes=64)
-                catT = operand.tile([P, 2, NB], BF16, bufs=4)
-                grouped = operand.tile([P, SUB, P * PACK], BF16, align_bytes=64)
-                operands[bb] = (h_codes, h_scales, catT, grouped)
+                new_operands(bb)
             catT, grouped = operands[bb][2], operands[bb][3]
             in_ps = turned_inputs[t]
-            copy_words(
+            nc.scalar.copy(
                 out=grouped[:, s, :].bitcast(F32).rearrange("p (b u) -> p b u", u=2),
                 in_=in_ps[:, 0:2, :].rearrange("p u b -> p b u"),
             )
@@ -159,20 +183,41 @@ def tile_wavernncell_pa_t_kernel(tc, x, feat, aux1, h, w_ih, w_hh_words, w_hh_sc
         def turn_weights(gate, columns, wt_ps):
             for jt in range(JT):
                 nc.tensor.transpose(
-                    out=wt_ps[:, jt * P : (jt + 1) * P], in_=w_sb[:, gate * JT + jt, columns], identity=ident_bf[:]
+                    out=wt_ps[:, jt * P : (jt + 1) * P], in_=w_sb[gate][:, jt, columns], identity=ident_bf[:]
                 )
 
         psum = ctx.enter_context(tc.psum_pool(name="psum", bufs=1))
 
-        for e in range(2):
-            wt_ps = psum.tile([P, HID], BF16, name="wt_ps", tag="z_bank", bufs=2)
-            turn_weights(R_GATE, slice(e, 2 * STREAM, 2), wt_ps)
-            nc.scalar.copy(out=wT[:, e, 0:HID], in_=wt_ps[:])
-        nc.vector.tensor_copy(out=wx[:, 0:JT, :], in_=w_sb[:, 0:JT, 2 * STREAM : IN])
+        new_operands(0)
+        catT, grouped = operands[0][2], operands[0][3]
+        for pair, copy in ((0, nc.vector.tensor_copy), (1, nc.scalar.copy)):
+            h_ps = psum.tile([P, 2, 2, P], F32, name="h_ps", tag="gh", bufs=3)
+            for s in range(2):
+                h_words = h_sb[:, 2 * pair + s, :].bitcast(F32)
+                for u in range(2):
+                    nc.tensor.transpose(out=h_ps[:, s, u, :], in_=h_words[:, u : HID // 2 : 2], identity=ident_f32[:])
+            copy(
+                out=grouped[:, 2 * pair : 2 * pair + 2, :].bitcast(F32).rearrange("p s (b u) -> p s b u", u=2),
+                in_=h_ps[:].rearrange("p s u b -> p s b u"),
+            )
         cols_ps = psum.tile([P, N_X, P], BF16, name="cols_ps", tag="in_ps")
         for c in range(N_X):
             nc.tensor.transpose(out=cols_ps[:, c, :], in_=x_block0[:, :, c], identity=ident_bf[:])
         nc.vector.tensor_copy(out=x_cols[:], in_=cols_ps[:, :, 0:SUB])
+        quantise(0)
+        for e in range(2):
+            half_ps = psum.tile([P, HID], BF16, name="half_ps", tag="z_bank", bufs=2)
+            turn_weights(R_GATE, slice(e, 2 * STREAM, 2), half_ps)
+            (nc.scalar.copy, nc.vector.tensor_copy)[e](out=wT[:, e, 0:HID], in_=half_ps[:])
+        nc.vector.tensor_copy(out=wx[:, 0:JT, :], in_=w_sb[R_GATE][:, :, 2 * STREAM : IN])
+        cat_ps = psum.tile([P, SUB, P], F32, name="cat_ps", tag="gi")
+        for s in range(SUB):
+            cat_words = fa_sb[:, s, :, :].rearrange("p s k -> p (s k)").bitcast(F32)
+            nc.tensor.transpose(out=cat_ps[:, s, :], in_=cat_words, identity=ident_f32[:])
+        cat_values = cat_ps[:].rearrange("p t b -> p (t b)").bitcast(BF16).rearrange("p (b e) -> p e b", e=2)
+        for e in range(2):
+            (nc.scalar.copy, nc.vector.tensor_copy)[e](out=catT[:, e, :], in_=cat_values[:, e, :])
+
         x_ps = psum.tile([P, N_X, NB], BF16, name="x_ps", tag="n_bank")
         for c in range(N_X):
             for s in range(SUB):
@@ -181,18 +226,11 @@ def tile_wavernncell_pa_t_kernel(tc, x, feat, aux1, h, w_ih, w_hh_words, w_hh_sc
                     in_=x_cols[:, c, s : s + 1].to_broadcast([P, P]),
                     identity=ident_bf[:],
                 )
-        nc.scalar.copy(out=x_bc0[:], in_=x_ps[:])
+        nc.vector.tensor_copy(out=x_bc0[:], in_=x_ps[:])
 
         def x_column(bb, c):
             return x_bc0[:, c, :] if bb == 0 else x_bc[:, bb, :, c]
 
-        for t in range(SUB):
-            if t == 0:
-                turn_inputs(t, "in_ps", 1)
-            else:
-                turn_inputs(t, "gh", 3)
-            keep_inputs(t, nc.scalar.copy if t == 3 else nc.vector.tensor_copy)
-        quantise(0)
         bias = const.tile([P, 2 * COL_TILES], F32)
         bias_rz = const.tile([P, 2 * JT], F32)
 
@@ -255,7 +293,7 @@ def tile_wavernncell_pa_t_kernel(tc, x, feat, aux1, h, w_ih, w_hh_words, w_hh_sc
             nc.tensor.matmul(out=bank[:], lhsT=catT[:, 0, rows], rhs=wT[:, 0, cols], start=True, stop=False)
             nc.tensor.matmul(out=bank[:], lhsT=catT[:, 1, rows], rhs=wT[:, 1, cols], start=False, stop=False)
             if gate == N_GATE:
-                nc.tensor.matmul(out=bank[:], lhsT=x_rows[:, v * P : (v + 1) * P, 0], rhs=wxT[:], start=False, stop=False)
+                nc.tensor.matmul(out=bank[:], lhsT=x_rows[bb % X_SETS][:, rows, 0], rhs=wxT[:], start=False, stop=False)
             return bank
 
         def add_turned(v, bank, sources):
@@ -272,125 +310,120 @@ def tile_wavernncell_pa_t_kernel(tc, x, feat, aux1, h, w_ih, w_hh_words, w_hh_sc
                         stop=(jt == JT - 1 and k == len(sources) - 1),
                     )
 
-        with tc.manual_schedule():
-            for i in range(UNITS + 9):
-                turning = () if i == 0 else (2 * i + 2, 2 * i + 3) if i < 4 else (i + 6,) if i + 6 < TILES else ()
-                late_weights = {2: Z_GATE, 3: N_GATE}.get(i)
-                if i == 4:
-                    nc.vector.tensor_copy(
-                        out=w_sb[:, N_GATE * JT : COL_TILES, IN - P + ONES_ROW : IN - P + ONES_ROW + 1],
-                        in_=bias[:, N_GATE * JT : COL_TILES].unsqueeze(2),
-                    )
-                if 0 <= i < UNITS:
-                    r_plain[i] = r_input_product(i)
-                    r_hidden_ps[i] = hidden_product(i, R_GATE)
-                    r_halves[i] = (
-                        with_x(i, R_GATE, 0, r_plain[i], "r_half0"),
-                        with_x(i, R_GATE, 1, r_hidden_ps[i], "r_half1"),
-                    )
-                if i == 0:
-                    turn_biases()
-                    nc.scalar.copy(out=wx[:, JT : 2 * JT, :], in_=w_sb[:, JT : 2 * JT, 2 * STREAM : IN])
-                if 0 <= i - 7 < TILES:
-                    v = i - 7
-                    h_minus_n[v] = work.tile([P, HID], F32, name="h_minus_n", tag="h_minus_n", bufs=3)
-                    subtractor = nc.vector if i > UNITS else nc.gpsimd
-                    subtractor.tensor_tensor(out=h_minus_n[v][:], in0=h_sb[:, v, :], in1=n_gate[v][:], op=ALU.subtract)
-                if 0 <= i < UNITS:
-                    r_args[i] = work.tile([P, NB], F32, name="r_arg", tag="r_arg")
-                    nc.gpsimd.tensor_tensor(out=r_args[i][:], in0=r_halves[i][0][:], in1=r_halves[i][1][:], op=ALU.add)
-                if i == 3:
-                    quantise(1)
-                if 0 <= i - 1 < UNITS:
-                    u = i - 1
-                    gh_n = hidden_product(u, N_GATE)
-                    c = N_GATE * JT + u % JT
-                    reset_hidden[u] = work.tile([P, NB], F32, name="reset_hidden", tag="reset_hidden", bufs=8)
-                    nc.vector.scalar_tensor_tensor(
-                        out=reset_hidden[u][:],
-                        in0=gh_n[:],
-                        scalar=bias[:, COL_TILES + c : COL_TILES + c + 1],
-                        in1=r_gate[u][:],
-                        op0=ALU.add,
-                        op1=ALU.mult,
-                    )
-                if 0 <= i < UNITS:
-                    gh_z = hidden_product(i, Z_GATE)
-                    z_hidden[i] = with_x(i, Z_GATE, 1, gh_z, "z_hidden")
-                mx_done = i > UNITS
-                z_tiles = [v for v in (i - 4,) if 0 <= v < TILES - 1] + ([TILES - 1] if i == TILES + 4 else [])
-                n_tiles = [v for v in (i - 5,) if 0 <= v < TILES - 1] + ([TILES - 1] if i == TILES + 3 else [])
-                for v in z_tiles:
-                    z_bank[v] = straight_products(v, Z_GATE, "z_bank", 2)
-                for v in n_tiles:
-                    if i > TILES - 6 and v % 2 == 1:
-                        n_bank[v] = straight_products(v, N_GATE, "in_ps", 1)
-                    else:
-                        n_bank[v] = straight_products(v, N_GATE, "n_bank", 1)
-                if i == 4:
-                    wx_ps = psum.tile([P, HID], BF16, name="wx_ps", tag="n_bank")
-                    turn_weights(N_GATE, slice(IN - P, IN), wx_ps)
-                for v in z_tiles:
-                    add_turned(v, z_bank[v], (z_hidden, z_input))
-                for v in n_tiles:
-                    add_turned(v, n_bank[v], (reset_hidden,))
-                if late_weights is not None:
-                    late_even = psum.tile([P, HID], BF16, name="late_even", tag="z_bank", bufs=2)
-                    turn_weights(late_weights, slice(0, 2 * STREAM, 2), late_even)
-                    late_odd = psum.tile([P, HID], BF16, name="late_odd", tag="n_bank")
-                    turn_weights(late_weights, slice(1, 2 * STREAM, 2), late_odd)
-                    nc.vector.tensor_copy(out=wT[:, 1, late_weights * HID : (late_weights + 1) * HID], in_=late_odd[:])
-                for k, t in enumerate(turning):
-                    if k == 0:
-                        turn_inputs(t, "in_ps", 1)
-                    else:
-                        turn_inputs(t, "z_bank", 2)
-                if 0 <= i - 8 < TILES:
-                    v = i - 8
-                    res = work.tile([P, HID], F32, tag="res", bufs=4)
-                    nc.vector.tensor_tensor(out=res[:], in0=n_gate[v][:], in1=z_diff[v][:], op=ALU.add)
-                    nc.sync.dma_start(out=out[v * P : (v + 1) * P, :], in_=res[:])
-                if 0 <= i - 7 < TILES:
-                    v = i - 7
-                    z_diff[v] = work.tile([P, HID], F32, name="z_diff", tag="z_diff")
-                    nc.vector.tensor_tensor(out=z_diff[v][:], in0=z_gate[v][:], in1=h_minus_n[v][:], op=ALU.mult)
-                if i > 3 and i % SUB == 2 and i + 2 < UNITS:
-                    quantise((i + 2) // SUB)
-                if i < 4:
-                    for t in turning:
-                        keep_inputs(t, nc.scalar.copy)
-                if 4 <= i < 7:
-                    part = slice((i - 3) * x_head, (i - 2) * x_head)
-                    nc.vector.tensor_copy(out=x_rows_flat[:, part], in_=ident_bf[:, ONES_ROW : ONES_ROW + 1].to_broadcast([P, x_head]))
-                    nc.sync.dma_start(out=x_rows_flat[P - 2 : P - 1, part], in_=x_flat[part].unsqueeze(0))
-                    last = min((i - 2) * x_head, BATCH * N_X - 1)
-                    nc.sync.dma_start(out=x_rows_flat[P - 1 : P, (i - 3) * x_head : last], in_=x_flat[(i - 3) * x_head + 1 : last + 1].unsqueeze(0))
-                if 0 <= i < UNITS:
-                    c = R_GATE * JT + i % JT
-                    r_gate[i] = work.tile([P, NB], F32, name="r_gate", tag="r_gate", bufs=3)
-                    nc.scalar.activation(
-                        out=r_gate[i][:], in_=r_args[i][:], func=ACT.Sigmoid, bias=bias_rz[:, c : c + 1], scale=1.0
-                    )
-                for v in z_tiles:
-                    z_gate[v] = work.tile([P, HID], F32, name="z_gate", tag="z_gate", bufs=5)
-                    nc.scalar.activation(out=z_gate[v][:], in_=z_bank[v][:], func=ACT.Sigmoid)
-                for v in n_tiles:
-                    n_gate[v] = work.tile([P, HID], F32, name="n_gate", tag="n_gate", bufs=5)
-                    nc.scalar.activation(out=n_gate[v][:], in_=n_bank[v][:], func=ACT.Tanh)
-                if late_weights is not None:
-                    nc.scalar.copy(out=wT[:, 0, late_weights * HID : (late_weights + 1) * HID], in_=late_even[:])
-                if i == 4:
-                    nc.scalar.copy(out=wxT[:], in_=wx_ps[:])
-                if i >= 4:
-                    for t in turning:
-                        keep_inputs(t, nc.scalar.copy)
-                if 0 <= i < UNITS:
-                    c = Z_GATE * JT + i % JT
-                    z_input[i] = work.tile([P, NB], F32, name="z_input", tag="z_input", bufs=8)
-                    nc.scalar.activation(
-                        out=z_input[i][:],
-                        in_=x_column(i // JT, 0),
-                        func=ACT.Identity,
-                        bias=bias_rz[:, c : c + 1],
-                        scale=wx[:, c, 0:1],
-                    )
+        for i in range(UNITS + 9):
+            turning = () if i == 0 else (2 * i + 2, 2 * i + 3) if i < 4 else (i + 6,) if i + 6 < TILES else ()
+            late_weights = {2: Z_GATE, 3: N_GATE}.get(i)
+            if i == 4:
+                nc.vector.tensor_copy(
+                    out=w_sb[N_GATE][:, :, IN - P + ONES_ROW : IN - P + ONES_ROW + 1],
+                    in_=bias[:, N_GATE * JT : COL_TILES].unsqueeze(2),
+                )
+            if 0 <= i < UNITS:
+                r_plain[i] = r_input_product(i)
+                r_hidden_ps[i] = hidden_product(i, R_GATE)
+                r_halves[i] = (
+                    with_x(i, R_GATE, 0, r_plain[i], "r_half0"),
+                    with_x(i, R_GATE, 1, r_hidden_ps[i], "r_half1"),
+                )
+            if i == 0:
+                turn_biases()
+                nc.scalar.copy(out=wx[:, JT : 2 * JT, :], in_=w_sb[Z_GATE][:, :, 2 * STREAM : IN])
+            if 0 <= i - 7 < TILES:
+                v = i - 7
+                h_minus_n[v] = work.tile([P, HID], F32, name="h_minus_n", tag="h_minus_n", bufs=3)
+                subtractor = nc.vector if i > UNITS else nc.gpsimd
+                subtractor.tensor_tensor(out=h_minus_n[v][:], in0=h_sb[:, v, :], in1=n_gate[v][:], op=ALU.subtract)
+            if 0 <= i < UNITS:
+                r_args[i] = work.tile([P, NB], F32, name="r_arg", tag="r_arg")
+                nc.gpsimd.tensor_tensor(out=r_args[i][:], in0=r_halves[i][0][:], in1=r_halves[i][1][:], op=ALU.add)
+            if i == 3:
+                quantise(1)
+            if 0 <= i - 1 < UNITS:
+                u = i - 1
+                gh_n = hidden_product(u, N_GATE)
+                c = N_GATE * JT + u % JT
+                reset_hidden[u] = work.tile([P, NB], F32, name="reset_hidden", tag="reset_hidden", bufs=8)
+                nc.vector.scalar_tensor_tensor(
+                    out=reset_hidden[u][:],
+                    in0=gh_n[:],
+                    scalar=bias[:, COL_TILES + c : COL_TILES + c + 1],
+                    in1=r_gate[u][:],
+                    op0=ALU.add,
+                    op1=ALU.mult,
+                )
+            if 0 <= i < UNITS:
+                gh_z = hidden_product(i, Z_GATE)
+                z_hidden[i] = with_x(i, Z_GATE, 1, gh_z, "z_hidden")
+            mx_done = i > UNITS
+            z_tiles = [v for v in (i - 4,) if 0 <= v < TILES - 1] + ([TILES - 1] if i == TILES + 4 else [])
+            n_tiles = [v for v in (i - 5,) if 0 <= v < TILES - 1] + ([TILES - 1] if i == TILES + 3 else [])
+            for v in z_tiles:
+                z_bank[v] = straight_products(v, Z_GATE, "z_bank", 2)
+            for v in n_tiles:
+                if i > TILES - 6 and v % 2 == 1:
+                    n_bank[v] = straight_products(v, N_GATE, "in_ps", 1)
+                else:
+                    n_bank[v] = straight_products(v, N_GATE, "n_bank", 1)
+            if i == 4:
+                wx_ps = psum.tile([P, HID], BF16, name="wx_ps", tag="n_bank")
+                turn_weights(N_GATE, slice(IN - P, IN), wx_ps)
+            for v in z_tiles:
+                add_turned(v, z_bank[v], (z_hidden, z_input))
+            for v in n_tiles:
+                add_turned(v, n_bank[v], (reset_hidden,))
+            if late_weights is not None:
+                late_even = psum.tile([P, HID], BF16, name="late_even", tag="z_bank", bufs=2)
+                turn_weights(late_weights, slice(0, 2 * STREAM, 2), late_even)
+                late_odd = psum.tile([P, HID], BF16, name="late_odd", tag="n_bank")
+                turn_weights(late_weights, slice(1, 2 * STREAM, 2), late_odd)
+                nc.vector.tensor_copy(out=wT[:, 1, late_weights * HID : (late_weights + 1) * HID], in_=late_odd[:])
+            for k, t in enumerate(turning):
+                if k == 0:
+                    turn_inputs(t, "in_ps", 1)
+                else:
+                    turn_inputs(t, "z_bank", 2)
+            if 0 <= i - 8 < TILES:
+                v = i - 8
+                res = work.tile([P, HID], F32, tag="res", bufs=4)
+                nc.vector.tensor_tensor(out=res[:], in0=n_gate[v][:], in1=z_diff[v][:], op=ALU.add)
+                nc.sync.dma_start(out=out[v * P : (v + 1) * P, :], in_=res[:])
+            if 0 <= i - 7 < TILES:
+                v = i - 7
+                z_diff[v] = work.tile([P, HID], F32, name="z_diff", tag="z_diff")
+                nc.vector.tensor_tensor(out=z_diff[v][:], in0=z_gate[v][:], in1=h_minus_n[v][:], op=ALU.mult)
+            if i > 3 and i % SUB == 2 and i + 2 < UNITS:
+                quantise((i + 2) // SUB)
+            if i < 4:
+                for t in turning:
+                    keep_inputs(t)
+            if i % SUB == 1 and X_SETS <= (i + 3) // SUB < NBLK:
+                load_x_rows((i + 3) // SUB)
+            if 0 <= i < UNITS:
+                c = R_GATE * JT + i % JT
+                r_gate[i] = work.tile([P, NB], F32, name="r_gate", tag="r_gate", bufs=3)
+                nc.scalar.activation(
+                    out=r_gate[i][:], in_=r_args[i][:], func=ACT.Sigmoid, bias=bias_rz[:, c : c + 1], scale=1.0
+                )
+            for v in z_tiles:
+                z_gate[v] = work.tile([P, HID], F32, name="z_gate", tag="z_gate", bufs=5)
+                nc.scalar.activation(out=z_gate[v][:], in_=z_bank[v][:], func=ACT.Sigmoid)
+            for v in n_tiles:
+                n_gate[v] = work.tile([P, HID], F32, name="n_gate", tag="n_gate", bufs=5)
+                nc.scalar.activation(out=n_gate[v][:], in_=n_bank[v][:], func=ACT.Tanh)
+            if late_weights is not None:
+                nc.scalar.copy(out=wT[:, 0, late_weights * HID : (late_weights + 1) * HID], in_=late_even[:])
+            if i == 4:
+                nc.scalar.copy(out=wxT[:], in_=wx_ps[:])
+            if i >= 4:
+                for t in turning:
+                    keep_inputs(t)
+            if 0 <= i < UNITS:
+                c = Z_GATE * JT + i % JT
+                z_input[i] = work.tile([P, NB], F32, name="z_input", tag="z_input", bufs=8)
+                nc.scalar.activation(
+                    out=z_input[i][:],
+                    in_=x_column(i // JT, 0),
+                    func=ACT.Identity,
+                    bias=bias_rz[:, c : c + 1],
+                    scale=wx[:, c, 0:1],
+                )

@@ -107,19 +107,19 @@ def tile_wavernncell_pa_t_kernel(tc, x, feat, aux1, h, w_ih, w_hh_words, w_hh_sc
             for first, last in ((0, 8), (8, COL_TILES)):
                 nc.sync.dma_start(out=bias_rows[row + first : row + last, :], in_=rows[first:last, :])
 
-        nc.gpsimd.dma_start(
+        load_h(0)
+        nc.sync.dma_start(
             out=x_block0[0:SUB, :, :].rearrange("s j c -> s (j c)"),
             in_=x[0:NB, :].rearrange("(s j) c -> s (j c)", s=SUB),
         )
-        load_h(0)
+        load_weights(R_GATE)
+        load_streams(0)
+        nc.sync.dma_start(out=w4_words[:].bitcast(I32), in_=w_hh_words[0].bitcast(I32))
         for quad in range(4):
             nc.sync.dma_start(
                 out=w4_scales[32 * quad : 32 * quad + 4, :].bitcast(I32),
                 in_=w_hh_scales[0, 4 * quad : 4 * quad + 4, :].bitcast(I32),
             )
-        load_weights(R_GATE)
-        load_streams(0)
-        nc.sync.dma_start(out=w4_words[:].bitcast(I32), in_=w_hh_words[0].bitcast(I32))
         load_weights(Z_GATE)
         load_biases(b_ih, 0)
         load_biases(b_hh, COL_TILES)
@@ -326,7 +326,6 @@ def tile_wavernncell_pa_t_kernel(tc, x, feat, aux1, h, w_ih, w_hh_words, w_hh_sc
                     with_x(i, R_GATE, 1, r_hidden_ps[i], "r_half1"),
                 )
             if i == 0:
-                turn_biases()
                 nc.scalar.copy(out=wx[:, JT : 2 * JT, :], in_=w_sb[Z_GATE][:, :, 2 * STREAM : IN])
             if 0 <= i - 7 < TILES:
                 v = i - 7
@@ -354,6 +353,8 @@ def tile_wavernncell_pa_t_kernel(tc, x, feat, aux1, h, w_ih, w_hh_words, w_hh_sc
             if 0 <= i < UNITS:
                 gh_z = hidden_product(i, Z_GATE)
                 z_hidden[i] = with_x(i, Z_GATE, 1, gh_z, "z_hidden")
+            if i == 0:
+                turn_biases()
             mx_done = i > UNITS
             z_tiles = [v for v in (i - 4,) if 0 <= v < TILES - 1] + ([TILES - 1] if i == TILES + 4 else [])
             n_tiles = [v for v in (i - 5,) if 0 <= v < TILES - 1] + ([TILES - 1] if i == TILES + 3 else [])

@@ -67,8 +67,7 @@ def tile_wavernncell_pa_t_kernel(tc, x, feat, aux1, h, w_ih, w_hh_words, w_hh_sc
         h_sb = const.tile([P, TILES, HID], BF16)
         fa_sb = const.tile([P, TILES, 2, STREAM], BF16)
         x_bc = const.tile([P, NBLK, NB, N_X], BF16)
-        x_bc0 = const.tile([P, N_X, NB], BF16)
-        x_cols = const.tile([P, N_X, SUB], BF16)
+        x_cols = const.tile([P, SUB], F32)
         w4_words = const.tile([P, 2 * GATES * HID], U8, align_bytes=64)
         h_view = h.rearrange("(t p) k -> p t k", p=P)
         feat_view = feat.rearrange("(t p) k -> p t k", p=P)
@@ -180,10 +179,22 @@ def tile_wavernncell_pa_t_kernel(tc, x, feat, aux1, h, w_ih, w_hh_words, w_hh_sc
         wx = const.tile([P, COL_TILES, N_X], F32)
         wxT = const.tile([P, HID], BF16)
 
-        def turn_weights(gate, columns, wt_ps):
-            for jt in range(JT):
-                nc.tensor.transpose(
-                    out=wt_ps[:, jt * P : (jt + 1) * P], in_=w_sb[gate][:, jt, columns], identity=ident_bf[:]
+        def turn_weights(gate, banks):
+            halves = []
+            for half, (tag, bufs) in enumerate(banks):
+                w_ps = psum.tile([P, JT // 2, P], F32, name="w_ps", tag=tag, bufs=bufs)
+                for q in range(JT // 2):
+                    words = w_sb[gate][:, half * (JT // 2) + q, :].bitcast(F32)
+                    nc.tensor.transpose(out=w_ps[:, q, :], in_=words[:, 0:P], identity=ident_f32[:])
+                halves.append(w_ps)
+            return halves
+
+        def keep_weights(gate, halves, copies):
+            for half, (w_ps, copy) in enumerate(zip(halves, copies)):
+                first = gate * HID + half * (HID // 2)
+                copy(
+                    out=wT[:, :, first : first + HID // 2],
+                    in_=w_ps[:].rearrange("p q j -> p (q j)").bitcast(BF16).rearrange("p (j e) -> p e j", e=2),
                 )
 
         psum = ctx.enter_context(tc.psum_pool(name="psum", bufs=1))
@@ -200,37 +211,27 @@ def tile_wavernncell_pa_t_kernel(tc, x, feat, aux1, h, w_ih, w_hh_words, w_hh_sc
                 out=grouped[:, 2 * pair : 2 * pair + 2, :].bitcast(F32).rearrange("p s (b u) -> p s b u", u=2),
                 in_=h_ps[:].rearrange("p s u b -> p s b u"),
             )
-        cols_ps = psum.tile([P, N_X, P], BF16, name="cols_ps", tag="in_ps")
-        for c in range(N_X):
-            nc.tensor.transpose(out=cols_ps[:, c, :], in_=x_block0[:, :, c], identity=ident_bf[:])
-        nc.vector.tensor_copy(out=x_cols[:], in_=cols_ps[:, :, 0:SUB])
+        cols_ps = psum.tile([P, P], F32, name="cols_ps", tag="in_ps")
+        nc.tensor.transpose(out=cols_ps[:], in_=x_block0[:].rearrange("p j c -> p (j c)").bitcast(F32), identity=ident_f32[:])
+        nc.vector.tensor_copy(out=x_cols[:], in_=cols_ps[:, 0:SUB])
         quantise(0)
-        for e in range(2):
-            half_ps = psum.tile([P, HID], BF16, name="half_ps", tag="z_bank", bufs=2)
-            turn_weights(R_GATE, slice(e, 2 * STREAM, 2), half_ps)
-            (nc.scalar.copy, nc.vector.tensor_copy)[e](out=wT[:, e, 0:HID], in_=half_ps[:])
+        keep_weights(R_GATE, turn_weights(R_GATE, (("z_bank", 2), ("z_bank", 2))), (nc.scalar.copy, nc.vector.tensor_copy))
         nc.vector.tensor_copy(out=wx[:, 0:JT, :], in_=w_sb[R_GATE][:, :, 2 * STREAM : IN])
-        cat_ps = psum.tile([P, SUB, P], F32, name="cat_ps", tag="gi")
+        for pair, (copy, tag, bufs) in enumerate(((nc.scalar.copy, "gi", 1), (nc.vector.tensor_copy, "gh", 3))):
+            cat_ps = psum.tile([P, 2, P], F32, name="cat_ps", tag=tag, bufs=bufs)
+            for s in range(2):
+                cat_words = fa_sb[:, 2 * pair + s, :, :].rearrange("p s k -> p (s k)").bitcast(F32)
+                nc.tensor.transpose(out=cat_ps[:, s, :], in_=cat_words, identity=ident_f32[:])
+            copy(
+                out=catT[:, :, 2 * pair * P : 2 * (pair + 1) * P],
+                in_=cat_ps[:].rearrange("p t b -> p (t b)").bitcast(BF16).rearrange("p (b e) -> p e b", e=2),
+            )
+        x_ps = psum.tile([P, NB], F32, name="x_ps", tag="n_bank")
         for s in range(SUB):
-            cat_words = fa_sb[:, s, :, :].rearrange("p s k -> p (s k)").bitcast(F32)
-            nc.tensor.transpose(out=cat_ps[:, s, :], in_=cat_words, identity=ident_f32[:])
-        cat_values = cat_ps[:].rearrange("p t b -> p (t b)").bitcast(BF16).rearrange("p (b e) -> p e b", e=2)
-        for e in range(2):
-            (nc.scalar.copy, nc.vector.tensor_copy)[e](out=catT[:, e, :], in_=cat_values[:, e, :])
-
-        x_ps = psum.tile([P, N_X, NB], BF16, name="x_ps", tag="n_bank")
-        for c in range(N_X):
-            for s in range(SUB):
-                nc.tensor.transpose(
-                    out=x_ps[:, c, s * P : (s + 1) * P],
-                    in_=x_cols[:, c, s : s + 1].to_broadcast([P, P]),
-                    identity=ident_bf[:],
-                )
-        nc.vector.tensor_copy(out=x_bc0[:], in_=x_ps[:])
-
-        def x_column(bb, c):
-            return x_bc0[:, c, :] if bb == 0 else x_bc[:, bb, :, c]
-
+            nc.tensor.transpose(
+                out=x_ps[:, s * P : (s + 1) * P], in_=x_cols[:, s : s + 1].to_broadcast([P, P]), identity=ident_f32[:]
+            )
+        nc.vector.tensor_copy(out=x_bc[:, 0, :, :].rearrange("p b c -> p (b c)").bitcast(F32), in_=x_ps[:])
         bias = const.tile([P, 2 * COL_TILES], F32)
         bias_rz = const.tile([P, 2 * JT], F32)
 
@@ -276,7 +277,7 @@ def tile_wavernncell_pa_t_kernel(tc, x, feat, aux1, h, w_ih, w_hh_words, w_hh_sc
             total = work.tile([P, NB], F32, tag=tag, bufs=(8 if tag == "z_hidden" else 2))
             nc.vector.scalar_tensor_tensor(
                 out=total[:],
-                in0=x_column(bb, column),
+                in0=x_bc[:, bb, :, column],
                 scalar=wx[:, gate * JT + jt, column : column + 1],
                 in1=product[:],
                 op0=ALU.mult,
@@ -367,17 +368,16 @@ def tile_wavernncell_pa_t_kernel(tc, x, feat, aux1, h, w_ih, w_hh_words, w_hh_sc
                     n_bank[v] = straight_products(v, N_GATE, "n_bank", 1)
             if i == 4:
                 wx_ps = psum.tile([P, HID], BF16, name="wx_ps", tag="n_bank")
-                turn_weights(N_GATE, slice(IN - P, IN), wx_ps)
+                for jt in range(JT):
+                    nc.tensor.transpose(
+                        out=wx_ps[:, jt * P : (jt + 1) * P], in_=w_sb[N_GATE][:, jt, IN - P : IN], identity=ident_bf[:]
+                    )
             for v in z_tiles:
                 add_turned(v, z_bank[v], (z_hidden, z_input))
             for v in n_tiles:
                 add_turned(v, n_bank[v], (reset_hidden,))
             if late_weights is not None:
-                late_even = psum.tile([P, HID], BF16, name="late_even", tag="z_bank", bufs=2)
-                turn_weights(late_weights, slice(0, 2 * STREAM, 2), late_even)
-                late_odd = psum.tile([P, HID], BF16, name="late_odd", tag="n_bank")
-                turn_weights(late_weights, slice(1, 2 * STREAM, 2), late_odd)
-                nc.vector.tensor_copy(out=wT[:, 1, late_weights * HID : (late_weights + 1) * HID], in_=late_odd[:])
+                late_ps = turn_weights(late_weights, (("z_bank", 2), ("n_bank", 1)))
             for k, t in enumerate(turning):
                 if k == 0:
                     turn_inputs(t, "in_ps", 1)
@@ -397,6 +397,8 @@ def tile_wavernncell_pa_t_kernel(tc, x, feat, aux1, h, w_ih, w_hh_words, w_hh_sc
             if i < 4:
                 for t in turning:
                     keep_inputs(t)
+            if late_weights is not None:
+                keep_weights(late_weights, late_ps, (nc.scalar.copy, nc.scalar.copy))
             if i % SUB == 1 and X_SETS <= (i + 3) // SUB < NBLK:
                 load_x_rows((i + 3) // SUB)
             if 0 <= i < UNITS:
@@ -411,8 +413,6 @@ def tile_wavernncell_pa_t_kernel(tc, x, feat, aux1, h, w_ih, w_hh_words, w_hh_sc
             for v in n_tiles:
                 n_gate[v] = work.tile([P, HID], F32, name="n_gate", tag="n_gate", bufs=5)
                 nc.scalar.activation(out=n_gate[v][:], in_=n_bank[v][:], func=ACT.Tanh)
-            if late_weights is not None:
-                nc.scalar.copy(out=wT[:, 0, late_weights * HID : (late_weights + 1) * HID], in_=late_even[:])
             if i == 4:
                 nc.scalar.copy(out=wxT[:], in_=wx_ps[:])
             if i >= 4:
@@ -423,7 +423,7 @@ def tile_wavernncell_pa_t_kernel(tc, x, feat, aux1, h, w_ih, w_hh_words, w_hh_sc
                 z_input[i] = work.tile([P, NB], F32, name="z_input", tag="z_input", bufs=8)
                 nc.scalar.activation(
                     out=z_input[i][:],
-                    in_=x_column(i // JT, 0),
+                    in_=x_bc[:, i // JT, :, 0],
                     func=ACT.Identity,
                     bias=bias_rz[:, c : c + 1],
                     scale=wx[:, c, 0:1],

@@ -169,11 +169,11 @@ def tile_wavernncell_pa_t_kernel(tc, x, feat, aux1, h, w_ih, w_hh_words, w_hh_sc
                 out=catT[:, :, s * P : (s + 1) * P], in_=in_ps[:, 2, :].bitcast(BF16).rearrange("p (b e) -> p e b", e=2)
             )
 
-        def quantise(bb):
+        def quantise(t):
+            bb, s = divmod(t, SUB)
             h_codes, h_scales, grouped = operands[bb][0], operands[bb][1], operands[bb][3]
-            nc.vector.quantize_mx(
-                out=h_codes[:].bitcast(FP8X4), scales=h_scales[:], in_=grouped[:].rearrange("p s e -> p (s e)")
-            )
+            rows = slice(s * P, (s + 1) * P)
+            nc.vector.quantize_mx(out=h_codes[:, rows].bitcast(FP8X4), scales=h_scales[:, rows], in_=grouped[:, s, :])
 
         wT = const.tile([P, 2, GATES * HID], BF16)
         wx = const.tile([P, COL_TILES, N_X], F32)
@@ -214,7 +214,8 @@ def tile_wavernncell_pa_t_kernel(tc, x, feat, aux1, h, w_ih, w_hh_words, w_hh_sc
         cols_ps = psum.tile([P, P], F32, name="cols_ps", tag="in_ps")
         nc.tensor.transpose(out=cols_ps[:], in_=x_block0[:].rearrange("p j c -> p (j c)").bitcast(F32), identity=ident_f32[:])
         nc.vector.tensor_copy(out=x_cols[:], in_=cols_ps[:, 0:SUB])
-        quantise(0)
+        for t in range(SUB):
+            quantise(t)
         keep_weights(R_GATE, turn_weights(R_GATE, (("z_bank", 2), ("z_bank", 2))), (nc.scalar.copy, nc.vector.tensor_copy))
         nc.vector.tensor_copy(out=wx[:, 0:JT, :], in_=w_sb[R_GATE][:, :, 2 * STREAM : IN])
         for pair, (copy, tag, bufs) in enumerate(((nc.scalar.copy, "gi", 1), (nc.vector.tensor_copy, "gh", 3))):
@@ -337,7 +338,8 @@ def tile_wavernncell_pa_t_kernel(tc, x, feat, aux1, h, w_ih, w_hh_words, w_hh_sc
                 r_args[i] = work.tile([P, NB], F32, name="r_arg", tag="r_arg")
                 nc.gpsimd.tensor_tensor(out=r_args[i][:], in0=r_halves[i][0][:], in1=r_halves[i][1][:], op=ALU.add)
             if i == 3:
-                quantise(1)
+                for t in range(SUB, 2 * SUB):
+                    quantise(t)
             if 0 <= i - 1 < UNITS:
                 u = i - 1
                 gh_n = hidden_product(u, N_GATE)
@@ -392,8 +394,10 @@ def tile_wavernncell_pa_t_kernel(tc, x, feat, aux1, h, w_ih, w_hh_words, w_hh_sc
                 v = i - 7
                 z_diff[v] = work.tile([P, HID], F32, name="z_diff", tag="z_diff")
                 nc.vector.tensor_tensor(out=z_diff[v][:], in0=z_gate[v][:], in1=h_minus_n[v][:], op=ALU.mult)
-            if i > 3 and i % SUB == 2 and i + 2 < UNITS:
-                quantise((i + 2) // SUB)
+            if i == 4:
+                quantise(8)
+            if 4 <= i and i + 5 < TILES:
+                quantise(i + 5)
             if i < 4:
                 for t in turning:
                     keep_inputs(t)

@@ -106,7 +106,9 @@ def tile_wavernncell_pa_t_kernel(tc, x, feat, aux1, h, w_ih, w_hh_words, w_hh_sc
             for first, last in ((0, 8), (8, COL_TILES)):
                 nc.sync.dma_start(out=bias_rows[row + first : row + last, :], in_=rows[first:last, :])
 
-        load_h(0)
+        for pair in range(2):
+            tiles = slice(2 * pair, 2 * pair + 2)
+            nc.sync.dma_start(out=h_sb[:, tiles, :], in_=h_view[:, tiles, :])
         nc.sync.dma_start(
             out=x_block0[0:SUB, :, :].rearrange("s j c -> s (j c)"),
             in_=x[0:NB, :].rearrange("(s j) c -> s (j c)", s=SUB),
@@ -406,6 +408,16 @@ def tile_wavernncell_pa_t_kernel(tc, x, feat, aux1, h, w_ih, w_hh_words, w_hh_sc
             if i % SUB == 1 and X_SETS <= (i + 3) // SUB < NBLK:
                 load_x_rows((i + 3) // SUB)
             if 0 <= i < UNITS:
+                c = Z_GATE * JT + i % JT
+                z_input[i] = work.tile([P, NB], F32, name="z_input", tag="z_input", bufs=8)
+                nc.scalar.activation(
+                    out=z_input[i][:],
+                    in_=x_bc[:, i // JT, :, 0],
+                    func=ACT.Identity,
+                    bias=bias_rz[:, c : c + 1],
+                    scale=wx[:, c, 0:1],
+                )
+            if 0 <= i < UNITS:
                 c = R_GATE * JT + i % JT
                 r_gate[i] = work.tile([P, NB], F32, name="r_gate", tag="r_gate", bufs=3)
                 nc.scalar.activation(
@@ -422,13 +434,3 @@ def tile_wavernncell_pa_t_kernel(tc, x, feat, aux1, h, w_ih, w_hh_words, w_hh_sc
             if i >= 4:
                 for t in turning:
                     keep_inputs(t)
-            if 0 <= i < UNITS:
-                c = Z_GATE * JT + i % JT
-                z_input[i] = work.tile([P, NB], F32, name="z_input", tag="z_input", bufs=8)
-                nc.scalar.activation(
-                    out=z_input[i][:],
-                    in_=x_bc[:, i // JT, :, 0],
-                    func=ACT.Identity,
-                    bias=bias_rz[:, c : c + 1],
-                    scale=wx[:, c, 0:1],
-                )

@@ -331,10 +331,10 @@ def tile_wavernncell_pa_t_kernel(tc, x, feat, aux1, h, w_ih, w_hh_words, w_hh_sc
                 )
             if i == 0:
                 nc.scalar.copy(out=wx[:, JT : 2 * JT, :], in_=w_sb[Z_GATE][:, :, 2 * STREAM : IN])
-            if 0 <= i - 7 < TILES:
-                v = i - 7
+            if 0 <= i - 6 < TILES:
+                v = i - 6
                 h_minus_n[v] = work.tile([P, HID], F32, name="h_minus_n", tag="h_minus_n", bufs=3)
-                subtractor = nc.vector if i > UNITS else nc.gpsimd
+                subtractor = nc.vector if i >= UNITS else nc.gpsimd
                 subtractor.tensor_tensor(out=h_minus_n[v][:], in0=h_sb[:, v, :], in1=n_gate[v][:], op=ALU.subtract)
             if 0 <= i < UNITS:
                 r_args[i] = work.tile([P, NB], F32, name="r_arg", tag="r_arg")
@@ -387,13 +387,16 @@ def tile_wavernncell_pa_t_kernel(tc, x, feat, aux1, h, w_ih, w_hh_words, w_hh_sc
                     turn_inputs(t, "in_ps", 1)
                 else:
                     turn_inputs(t, "z_bank", 2)
-            if 0 <= i - 8 < TILES:
-                v = i - 8
-                res = work.tile([P, HID], F32, tag="res", bufs=4)
-                nc.vector.tensor_tensor(out=res[:], in0=n_gate[v][:], in1=z_diff[v][:], op=ALU.add)
-                nc.sync.dma_start(out=out[v * P : (v + 1) * P, :], in_=res[:])
             if 0 <= i - 7 < TILES:
                 v = i - 7
+                res = work.tile([P, HID], F32, tag="res", bufs=4)
+                parts = 2 if v == TILES - 1 else 1
+                for k in range(parts):
+                    cols = slice(k * HID // parts, (k + 1) * HID // parts)
+                    nc.vector.tensor_tensor(out=res[:, cols], in0=n_gate[v][:, cols], in1=z_diff[v][:, cols], op=ALU.add)
+                    nc.sync.dma_start(out=out[v * P : (v + 1) * P, cols], in_=res[:, cols])
+            if 0 <= i - 6 < TILES:
+                v = i - 6
                 z_diff[v] = work.tile([P, HID], F32, name="z_diff", tag="z_diff")
                 nc.vector.tensor_tensor(out=z_diff[v][:], in0=z_gate[v][:], in1=h_minus_n[v][:], op=ALU.mult)
             if i == 4:
@@ -417,18 +420,18 @@ def tile_wavernncell_pa_t_kernel(tc, x, feat, aux1, h, w_ih, w_hh_words, w_hh_sc
                     bias=bias_rz[:, c : c + 1],
                     scale=wx[:, c, 0:1],
                 )
-            if 0 <= i < UNITS:
-                c = R_GATE * JT + i % JT
-                r_gate[i] = work.tile([P, NB], F32, name="r_gate", tag="r_gate", bufs=3)
-                nc.scalar.activation(
-                    out=r_gate[i][:], in_=r_args[i][:], func=ACT.Sigmoid, bias=bias_rz[:, c : c + 1], scale=1.0
-                )
             for v in z_tiles:
                 z_gate[v] = work.tile([P, HID], F32, name="z_gate", tag="z_gate", bufs=5)
                 nc.scalar.activation(out=z_gate[v][:], in_=z_bank[v][:], func=ACT.Sigmoid)
             for v in n_tiles:
                 n_gate[v] = work.tile([P, HID], F32, name="n_gate", tag="n_gate", bufs=5)
                 nc.scalar.activation(out=n_gate[v][:], in_=n_bank[v][:], func=ACT.Tanh)
+            if 0 <= i < UNITS:
+                c = R_GATE * JT + i % JT
+                r_gate[i] = work.tile([P, NB], F32, name="r_gate", tag="r_gate", bufs=3)
+                nc.scalar.activation(
+                    out=r_gate[i][:], in_=r_args[i][:], func=ACT.Sigmoid, bias=bias_rz[:, c : c + 1], scale=1.0
+                )
             if i == 4:
                 nc.scalar.copy(out=wxT[:], in_=wx_ps[:])
             if i >= 4:

from contextlib import ExitStack

import concourse.mybir as mybir
from concourse.masks import make_identity

FP8X4 = mybir.dt.float8_e4m3fn_x4
FP4X4 = mybir.dt.float4_e2m1fn_x4
BF16 = mybir.dt.bfloat16
F32 = mybir.dt.float32
I32 = mybir.dt.int32
U32 = mybir.dt.uint32
U8 = mybir.dt.uint8
ALU = mybir.AluOpType
ACT = mybir.ActivationFunctionType

P = 128
PACK = 4
BATCH = 4096
HID = 512
STREAM = 128
N_X = 2
IN = 2 * STREAM + N_X
GATES = 3
R_GATE, Z_GATE, N_GATE = 0, 1, 2
JT = HID // P
COL_TILES = GATES * JT
NB = 512
SUB = NB // P
NBLK = BATCH // NB
TILES = BATCH // P
UNITS = NBLK * JT
X_SETS = 3
ONES_ROW = P - 3

FLOPS = 2 * BATCH * GATES * HID * (HID + IN)


def tile_wavernncell_pa_t_kernel(tc, x, feat, aux1, h, w_ih, w_hh_words, w_hh_scales, b_ih, b_hh, out):
    nc = tc.nc
    with ExitStack() as ctx:
        const = ctx.enter_context(tc.tile_pool(name="const", bufs=1))
        operand = ctx.enter_context(tc.tile_pool(name="operand", bufs=3))
        work = ctx.enter_context(tc.tile_pool(name="work", bufs=2))
        ctx.enter_context(tc.manual_schedule())

        ident_bf = const.tile([P, P], BF16)
        make_identity(nc, ident_bf[:])
        ident_f32 = const.tile([P, P], F32)
        make_identity(nc, ident_f32[:])

        table_use = const.tile([P, 1], F32)
        nc.scalar.activation(out=table_use[:], in_=ident_f32[:, 0:1], func=ACT.Sigmoid)

        w4_scales = const.tile([P, GATES * HID], U8, align_bytes=64)
        nc.vector.memset(w4_scales[:].bitcast(I32), 0)
        x_block0 = const.tile([P, P, N_X], BF16)
        nc.vector.memset(x_block0[:].rearrange("p j c -> p (j c)").bitcast(I32), 0)
        bias_rows = const.tile([P, P], BF16)
        nc.vector.memset(bias_rows[:].bitcast(I32), 0)
        x_rows = [const.tile([P, NB, N_X], BF16, name="x_rows_%d" % k) for k in range(X_SETS)]
        for rows in x_rows:
            nc.vector.tensor_copy(
                out=rows[:].rearrange("p b c -> p (b c)"), in_=ident_bf[:, ONES_ROW : ONES_ROW + 1].to_broadcast([P, NB * N_X])
            )

        w_sb = [const.tile([P, JT, IN], BF16, name="w_sb_%d" % gate) for gate in range(GATES)]
        h_sb = const.tile([P, TILES, HID], BF16)
        fa_sb = const.tile([P, TILES, 2, STREAM], BF16)
        x_bc = const.tile([P, NBLK, NB, N_X], BF16)
        x_cols = const.tile([P, SUB], F32)
        w4_words = const.tile([P, 2 * GATES * HID], U8, align_bytes=64)
        h_view = h.rearrange("(t p) k -> p t k", p=P)
        feat_view = feat.rearrange("(t p) k -> p t k", p=P)
        aux_view = aux1.rearrange("(t p) k -> p t k", p=P)
        x_flat = x.rearrange("b c -> (b c)")

        def load_h(bb):
            tiles = slice(bb * SUB, (bb + 1) * SUB)
            nc.sync.dma_start(out=h_sb[:, tiles, :], in_=h_view[:, tiles, :])

        def load_streams(bb):
            tiles = slice(bb * SUB, (bb + 1) * SUB)
            nc.sync.dma_start(out=fa_sb[:, tiles, 0, :], in_=feat_view[:, tiles, :])
            nc.sync.dma_start(out=fa_sb[:, tiles, 1, :], in_=aux_view[:, tiles, :])

        def load_x(bb):
            nc.sync.dma_start(
                out=x_bc[:, bb, :, :].rearrange("p b c -> p (b c)"),
                in_=x_flat[bb * NB * N_X : (bb + 1) * NB * N_X].partition_broadcast(P),
            )

        def load_x_rows(bb):
            rows = x_rows[bb % X_SETS][:].rearrange("p b c -> p (b c)")
            first, count = bb * NB * N_X, NB * N_X
            nc.sync.dma_start(out=rows[P - 2 : P - 1, :], in_=x_flat[first : first + count].unsqueeze(0))
            nc.sync.dma_start(out=rows[P - 1 : P, 0 : count - 1], in_=x_flat[first + 1 : first + count].unsqueeze(0))

        w_view = w_ih.rearrange("(c p) k -> p c k", p=P)

        def load_weights(gate):
            rows = slice(gate * JT, (gate + 1) * JT)
            nc.sync.dma_start(out=w_sb[gate][:], in_=w_view[:, rows, :])

        def load_biases(vector, row):
            rows = vector.rearrange("(c p) -> c p", p=P)
            for first, last in ((0, 8), (8, COL_TILES)):
                nc.sync.dma_start(out=bias_rows[row + first : row + last, :], in_=rows[first:last, :])

        for pair in range(2):
            tiles = slice(2 * pair, 2 * pair + 2)
            nc.sync.dma_start(out=h_sb[:, tiles, :], in_=h_view[:, tiles, :])
        nc.sync.dma_start(
            out=x_block0[0:SUB, :, :].rearrange("s j c -> s (j c)"),
            in_=x[0:NB, :].rearrange("(s j) c -> s (j c)", s=SUB),
        )
        load_weights(R_GATE)
        load_streams(0)
        nc.sync.dma_start(out=w4_words[:].bitcast(I32), in_=w_hh_words[0].bitcast(I32))
        for quad in range(4):
            nc.sync.dma_start(
                out=w4_scales[32 * quad : 32 * quad + 4, :].bitcast(I32),
                in_=w_hh_scales[0, 4 * quad : 4 * quad + 4, :].bitcast(I32),
            )
        load_weights(Z_GATE)
        load_biases(b_ih, 0)
        load_biases(b_hh, COL_TILES)
        load_h(1)
        load_streams(1)
        load_weights(N_GATE)
        load_h(2)
        load_streams(2)
        for bb in range(X_SETS):
            load_x_rows(bb)
        load_x(1)
        for bb in range(3, NBLK):
            load_h(bb)
            load_streams(bb)
            load_x(bb - 1)
        load_x(NBLK - 1)

        operands = {}
        turned_inputs = {}

        def turn_inputs(t, pool_tag, bufs):
            in_ps = psum.tile([P, 3, P], F32, name="in_ps", tag=pool_tag, bufs=bufs)
            h_words = h_sb[:, t, :].bitcast(F32)
            for u in range(2):
                nc.tensor.transpose(out=in_ps[:, u, :], in_=h_words[:, u : HID // 2 : 2], identity=ident_f32[:])
            cat_words = fa_sb[:, t, :, :].rearrange("p s k -> p (s k)").bitcast(F32)
            nc.tensor.transpose(out=in_ps[:, 2, :], in_=cat_words, identity=ident_f32[:])
            turned_inputs[t] = in_ps

        def new_operands(bb):
            h_codes = operand.tile([P, NB], U32, align_bytes=64)
            h_scales = operand.tile([P, NB], U8, align_bytes=64)
            catT = operand.tile([P, 2, NB], BF16, bufs=4)
            grouped = operand.tile([P, SUB, P * PACK], BF16, align_bytes=64)
            operands[bb] = (h_codes, h_scales, catT, grouped)

        def keep_inputs(t):
            bb, s = divmod(t, SUB)
            if s == 0:
                new_operands(bb)
            catT, grouped = operands[bb][2], operands[bb][3]
            in_ps = turned_inputs[t]
            nc.scalar.copy(
                out=grouped[:, s, :].bitcast(F32).rearrange("p (b u) -> p b u", u=2),
                in_=in_ps[:, 0:2, :].rearrange("p u b -> p b u"),
            )
            nc.scalar.copy(
                out=catT[:, :, s * P : (s + 1) * P], in_=in_ps[:, 2, :].bitcast(BF16).rearrange("p (b e) -> p e b", e=2)
            )

        def quantise(t):
            bb, s = divmod(t, SUB)
            h_codes, h_scales, grouped = operands[bb][0], operands[bb][1], operands[bb][3]
            rows = slice(s * P, (s + 1) * P)
            nc.vector.quantize_mx(out=h_codes[:, rows].bitcast(FP8X4), scales=h_scales[:, rows], in_=grouped[:, s, :])

        wT = const.tile([P, 2, GATES * HID], BF16)
        wx = const.tile([P, COL_TILES, N_X], F32)
        wxT = const.tile([P, HID], BF16)

        def turn_weights(gate, banks):
            halves = []
            for half, (tag, bufs) in enumerate(banks):
                w_ps = psum.tile([P, JT // 2, P], F32, name="w_ps", tag=tag, bufs=bufs)
                for q in range(JT // 2):
                    words = w_sb[gate][:, half * (JT // 2) + q, :].bitcast(F32)
                    nc.tensor.transpose(out=w_ps[:, q, :], in_=words[:, 0:P], identity=ident_f32[:])
                halves.append(w_ps)
            return halves

        def keep_weights(gate, halves, copies):
            for half, (w_ps, copy) in enumerate(zip(halves, copies)):
                first = gate * HID + half * (HID // 2)
                copy(
                    out=wT[:, :, first : first + HID // 2],
                    in_=w_ps[:].rearrange("p q j -> p (q j)").bitcast(BF16).rearrange("p (j e) -> p e j", e=2),
                )

        psum = ctx.enter_context(tc.psum_pool(name="psum", bufs=1))

        new_operands(0)
        catT, grouped = operands[0][2], operands[0][3]
        for pair, copy in ((0, nc.vector.tensor_copy), (1, nc.scalar.copy)):
            h_ps = psum.tile([P, 2, 2, P], F32, name="h_ps", tag="gh", bufs=3)
            for s in range(2):
                h_words = h_sb[:, 2 * pair + s, :].bitcast(F32)
                for u in range(2):
                    nc.tensor.transpose(out=h_ps[:, s, u, :], in_=h_words[:, u : HID // 2 : 2], identity=ident_f32[:])
            copy(
                out=grouped[:, 2 * pair : 2 * pair + 2, :].bitcast(F32).rearrange("p s (b u) -> p s b u", u=2),
                in_=h_ps[:].rearrange("p s u b -> p s b u"),
            )
        cols_ps = psum.tile([P, P], F32, name="cols_ps", tag="in_ps")
        nc.tensor.transpose(out=cols_ps[:], in_=x_block0[:].rearrange("p j c -> p (j c)").bitcast(F32), identity=ident_f32[:])
        nc.vector.tensor_copy(out=x_cols[:], in_=cols_ps[:, 0:SUB])
        for t in range(SUB):
            quantise(t)
        keep_weights(R_GATE, turn_weights(R_GATE, (("z_bank", 2), ("z_bank", 2))), (nc.scalar.copy, nc.vector.tensor_copy))
        nc.vector.tensor_copy(out=wx[:, 0:JT, :], in_=w_sb[R_GATE][:, :, 2 * STREAM : IN])
        for pair, (copy, tag, bufs) in enumerate(((nc.scalar.copy, "gi", 1), (nc.vector.tensor_copy, "gh", 3))):
            cat_ps = psum.tile([P, 2, P], F32, name="cat_ps", tag=tag, bufs=bufs)
            for s in range(2):
                cat_words = fa_sb[:, 2 * pair + s, :, :].rearrange("p s k -> p (s k)").bitcast(F32)
                nc.tensor.transpose(out=cat_ps[:, s, :], in_=cat_words, identity=ident_f32[:])
            copy(
                out=catT[:, :, 2 * pair * P : 2 * (pair + 1) * P],
                in_=cat_ps[:].rearrange("p t b -> p (t b)").bitcast(BF16).rearrange("p (b e) -> p e b", e=2),
            )
        x_ps = psum.tile([P, NB], F32, name="x_ps", tag="n_bank")
        for s in range(SUB):
            nc.tensor.transpose(
                out=x_ps[:, s * P : (s + 1) * P], in_=x_cols[:, s : s + 1].to_broadcast([P, P]), identity=ident_f32[:]
            )
        nc.vector.tensor_copy(out=x_bc[:, 0, :, :].rearrange("p b c -> p (b c)").bitcast(F32), in_=x_ps[:])
        bias = const.tile([P, 2 * COL_TILES], F32)
        bias_rz = const.tile([P, 2 * JT], F32)

        def turn_biases():
            bias_ps = psum.tile([P, P], BF16, name="bias_ps", tag="n_bank")
            nc.tensor.transpose(out=bias_ps[:], in_=bias_rows[:], identity=ident_bf[:])
            nc.vector.tensor_copy(out=bias[:], in_=bias_ps[:, 0 : 2 * COL_TILES])
            nc.vector.tensor_tensor(
                out=bias_rz[:], in0=bias_ps[:, 0 : 2 * JT], in1=bias[:, COL_TILES : COL_TILES + 2 * JT], op=ALU.add
            )

        r_plain, r_hidden_ps, r_halves, r_args, r_gate = {}, {}, {}, {}, {}
        reset_hidden, z_hidden, z_input = {}, {}, {}
        z_bank, n_bank, z_gate, n_gate, h_minus_n, z_diff = {}, {}, {}, {}, {}, {}

        def hidden_product(u, gate):
            bb, jt = divmod(u, JT)
            h_codes, h_scales = operands[bb][0], operands[bb][1]
            c = gate * JT + jt
            gh = psum.tile([P, NB], F32, tag="gh", bufs=3)
            nc.tensor.matmul_mx(
                out=gh[:],
                lhsT=w4_words[:, 2 * c * P : 2 * (c + 1) * P].bitcast(FP4X4),
                lhsT_scale=w4_scales[:, c * P : (c + 1) * P],
                rhs=h_codes[:].bitcast(FP8X4),
                rhs_scale=h_scales[:],
                start=True,
                stop=True,
            )
            return gh

        def r_input_product(u):
            bb, jt = divmod(u, JT)
            catT = operands[bb][2]
            c = R_GATE * JT + jt
            gi = psum.tile([P, NB], F32, tag="gi")
            nc.tensor.matmul(out=gi[:], lhsT=wT[:, 0, c * P : (c + 1) * P], rhs=catT[:, 0, :], start=True, stop=False)
            nc.tensor.matmul(out=gi[:], lhsT=wT[:, 1, c * P : (c + 1) * P], rhs=catT[:, 1, :], start=False, stop=True)
            return gi

        def with_x(u, gate, column, product, tag):
            bb, jt = divmod(u, JT)
            total = work.tile([P, NB], F32, tag=tag, bufs=(8 if tag == "z_hidden" else 2))
            nc.vector.scalar_tensor_tensor(
                out=total[:],
                in0=x_bc[:, bb, :, column],
                scalar=wx[:, gate * JT + jt, column : column + 1],
                in1=product[:],
                op0=ALU.mult,
                op1=ALU.add,
            )
            return total

        def straight_products(v, gate, tag, bufs):
            bb, s = divmod(v, SUB)
            catT = operands[bb][2]
            rows = slice(s * P, (s + 1) * P)
            cols = slice(gate * HID, (gate + 1) * HID)
            bank = psum.tile([P, HID], F32, tag=tag, bufs=bufs)
            nc.tensor.matmul(out=bank[:], lhsT=catT[:, 0, rows], rhs=wT[:, 0, cols], start=True, stop=False)
            nc.tensor.matmul(out=bank[:], lhsT=catT[:, 1, rows], rhs=wT[:, 1, cols], start=False, stop=False)
            if gate == N_GATE:
                nc.tensor.matmul(out=bank[:], lhsT=x_rows[bb % X_SETS][:, rows, 0], rhs=wxT[:], start=False, stop=False)
            return bank

        def add_turned(v, bank, sources):
            bb, s = divmod(v, SUB)
            rows = slice(s * P, (s + 1) * P)
            for jt in range(JT):
                for k, source in enumerate(sources):
                    nc.tensor.matmul(
                        out=bank[:, jt * P : (jt + 1) * P],
                        lhsT=source[bb * JT + jt][:, rows],
                        rhs=ident_f32[:],
                        is_transpose=True,
                        start=False,
                        stop=(jt == JT - 1 and k == len(sources) - 1),
                    )

        for i in range(UNITS + 9):
            turning = () if i == 0 else (2 * i + 2, 2 * i + 3) if i < 4 else (i + 6,) if i + 6 < TILES else ()
            late_weights = {2: Z_GATE, 3: N_GATE}.get(i)
            if i == 4:
                nc.vector.tensor_copy(
                    out=w_sb[N_GATE][:, :, IN - P + ONES_ROW : IN - P + ONES_ROW + 1],
                    in_=bias[:, N_GATE * JT : COL_TILES].unsqueeze(2),
                )
            if 0 <= i < UNITS:
                r_plain[i] = r_input_product(i)
                r_hidden_ps[i] = hidden_product(i, R_GATE)
                r_halves[i] = (
                    with_x(i, R_GATE, 0, r_plain[i], "r_half0"),
                    with_x(i, R_GATE, 1, r_hidden_ps[i], "r_half1"),
                )
            if i == 0:
                nc.scalar.copy(out=wx[:, JT : 2 * JT, :], in_=w_sb[Z_GATE][:, :, 2 * STREAM : IN])
            if 0 <= i - 6 < TILES:
                v = i - 6
                h_minus_n[v] = work.tile([P, HID], F32, name="h_minus_n", tag="h_minus_n", bufs=3)
                subtractor = nc.vector if i >= UNITS else nc.gpsimd
                subtractor.tensor_tensor(out=h_minus_n[v][:], in0=h_sb[:, v, :], in1=n_gate[v][:], op=ALU.subtract)
            if 0 <= i < UNITS:
                r_args[i] = work.tile([P, NB], F32, name="r_arg", tag="r_arg")
                nc.gpsimd.tensor_tensor(out=r_args[i][:], in0=r_halves[i][0][:], in1=r_halves[i][1][:], op=ALU.add)
            if i == 3:
                for t in range(SUB, 2 * SUB):
                    quantise(t)
            if 0 <= i - 1 < UNITS:
                u = i - 1
                gh_n = hidden_product(u, N_GATE)
                c = N_GATE * JT + u % JT
                reset_hidden[u] = work.tile([P, NB], F32, name="reset_hidden", tag="reset_hidden", bufs=8)
                nc.vector.scalar_tensor_tensor(
                    out=reset_hidden[u][:],
                    in0=gh_n[:],
                    scalar=bias[:, COL_TILES + c : COL_TILES + c + 1],
                    in1=r_gate[u][:],
                    op0=ALU.add,
                    op1=ALU.mult,
                )
            if 0 <= i < UNITS:
                gh_z = hidden_product(i, Z_GATE)
                z_hidden[i] = with_x(i, Z_GATE, 1, gh_z, "z_hidden")
            if i == 0:
                turn_biases()
            mx_done = i > UNITS
            z_tiles = [v for v in (i - 4,) if 0 <= v < TILES - 1] + ([TILES - 1] if i == TILES + 4 else [])
            n_tiles = [v for v in (i - 5,) if 0 <= v < TILES - 1] + ([TILES - 1] if i == TILES + 3 else [])
            for v in z_tiles:
                z_bank[v] = straight_products(v, Z_GATE, "z_bank", 2)
            for v in n_tiles:
                if i > TILES - 6 and v % 2 == 1:
                    n_bank[v] = straight_products(v, N_GATE, "in_ps", 1)
                else:
                    n_bank[v] = straight_products(v, N_GATE, "n_bank", 1)
            if i == 4:
                wx_ps = psum.tile([P, HID], BF16, name="wx_ps", tag="n_bank")
                for jt in range(JT):
                    nc.tensor.transpose(
                        out=wx_ps[:, jt * P : (jt + 1) * P], in_=w_sb[N_GATE][:, jt, IN - P : IN], identity=ident_bf[:]
                    )
            for v in z_tiles:
                add_turned(v, z_bank[v], (z_hidden, z_input))
            for v in n_tiles:
                add_turned(v, n_bank[v], (reset_hidden,))
            if late_weights is not None:
                late_ps = turn_weights(late_weights, (("z_bank", 2), ("n_bank", 1)))
            for k, t in enumerate(turning):
                if k == 0:
                    turn_inputs(t, "in_ps", 1)
                else:
                    turn_inputs(t, "z_bank", 2)
            if 0 <= i - 7 < TILES:
                v = i - 7
                res = work.tile([P, HID], F32, tag="res", bufs=4)
                parts = 2 if v == TILES - 1 else 1
                for k in range(parts):
                    cols = slice(k * HID // parts, (k + 1) * HID // parts)
                    nc.vector.tensor_tensor(out=res[:, cols], in0=n_gate[v][:, cols], in1=z_diff[v][:, cols], op=ALU.add)
                    nc.sync.dma_start(out=out[v * P : (v + 1) * P, cols], in_=res[:, cols])
            if 0 <= i - 6 < TILES:
                v = i - 6
                z_diff[v] = work.tile([P, HID], F32, name="z_diff", tag="z_diff")
                nc.vector.tensor_tensor(out=z_diff[v][:], in0=z_gate[v][:], in1=h_minus_n[v][:], op=ALU.mult)
            if i == 4:
                quantise(8)
            if 4 <= i and i + 5 < TILES:
                quantise(i + 5)
            if i < 4:
                for t in turning:
                    keep_inputs(t)
            if late_weights is not None:
                keep_weights(late_weights, late_ps, (nc.scalar.copy, nc.scalar.copy))
            if i % SUB == 1 and X_SETS <= (i + 3) // SUB < NBLK:
                load_x_rows((i + 3) // SUB)
            if 0 <= i < UNITS:
                c = Z_GATE * JT + i % JT
                z_input[i] = work.tile([P, NB], F32, name="z_input", tag="z_input", bufs=8)
                nc.scalar.activation(
                    out=z_input[i][:],
                    in_=x_bc[:, i // JT, :, 0],
                    func=ACT.Identity,
                    bias=bias_rz[:, c : c + 1],
                    scale=wx[:, c, 0:1],
                )
            for v in z_tiles:
                z_gate[v] = work.tile([P, HID], F32, name="z_gate", tag="z_gate", bufs=5)
                nc.scalar.activation(out=z_gate[v][:], in_=z_bank[v][:], func=ACT.Sigmoid)
            for v in n_tiles:
                n_gate[v] = work.tile([P, HID], F32, name="n_gate", tag="n_gate", bufs=5)
                nc.scalar.activation(out=n_gate[v][:], in_=n_bank[v][:], func=ACT.Tanh)
            if 0 <= i < UNITS:
                c = R_GATE * JT + i % JT
                r_gate[i] = work.tile([P, NB], F32, name="r_gate", tag="r_gate", bufs=3)
                nc.scalar.activation(
                    out=r_gate[i][:], in_=r_args[i][:], func=ACT.Sigmoid, bias=bias_rz[:, c : c + 1], scale=1.0
                )
            if i == 4:
                nc.scalar.copy(out=wxT[:], in_=wx_ps[:])
            if i >= 4:
                for t in turning:
                    keep_inputs(t)
